import numpy as np
import ml_dtypes

BF16 = ml_dtypes.bfloat16


def bf(x):
    return np.asarray(x, np.float32).astype(BF16)


def f32(x):
    return np.asarray(x, np.float32)


def f64(x):
    return np.asarray(x).astype(np.float64)


def striped(idx):
    return np.tile(idx.reshape(-1, 16).T, (8, 1))


S, LD, QD, N, NS, B, KS, VS, H, HID, QKV, PROJ, IN = 4096, 128, 256, 2048, 128, 16, 128, 128, 4, 512, 384, 1536, 641
EPS = 1e-5


def setup_inputs():
    r = np.random.standard_normal
    return {
        "table": bf(r((LD, S))),
        "w_lab": bf(r((LD, HID)) / np.sqrt(IN)),
        "emb": bf(r((QD, N))),
        "w_emb": bf(r((QD, HID)) / np.sqrt(IN)),
        "query": bf(r((QD, B))),
        "w_qry": bf(r((QD, HID)) / np.sqrt(IN)),
        "distances": f32(3.0 * np.random.random((1, N))),
        "w_dist": f32(10.0 * r((HID, 1))),
        "pre_b": f32(0.1 * r((HID, 1))),
        "qkv_w": bf(r((HID, PROJ)) / np.sqrt(HID)),
        "qkv_b": f32(0.1 * r((PROJ, 1))),
        "qkv_ln_w": f32(1.0 + 0.2 * r((PROJ, NS))),
        "qkv_ln_b": f32(0.2 * r((PROJ, NS))),
        "mlp_w": bf(r((HID, HID)) / np.sqrt(HID)),
        "mlp_b": f32(0.1 * r((HID, 1))),
        "mlp_ln_w": f32(1.0 + 0.1 * r((HID, 1))),
        "mlp_ln_b": f32(0.1 * r((HID, 1))),
        "offs": striped(np.random.permutation(np.tile(np.arange(S), 2))[:N]),
    }


def reference(table, w_lab, emb, w_emb, query, w_qry, distances, w_dist, pre_b, qkv_w, qkv_b, qkv_ln_w, qkv_ln_b, mlp_w, mlp_b, mlp_ln_w, mlp_ln_b, offs):
    idx = offs[:16].T.reshape(-1)
    e = np.exp(-f64(distances).reshape(B, NS))
    d = (e / e.sum(axis=1, keepdims=True)).reshape(1, N)
    mem0 = f64(w_lab).T @ f64(table)[:, idx] + f64(w_emb).T @ f64(emb) + f64(w_qry).T @ np.repeat(f64(query), NS, axis=1) + f64(w_dist) * d + f64(pre_b)
    y = (f64(qkv_w).T @ mem0 + f64(qkv_b)).reshape(PROJ, B, NS)
    mu = y.mean(axis=(0, 2), keepdims=True)
    var = np.square(y - mu).mean(axis=(0, 2), keepdims=True)
    z = (y - mu) / np.sqrt(var + EPS) * f64(qkv_ln_w)[:, None, :] + f64(qkv_ln_b)[:, None, :]
    z = z.reshape(H, QKV, B, NS)
    q = z[:, :KS] * KS ** -0.5
    ky = z[:, KS:KS + KS]
    v = z[:, KS + KS:]
    sc = np.einsum('hkbn,hkbm->hbnm', q, ky)
    sc = np.exp(sc - sc.max(axis=-1, keepdims=True))
    att = sc / sc.sum(axis=-1, keepdims=True)
    o = np.einsum('hbnm,hvbm->hvbn', att, v).reshape(HID, N)
    mem1 = mem0 + o
    f = f64(mlp_w).T @ np.maximum(mem1, 0.0) + f64(mlp_b)
    mu2 = f.mean(axis=0, keepdims=True)
    var2 = np.square(f - mu2).mean(axis=0, keepdims=True)
    return mem1 + (f - mu2) / np.sqrt(var2 + EPS) * f64(mlp_ln_w) + f64(mlp_ln_b)

@@ -1,0 +1,323 @@
+from contextlib import ExitStack
+
+import concourse.mybir as mybir
+from concourse.masks import make_identity
+
+F32 = mybir.dt.float32
+BF16 = mybir.dt.bfloat16
+U16 = mybir.dt.uint16
+FUNC = mybir.ActivationFunctionType
+ALU = mybir.AluOpType
+AXIS_X = mybir.AxisListType.X
+
+P = 128
+TABLE_COLS = 4096
+N_TOK = 2048
+N_SAMPLES = 16
+SLOTS = 128
+HID = 512
+HID_BLOCKS = HID // P
+EMB_BLOCKS = 2
+HEADS = 4
+HEAD_ROWS = 384
+PROJ = 3 * HEADS * P
+LOOKUP = 512
+LOOKUPS = N_TOK // LOOKUP
+LOOKUP_SAMPLES = LOOKUP // SLOTS
+PIECE = 256
+PIECES = N_TOK // PIECE
+PIECE_SAMPLES = PIECE // SLOTS
+AHEAD = 2
+STAT_CHUNK = 512
+EPS = 1e-5
+Q_SCALE = 128.0 ** -0.5
+
+COL_W_DIST = 0
+COL_PRE_B = 4
+COL_MLP_LN_W = 8
+COL_MLP_LN_B = 12
+COL_QKV_B = 16
+N_COLS = 28
+
+FLOPS = 2 * (128 + 256) * HID * N_TOK + 2 * 256 * HID * N_SAMPLES + 2 * HID * PROJ * N_TOK \
+    + 2 * 2 * HEADS * N_SAMPLES * SLOTS * SLOTS * P + 2 * HID * HID * N_TOK
+
+
+def tile_rsaffdecoder_b_kernel(
+    tc, table, w_lab, emb, w_emb, query, w_qry, distances, w_dist, pre_b, qkv_w, qkv_b,
+    qkv_ln_w, qkv_ln_b, mlp_w, mlp_b, mlp_ln_w, mlp_ln_b, offs, out,
+):
+    nc = tc.nc
+    with ExitStack() as ctx:
+        held = ctx.enter_context(tc.tile_pool(name="held", bufs=1))
+        by_piece = ctx.enter_context(tc.tile_pool(name="by_piece", bufs=3))
+        by_sample = ctx.enter_context(tc.tile_pool(name="by_sample", bufs=3))
+        stats = ctx.enter_context(tc.tile_pool(name="stats", bufs=6))
+
+        identity_f32 = held.tile([P, P], F32)
+        make_identity(nc, identity_f32[:])
+        identity_bf16 = held.tile([P, P], BF16)
+        nc.vector.tensor_copy(identity_bf16[:], identity_f32[:])
+
+        offsets = held.tile([P, N_TOK // 16], U16, name="offsets")
+        nc.sync.dma_start(offsets[:], offs)
+        w_lab_sb = held.tile([P, HID], BF16)
+        nc.sync.dma_start(w_lab_sb[:], w_lab)
+        table_sb = held.tile([P, TABLE_COLS], BF16)
+        nc.sync.dma_start(table_sb[:], table)
+
+        rows = held.tile([P, P], F32)
+        nc.vector.memset(rows[:], 0.0)
+        edist = held.tile([P, N_TOK], F32)
+        nc.scalar.dma_start(edist[:], distances.rearrange("o n -> (o n)").partition_broadcast(P))
+        for vector, col in ((w_dist, COL_W_DIST), (pre_b, COL_PRE_B), (mlp_ln_w, COL_MLP_LN_W),
+                            (mlp_ln_b, COL_MLP_LN_B), (qkv_b, COL_QKV_B)):
+            as_rows = vector.rearrange("(k p) o -> k (p o)", p=P)
+            nc.scalar.dma_start(rows[col:col + as_rows.shape[0], :], as_rows)
+
+        w_emb_sb = held.tile([P, EMB_BLOCKS, HID], BF16)
+        nc.sync.dma_start(w_emb_sb[:], w_emb.rearrange("(k p) h -> p k h", p=P))
+        emb_sb = held.tile([P, EMB_BLOCKS, N_TOK], BF16)
+        emb_blocks = emb.rearrange("(k p) n -> p k n", p=P)
+        nc.sync.dma_start(emb_sb[:, :, 0:LOOKUP], emb_blocks[:, :, 0:LOOKUP])
+        query_sb = held.tile([P, EMB_BLOCKS, N_SAMPLES], BF16)
+        nc.sync.dma_start(query_sb[:], query.rearrange("(k p) b -> p k b", p=P))
+        w_qry_sb = held.tile([P, EMB_BLOCKS, HID], BF16)
+        nc.sync.dma_start(w_qry_sb[:], w_qry.rearrange("(k p) h -> p k h", p=P))
+
+        w_qk_sb = held.tile([P, HID_BLOCKS, 2 * HEADS * P], BF16)
+        w_v_sb = held.tile([P, HID_BLOCKS, HID], BF16)
+        for hb in range(HID_BLOCKS):
+            by_head = qkv_w[hb * P:(hb + 1) * P, :].rearrange("p (t r) -> p t r", t=HEADS)
+            nc.sync.dma_start(w_qk_sb[:, hb, :].rearrange("p (t r) -> p t r", t=HEADS),
+                              by_head[:, :, 0:2 * P])
+            nc.gpsimd.dma_start(w_v_sb[:, hb, :].rearrange("p (t r) -> p t r", t=HEADS),
+                                by_head[:, :, 2 * P:3 * P])
+        nc.sync.dma_start(emb_sb[:, :, LOOKUP:N_TOK], emb_blocks[:, :, LOOKUP:N_TOK])
+
+        qkv_b_sb = held.tile([P, PROJ], F32)
+        nc.gpsimd.dma_start(qkv_b_sb[:], qkv_b.rearrange("r o -> (r o)").partition_broadcast(P))
+        mlp_b_sb = held.tile([P, HID], F32)
+        nc.gpsimd.dma_start(mlp_b_sb[:], mlp_b.rearrange("r o -> (r o)").partition_broadcast(P))
+
+        ln_gain = held.tile([P, PROJ], F32)
+        nc.sync.dma_start(ln_gain[:].rearrange("p (r n) -> p r n", n=SLOTS),
+                          qkv_ln_w.rearrange("(r p) n -> p r n", p=P))
+        ln_bias = held.tile([P, PROJ], F32)
+        nc.sync.dma_start(ln_bias[:].rearrange("p (r n) -> p r n", n=SLOTS),
+                          qkv_ln_b.rearrange("(r p) n -> p r n", p=P))
+        mlp_w_sb = held.tile([P, HID_BLOCKS, HID], BF16)
+        nc.sync.dma_start(mlp_w_sb[:], mlp_w.rearrange("(hb p) r -> p hb r", p=P))
+
+        mean_over_partitions = held.tile([P, P], F32)
+        nc.vector.memset(mean_over_partitions[:], 1.0 / P)
+        minus_half = held.tile([P, PIECE_SAMPLES], F32)
+        nc.vector.memset(minus_half[:], -0.5)
+        scratch = held.tile([P, 1], F32)
+        nc.vector.memset(scratch[:], 0.0)
+        nc.scalar.activation(scratch[:], scratch[:], FUNC.Exp)
+
+        mem = held.tile([P, HID_BLOCKS, N_TOK], F32)
+        cols = held.tile([P, N_COLS], F32)
+        w_dist_scaled = held.tile([P, HID_BLOCKS, N_SAMPLES], F32)
+        dist_min = held.tile([P, N_SAMPLES], F32)
+        edist_sum = held.tile([P, N_SAMPLES], F32)
+        edist_rsum = held.tile([P, N_SAMPLES], F32)
+
+        with tc.psum_pool(name="first_psum", bufs=1) as first_psum:
+            cols_ps = first_psum.tile([P, P], F32)
+            nc.tensor.transpose(cols_ps[:], rows[:], identity_f32[:])
+            nc.vector.tensor_copy(cols[:], cols_ps[:, 0:N_COLS])
+
+            for u in range(LOOKUPS):
+                group = slice(u * LOOKUP_SAMPLES, (u + 1) * LOOKUP_SAMPLES)
+                nc.vector.tensor_reduce(
+                    dist_min[:, group],
+                    edist[:, u * LOOKUP:(u + 1) * LOOKUP].rearrange("p (b n) -> p b n", n=SLOTS), AXIS_X, ALU.min)
+                for b in range(u * LOOKUP_SAMPLES, (u + 1) * LOOKUP_SAMPLES):
+                    sample = slice(b * SLOTS, (b + 1) * SLOTS)
+                    nc.scalar.activation(edist[:, sample], edist[:, sample], FUNC.Exp, bias=dist_min[:, b:b + 1],
+                                         scale=-1.0, accum_out=edist_sum[:, b:b + 1])
+                nc.vector.reciprocal(edist_rsum[:, group], edist_sum[:, group])
+                for hb in range(HID_BLOCKS):
+                    nc.vector.tensor_scalar_mul(w_dist_scaled[:, hb, group], edist_rsum[:, group],
+                                                cols[:, COL_W_DIST + hb:COL_W_DIST + hb + 1])
+
+            for u in range(LOOKUPS):
+                lookup_offsets = offsets[:, u * (LOOKUP // 16):(u + 1) * (LOOKUP // 16)]
+                for hb in range(HID_BLOCKS):
+                    label_ps = first_psum.tile([P, LOOKUP_SAMPLES, SLOTS], F32, bufs=7)
+                    nc.tensor.matmul(label_ps[:].rearrange("p s n -> p (s n)"), w_lab_sb[:, hb * P:(hb + 1) * P],
+                                     table_sb[:].indirect(lookup_offsets), start=True, stop=True)
+                    for s in range(LOOKUP_SAMPLES):
+                        b = u * LOOKUP_SAMPLES + s
+                        sample = slice(b * SLOTS, (b + 1) * SLOTS)
+                        nc.vector.scalar_tensor_tensor(mem[:, hb, sample], edist[:, sample],
+                                                       w_dist_scaled[:, hb, b:b + 1], label_ps[:, s, :],
+                                                       ALU.mult, ALU.add)
+
+        psum = ctx.enter_context(tc.psum_pool(name="psum", bufs=1))
+
+        query_term = held.tile([P, HID_BLOCKS, N_SAMPLES], F32)
+        query_ps = psum.tile([P, HID_BLOCKS, N_SAMPLES], F32, tag="other")
+        for hb in range(HID_BLOCKS):
+            for kb in range(EMB_BLOCKS):
+                nc.tensor.matmul(query_ps[:, hb, :], w_qry_sb[:, kb, hb * P:(hb + 1) * P], query_sb[:, kb, :],
+                                 start=(kb == 0), stop=(kb == EMB_BLOCKS - 1))
+            nc.vector.tensor_scalar_add(query_term[:, hb, :], query_ps[:, hb, :],
+                                        cols[:, COL_PRE_B + hb:COL_PRE_B + hb + 1])
+
+        for param in (ln_gain, ln_bias):
+            by_kind = param[:].rearrange("p (t c n) -> p t c n", c=3, n=SLOTS)
+            v_flipped = psum.tile([P, HEADS, P], F32, tag="other")
+            for t in range(HEADS):
+                nc.tensor.transpose(v_flipped[:, t, :], by_kind[:, t, 2, :], identity_f32[:])
+            nc.vector.tensor_copy(by_kind[:, :, 2, :], v_flipped[:])
+            nc.vector.tensor_scalar_mul(by_kind[:, :, 0, :], by_kind[:, :, 0, :], Q_SCALE)
+
+        out_blocks = out.rearrange("(rb p) n -> p rb n", p=P)
+        y_of_piece = {}
+        z_of_piece = {}
+
+        def project(g):
+            piece = slice(g * PIECE, (g + 1) * PIECE)
+            for hb in range(HID_BLOCKS):
+                emb_ps = psum.tile([P, PIECE_SAMPLES, SLOTS], F32, tag="bank", bufs=3)
+                for kb in range(EMB_BLOCKS):
+                    nc.tensor.matmul(emb_ps[:].rearrange("p s n -> p (s n)"), w_emb_sb[:, kb, hb * P:(hb + 1) * P],
+                                     emb_sb[:, kb, piece], start=(kb == 0), stop=(kb == EMB_BLOCKS - 1))
+                for s in range(PIECE_SAMPLES):
+                    b = g * PIECE_SAMPLES + s
+                    sample = slice(b * SLOTS, (b + 1) * SLOTS)
+                    nc.vector.scalar_tensor_tensor(mem[:, hb, sample], emb_ps[:, s, :], query_term[:, hb, b:b + 1],
+                                                   mem[:, hb, sample], ALU.add, ALU.add)
+            mem0_bf16 = by_piece.tile([P, HID_BLOCKS, PIECE], BF16)
+            nc.scalar.activation(mem0_bf16[:], mem[:, :, piece], FUNC.Copy)
+
+            y = by_piece.tile([P, PIECE_SAMPLES, PROJ], F32)
+            y_of_piece[g] = y
+            for t in range(HEADS):
+                for c in range(2):
+                    qk_ps = psum.tile([P, PIECE_SAMPLES, SLOTS], F32, tag="bank", bufs=3)
+                    for hb in range(HID_BLOCKS):
+                        nc.tensor.matmul(qk_ps[:].rearrange("p s n -> p (s n)"),
+                                         w_qk_sb[:, hb, (2 * t + c) * P:(2 * t + c + 1) * P],
+                                         mem0_bf16[:, hb, :], start=(hb == 0), stop=(hb == HID_BLOCKS - 1))
+                    r = 3 * t + c
+                    nc.scalar.activation(y[:, :, r * P:(r + 1) * P], qk_ps[:], FUNC.Identity,
+                                         bias=cols[:, COL_QKV_B + r:COL_QKV_B + r + 1])
+            v_bias = qkv_b_sb[:].rearrange("p (t c u) -> p t c u", c=3, u=P)[:, :, 2, :]
+            for s in range(PIECE_SAMPLES):
+                v_ps = psum.tile([P, HEADS, P], F32, tag="bank", bufs=3)
+                for hb in range(HID_BLOCKS):
+                    nc.tensor.matmul(v_ps[:].rearrange("p t u -> p (t u)"), mem0_bf16[:, hb, s * SLOTS:(s + 1) * SLOTS],
+                                     w_v_sb[:, hb, :], start=(hb == 0), stop=(hb == HID_BLOCKS - 1))
+                nc.vector.tensor_tensor(y[:, s, :].rearrange("p (t c u) -> p t c u", c=3, u=P)[:, :, 2, :],
+                                        v_ps[:], v_bias, ALU.add)
+
+        def normalise(g):
+            y = y_of_piece[g]
+            chunk_stats = stats.tile([P, PIECE_SAMPLES, PROJ // STAT_CHUNK, 6], F32)
+            moments = stats.tile([P, PIECE_SAMPLES, 2], F32)
+            for s in range(PIECE_SAMPLES):
+                for k in range(PROJ // STAT_CHUNK):
+                    nc.vector.bn_stats(chunk_stats[:, s, k, :], y[:, s, k * STAT_CHUNK:(k + 1) * STAT_CHUNK])
+                nc.vector.bn_aggr(moments[:, s, :], chunk_stats[:, s, :, :].rearrange("p k f -> p (k f)"))
+            mean_sq = stats.tile([P, PIECE_SAMPLES], F32)
+            nc.vector.tensor_tensor(mean_sq[:], moments[:, :, 0], moments[:, :, 0], ALU.mult)
+            nc.vector.tensor_tensor(moments[:, :, 1], moments[:, :, 1], mean_sq[:], ALU.add)
+            sample_ps = psum.tile([P, PIECE_SAMPLES, 2], F32, tag="other")
+            nc.tensor.matmul(sample_ps[:].rearrange("p s m -> p (s m)"), mean_over_partitions[:],
+                             moments[:].rearrange("p s m -> p (s m)"), start=True, stop=True)
+            sample_moments = stats.tile([P, PIECE_SAMPLES, 2], F32)
+            nc.vector.tensor_copy(sample_moments[:], sample_ps[:])
+            mu_sq = stats.tile([P, PIECE_SAMPLES], F32)
+            nc.vector.tensor_tensor(mu_sq[:], sample_moments[:, :, 0], sample_moments[:, :, 0], ALU.mult)
+            var = stats.tile([P, PIECE_SAMPLES], F32)
+            nc.vector.tensor_tensor(var[:], sample_moments[:, :, 1], mu_sq[:], ALU.subtract)
+            nc.vector.tensor_scalar(var[:], var[:], 0.0, EPS, ALU.max, ALU.add)
+            rstd = stats.tile([P, PIECE_SAMPLES], F32)
+            nc.gpsimd.tensor_tensor(rstd[:], var[:], minus_half[:], ALU.pow)
+
+            z = by_piece.tile([P, PIECE_SAMPLES, PROJ], BF16)
+            z_of_piece[g] = z
+            for s in range(PIECE_SAMPLES):
+                centred = by_sample.tile([P, PROJ], F32, bufs=2)
+                nc.vector.scalar_tensor_tensor(centred[:], y[:, s, :], sample_moments[:, s, 0:1], ln_gain[:],
+                                               ALU.subtract, ALU.mult)
+                nc.vector.scalar_tensor_tensor(z[:, s, :], centred[:], rstd[:, s:s + 1], ln_bias[:],
+                                               ALU.mult, ALU.add)
+
+        def attend_and_mlp(g, s):
+            b = g * PIECE_SAMPLES + s
+            sample = slice(b * SLOTS, (b + 1) * SLOTS)
+            q_k_v = z_of_piece[g][:, s, :].rearrange("p (t c n) -> p t c n", c=3, n=P)
+
+            scores = psum.tile([P, HEADS, SLOTS], F32, tag="scores")
+            for t in range(HEADS):
+                nc.tensor.matmul(scores[:, t, :], q_k_v[:, t, 0, :], q_k_v[:, t, 1, :], start=True, stop=True)
+            minus_max = stats.tile([P, HEADS], F32)
+            nc.vector.tensor_reduce(minus_max[:], scores[:], AXIS_X, ALU.max, negate=True)
+            exp_scores = by_sample.tile([P, HEADS, SLOTS], F32)
+            exp_sum = stats.tile([P, HEADS], F32)
+            for t in range(HEADS):
+                nc.scalar.activation(exp_scores[:, t, :], scores[:, t, :], FUNC.Exp,
+                                     bias=minus_max[:, t:t + 1], accum_out=exp_sum[:, t:t + 1])
+            exp_rsum = stats.tile([P, HEADS], F32)
+            nc.vector.reciprocal(exp_rsum[:], exp_sum[:])
+            att = by_sample.tile([P, HEADS, SLOTS], BF16)
+            for t in range(HEADS):
+                nc.scalar.activation(att[:, t, :], exp_scores[:, t, :], FUNC.Copy, scale=exp_rsum[:, t:t + 1])
+            att_flipped_ps = psum.tile([P, HEADS, SLOTS], BF16, tag="att_flipped")
+            for t in range(HEADS):
+                nc.tensor.transpose(att_flipped_ps[:, t, :], att[:, t, :], identity_bf16[:])
+            att_flipped = by_sample.tile([P, HEADS, SLOTS], BF16)
+            nc.scalar.activation(att_flipped[:], att_flipped_ps[:], FUNC.Copy)
+            o_ps = psum.tile([P, HEADS, SLOTS], F32, tag="o")
+            for t in range(HEADS):
+                nc.tensor.matmul(o_ps[:, t, :], q_k_v[:, t, 2, :], att_flipped[:, t, :], start=True, stop=True)
+
+            mem1 = by_sample.tile([P, HID_BLOCKS, SLOTS], F32, bufs=4)
+            nc.vector.tensor_tensor(mem1[:], o_ps[:], mem[:, :, sample], ALU.add)
+
+            relu_mem1 = by_sample.tile([P, HID_BLOCKS, SLOTS], BF16)
+            nc.scalar.activation(relu_mem1[:], mem1[:], FUNC.Relu)
+            f_ps = psum.tile([P, HID], F32, tag="f")
+            for hb in range(HID_BLOCKS):
+                nc.tensor.matmul(f_ps[:], relu_mem1[:, hb, :], mlp_w_sb[:, hb, :],
+                                 start=(hb == 0), stop=(hb == HID_BLOCKS - 1))
+            f = by_sample.tile([P, HID], F32)
+            nc.vector.tensor_tensor(f[:], f_ps[:], mlp_b_sb[:], ALU.add)
+            f_stats = stats.tile([P, 6], F32)
+            nc.vector.bn_stats(f_stats[:], f[:])
+            f_moments = stats.tile([P, 2], F32)
+            nc.vector.bn_aggr(f_moments[:], f_stats[:])
+            var2 = stats.tile([P, 1], F32)
+            nc.vector.tensor_scalar_add(var2[:], f_moments[:, 1:2], EPS)
+            rstd2 = stats.tile([P, 1], F32)
+            nc.gpsimd.tensor_tensor(rstd2[:], var2[:], minus_half[:, 0:1], ALU.pow)
+            shift2 = stats.tile([P, 1], F32)
+            nc.vector.scalar_tensor_tensor(shift2[:], f_moments[:, 0:1], -1.0, rstd2[:], ALU.mult, ALU.mult)
+            normed = by_sample.tile([P, HID], F32)
+            nc.scalar.activation(normed[:], f[:], FUNC.Identity, bias=shift2[:], scale=rstd2[:])
+
+            normed_flipped = psum.tile([P, HID_BLOCKS, SLOTS], F32, tag="other")
+            for rb in range(HID_BLOCKS):
+                nc.tensor.transpose(normed_flipped[:, rb, :], normed[:, rb * P:(rb + 1) * P], identity_f32[:])
+            scaled = by_sample.tile([P, HID_BLOCKS, SLOTS], F32)
+            for rb in range(HID_BLOCKS):
+                nc.scalar.activation(scaled[:, rb, :], normed_flipped[:, rb, :], FUNC.Identity,
+                                     bias=cols[:, COL_MLP_LN_B + rb:COL_MLP_LN_B + rb + 1],
+                                     scale=cols[:, COL_MLP_LN_W + rb:COL_MLP_LN_W + rb + 1])
+            result = by_sample.tile([P, HID_BLOCKS, SLOTS], F32)
+            nc.gpsimd.tensor_tensor(result[:], scaled[:], mem1[:], ALU.add)
+            nc.sync.dma_start(out_blocks[:, :, sample], result[:])
+
+        for g in range(AHEAD):
+            project(g)
+        for g in range(PIECES):
+            normalise(g)
+            for s in range(PIECE_SAMPLES):
+                attend_and_mlp(g, s)
+            if g + AHEAD < PIECES:
+                project(g + AHEAD)

@@ -28,7 +28,6 @@ PIECE = 256
 PIECES = N_TOK // PIECE
 PIECE_SAMPLES = PIECE // SLOTS
 AHEAD = 2
-STAT_CHUNK = 512
 EPS = 1e-5
 Q_SCALE = 128.0 ** -0.5
 
@@ -38,6 +37,14 @@ COL_MLP_LN_W = 8
 COL_MLP_LN_B = 12
 COL_QKV_B = 16
 N_COLS = 28
+
+SBUF_RINGS = (
+    ("y", 3), ("z", 3), ("centred", 2), ("qk_sum", 3), ("v_sum", 3), ("y_sum", 3), ("sq_sum", 3), ("squares", 1), ("sample_moments", 3),
+    ("mu_sq", 3), ("var", 3), ("rstd", 3), ("exp_scores", 2), ("att", 3), ("att_flipped", 3), ("mem1", 4),
+    ("relu_mem1", 3), ("f", 2), ("normed", 2), ("scaled", 2), ("result", 3), ("minus_max", 3), ("exp_sum", 3),
+    ("exp_rsum", 3), ("f_stats", 3), ("f_moments", 3), ("var2", 3), ("rstd2", 3),
+)
+PSUM_RINGS = (("bank", 3), ("scores", 1), ("att_flipped", 1), ("o", 1), ("f", 1), ("flipped", 1))
 
 FLOPS = 2 * (128 + 256) * HID * N_TOK + 2 * 256 * HID * N_SAMPLES + 2 * HID * PROJ * N_TOK \
     + 2 * 2 * HEADS * N_SAMPLES * SLOTS * SLOTS * P + 2 * HID * HID * N_TOK
@@ -50,15 +57,22 @@ def tile_rsaffdecoder_b_kernel(
     nc = tc.nc
     with ExitStack() as ctx:
         held = ctx.enter_context(tc.tile_pool(name="held", bufs=1))
-        by_piece = ctx.enter_context(tc.tile_pool(name="by_piece", bufs=3))
-        by_sample = ctx.enter_context(tc.tile_pool(name="by_sample", bufs=3))
-        stats = ctx.enter_context(tc.tile_pool(name="stats", bufs=6))
+        ring = {kind: ctx.enter_context(tc.tile_pool(name=kind, bufs=bufs)) for kind, bufs in SBUF_RINGS}
 
         identity_f32 = held.tile([P, P], F32)
         make_identity(nc, identity_f32[:])
         identity_bf16 = held.tile([P, P], BF16)
         nc.vector.tensor_copy(identity_bf16[:], identity_f32[:])
 
+        edist = held.tile([P, N_TOK], F32)
+        nc.sync.dma_start(edist[:], distances.rearrange("o n -> (o n)").partition_broadcast(P))
+        w_qry_sb = held.tile([P, EMB_BLOCKS, HID], BF16)
+        nc.sync.dma_start(w_qry_sb[:], w_qry.rearrange("(k p) h -> p k h", p=P))
+        w_emb_sb = held.tile([P, EMB_BLOCKS, HID], BF16)
+        nc.sync.dma_start(w_emb_sb[:], w_emb.rearrange("(k p) h -> p k h", p=P))
+        emb_sb = held.tile([P, EMB_BLOCKS, N_TOK], BF16)
+        emb_blocks = emb.rearrange("(k p) n -> p k n", p=P)
+        nc.sync.dma_start(emb_sb[:, :, 0:LOOKUP], emb_blocks[:, :, 0:LOOKUP])
         offsets = held.tile([P, N_TOK // 16], U16, name="offsets")
         nc.sync.dma_start(offsets[:], offs)
         w_lab_sb = held.tile([P, HID], BF16)
@@ -68,22 +82,12 @@ def tile_rsaffdecoder_b_kernel(
 
         rows = held.tile([P, P], F32)
         nc.vector.memset(rows[:], 0.0)
-        edist = held.tile([P, N_TOK], F32)
-        nc.scalar.dma_start(edist[:], distances.rearrange("o n -> (o n)").partition_broadcast(P))
         for vector, col in ((w_dist, COL_W_DIST), (pre_b, COL_PRE_B), (mlp_ln_w, COL_MLP_LN_W),
                             (mlp_ln_b, COL_MLP_LN_B), (qkv_b, COL_QKV_B)):
             as_rows = vector.rearrange("(k p) o -> k (p o)", p=P)
             nc.scalar.dma_start(rows[col:col + as_rows.shape[0], :], as_rows)
-
-        w_emb_sb = held.tile([P, EMB_BLOCKS, HID], BF16)
-        nc.sync.dma_start(w_emb_sb[:], w_emb.rearrange("(k p) h -> p k h", p=P))
-        emb_sb = held.tile([P, EMB_BLOCKS, N_TOK], BF16)
-        emb_blocks = emb.rearrange("(k p) n -> p k n", p=P)
-        nc.sync.dma_start(emb_sb[:, :, 0:LOOKUP], emb_blocks[:, :, 0:LOOKUP])
         query_sb = held.tile([P, EMB_BLOCKS, N_SAMPLES], BF16)
-        nc.sync.dma_start(query_sb[:], query.rearrange("(k p) b -> p k b", p=P))
-        w_qry_sb = held.tile([P, EMB_BLOCKS, HID], BF16)
-        nc.sync.dma_start(w_qry_sb[:], w_qry.rearrange("(k p) h -> p k h", p=P))
+        nc.scalar.dma_start(query_sb[:], query.rearrange("(k p) b -> p k b", p=P))
 
         w_qk_sb = held.tile([P, HID_BLOCKS, 2 * HEADS * P], BF16)
         w_v_sb = held.tile([P, HID_BLOCKS, HID], BF16)
@@ -109,8 +113,8 @@ def tile_rsaffdecoder_b_kernel(
         mlp_w_sb = held.tile([P, HID_BLOCKS, HID], BF16)
         nc.sync.dma_start(mlp_w_sb[:], mlp_w.rearrange("(hb p) r -> p hb r", p=P))
 
-        mean_over_partitions = held.tile([P, P], F32)
-        nc.vector.memset(mean_over_partitions[:], 1.0 / P)
+        spread_mean = held.tile([P, P], F32)
+        nc.vector.memset(spread_mean[:], 1.0 / (P * PROJ))
         minus_half = held.tile([P, PIECE_SAMPLES], F32)
         nc.vector.memset(minus_half[:], -0.5)
         scratch = held.tile([P, 1], F32)
@@ -118,16 +122,40 @@ def tile_rsaffdecoder_b_kernel(
         nc.scalar.activation(scratch[:], scratch[:], FUNC.Exp)
 
         mem = held.tile([P, HID_BLOCKS, N_TOK], F32)
+        mem0_bf16 = held.tile([P, HID_BLOCKS, N_TOK], BF16)
         cols = held.tile([P, N_COLS], F32)
+        query_term = held.tile([P, HID_BLOCKS, N_SAMPLES], F32)
         w_dist_scaled = held.tile([P, HID_BLOCKS, N_SAMPLES], F32)
         dist_min = held.tile([P, N_SAMPLES], F32)
         edist_sum = held.tile([P, N_SAMPLES], F32)
         edist_rsum = held.tile([P, N_SAMPLES], F32)
 
-        with tc.psum_pool(name="first_psum", bufs=1) as first_psum:
-            cols_ps = first_psum.tile([P, P], F32)
+        def add_emb(u, banks, bufs):
+            lookup = slice(u * LOOKUP, (u + 1) * LOOKUP)
+            for hb in range(HID_BLOCKS):
+                emb_ps = banks.tile([P, LOOKUP], F32, tag="bank", bufs=bufs)
+                for kb in range(EMB_BLOCKS):
+                    nc.tensor.matmul(emb_ps[:], w_emb_sb[:, kb, hb * P:(hb + 1) * P], emb_sb[:, kb, lookup],
+                                     start=(kb == 0), stop=(kb == EMB_BLOCKS - 1))
+                nc.vector.tensor_tensor(mem[:, hb, lookup], emb_ps[:], mem[:, hb, lookup], ALU.add)
+
+        def round_mem0(u):
+            lookup = slice(u * LOOKUP, (u + 1) * LOOKUP)
+            for hb in range(HID_BLOCKS):
+                nc.scalar.activation(mem0_bf16[:, hb, lookup], mem[:, hb, lookup], FUNC.Copy)
+
+        with tc.psum_pool(name="setup_psum", bufs=1) as setup_psum:
+            cols_ps = setup_psum.tile([P, P], F32)
             nc.tensor.transpose(cols_ps[:], rows[:], identity_f32[:])
             nc.vector.tensor_copy(cols[:], cols_ps[:, 0:N_COLS])
+            query_ps = setup_psum.tile([P, HID_BLOCKS, N_SAMPLES], F32)
+            for hb in range(HID_BLOCKS):
+                for kb in range(EMB_BLOCKS):
+                    nc.tensor.matmul(query_ps[:, hb, :], w_qry_sb[:, kb, hb * P:(hb + 1) * P], query_sb[:, kb, :],
+                                     start=(kb == 0), stop=(kb == EMB_BLOCKS - 1))
+            pre_b_cols = cols[:, COL_PRE_B:COL_PRE_B + HID_BLOCKS].unsqueeze(2)
+            nc.vector.tensor_tensor(query_term[:], query_ps[:],
+                                    pre_b_cols.to_broadcast([P, HID_BLOCKS, N_SAMPLES]), ALU.add)
 
             for u in range(LOOKUPS):
                 group = slice(u * LOOKUP_SAMPLES, (u + 1) * LOOKUP_SAMPLES)
@@ -142,108 +170,94 @@ def tile_rsaffdecoder_b_kernel(
                 for hb in range(HID_BLOCKS):
                     nc.vector.tensor_scalar_mul(w_dist_scaled[:, hb, group], edist_rsum[:, group],
                                                 cols[:, COL_W_DIST + hb:COL_W_DIST + hb + 1])
+                    for b in range(u * LOOKUP_SAMPLES, (u + 1) * LOOKUP_SAMPLES):
+                        sample = slice(b * SLOTS, (b + 1) * SLOTS)
+                        nc.scalar.activation(mem[:, hb, sample], edist[:, sample], FUNC.Identity,
+                                             bias=query_term[:, hb, b:b + 1], scale=w_dist_scaled[:, hb, b:b + 1])
+                if u == 0:
+                    add_emb(0, setup_psum, 4)
 
+        with tc.psum_pool(name="label_psum", bufs=8) as label_psum:
             for u in range(LOOKUPS):
+                lookup = slice(u * LOOKUP, (u + 1) * LOOKUP)
                 lookup_offsets = offsets[:, u * (LOOKUP // 16):(u + 1) * (LOOKUP // 16)]
                 for hb in range(HID_BLOCKS):
-                    label_ps = first_psum.tile([P, LOOKUP_SAMPLES, SLOTS], F32, bufs=7)
-                    nc.tensor.matmul(label_ps[:].rearrange("p s n -> p (s n)"), w_lab_sb[:, hb * P:(hb + 1) * P],
+                    label_ps = label_psum.tile([P, LOOKUP], F32)
+                    nc.tensor.matmul(label_ps[:], w_lab_sb[:, hb * P:(hb + 1) * P],
                                      table_sb[:].indirect(lookup_offsets), start=True, stop=True)
-                    for s in range(LOOKUP_SAMPLES):
-                        b = u * LOOKUP_SAMPLES + s
-                        sample = slice(b * SLOTS, (b + 1) * SLOTS)
-                        nc.vector.scalar_tensor_tensor(mem[:, hb, sample], edist[:, sample],
-                                                       w_dist_scaled[:, hb, b:b + 1], label_ps[:, s, :],
-                                                       ALU.mult, ALU.add)
+                    nc.vector.tensor_tensor(mem[:, hb, lookup], label_ps[:], mem[:, hb, lookup], ALU.add)
+            round_mem0(0)
 
-        psum = ctx.enter_context(tc.psum_pool(name="psum", bufs=1))
-
-        query_term = held.tile([P, HID_BLOCKS, N_SAMPLES], F32)
-        query_ps = psum.tile([P, HID_BLOCKS, N_SAMPLES], F32, tag="other")
-        for hb in range(HID_BLOCKS):
-            for kb in range(EMB_BLOCKS):
-                nc.tensor.matmul(query_ps[:, hb, :], w_qry_sb[:, kb, hb * P:(hb + 1) * P], query_sb[:, kb, :],
-                                 start=(kb == 0), stop=(kb == EMB_BLOCKS - 1))
-            nc.vector.tensor_scalar_add(query_term[:, hb, :], query_ps[:, hb, :],
-                                        cols[:, COL_PRE_B + hb:COL_PRE_B + hb + 1])
-
-        for param in (ln_gain, ln_bias):
-            by_kind = param[:].rearrange("p (t c n) -> p t c n", c=3, n=SLOTS)
-            v_flipped = psum.tile([P, HEADS, P], F32, tag="other")
-            for t in range(HEADS):
-                nc.tensor.transpose(v_flipped[:, t, :], by_kind[:, t, 2, :], identity_f32[:])
-            nc.vector.tensor_copy(by_kind[:, :, 2, :], v_flipped[:])
-            nc.vector.tensor_scalar_mul(by_kind[:, :, 0, :], by_kind[:, :, 0, :], Q_SCALE)
+        psum_ring = {kind: ctx.enter_context(tc.psum_pool(name="psum_" + kind, bufs=bufs)) for kind, bufs in PSUM_RINGS}
 
         out_blocks = out.rearrange("(rb p) n -> p rb n", p=P)
         y_of_piece = {}
         z_of_piece = {}
+        mu_rstd_of_piece = {}
+        sums_of_piece = {}
 
         def project(g):
             piece = slice(g * PIECE, (g + 1) * PIECE)
-            for hb in range(HID_BLOCKS):
-                emb_ps = psum.tile([P, PIECE_SAMPLES, SLOTS], F32, tag="bank", bufs=3)
-                for kb in range(EMB_BLOCKS):
-                    nc.tensor.matmul(emb_ps[:].rearrange("p s n -> p (s n)"), w_emb_sb[:, kb, hb * P:(hb + 1) * P],
-                                     emb_sb[:, kb, piece], start=(kb == 0), stop=(kb == EMB_BLOCKS - 1))
-                for s in range(PIECE_SAMPLES):
-                    b = g * PIECE_SAMPLES + s
-                    sample = slice(b * SLOTS, (b + 1) * SLOTS)
-                    nc.vector.scalar_tensor_tensor(mem[:, hb, sample], emb_ps[:, s, :], query_term[:, hb, b:b + 1],
-                                                   mem[:, hb, sample], ALU.add, ALU.add)
-            mem0_bf16 = by_piece.tile([P, HID_BLOCKS, PIECE], BF16)
-            nc.scalar.activation(mem0_bf16[:], mem[:, :, piece], FUNC.Copy)
-
-            y = by_piece.tile([P, PIECE_SAMPLES, PROJ], F32)
+            y = ring["y"].tile([P, PIECE_SAMPLES, PROJ], F32)
             y_of_piece[g] = y
+            qk_sum = ring["qk_sum"].tile([P, PIECE_SAMPLES, 2 * HEADS], F32)
+            v_sum = ring["v_sum"].tile([P, PIECE_SAMPLES], F32)
+            sums_of_piece[g] = (qk_sum, v_sum)
             for t in range(HEADS):
                 for c in range(2):
-                    qk_ps = psum.tile([P, PIECE_SAMPLES, SLOTS], F32, tag="bank", bufs=3)
+                    qk_ps = psum_ring["bank"].tile([P, PIECE_SAMPLES, SLOTS], F32, tag="bank")
                     for hb in range(HID_BLOCKS):
                         nc.tensor.matmul(qk_ps[:].rearrange("p s n -> p (s n)"),
                                          w_qk_sb[:, hb, (2 * t + c) * P:(2 * t + c + 1) * P],
-                                         mem0_bf16[:, hb, :], start=(hb == 0), stop=(hb == HID_BLOCKS - 1))
+                                         mem0_bf16[:, hb, piece], start=(hb == 0), stop=(hb == HID_BLOCKS - 1))
                     r = 3 * t + c
-                    nc.scalar.activation(y[:, :, r * P:(r + 1) * P], qk_ps[:], FUNC.Identity,
-                                         bias=cols[:, COL_QKV_B + r:COL_QKV_B + r + 1])
+                    for s in range(PIECE_SAMPLES):
+                        nc.scalar.activation(y[:, s, r * P:(r + 1) * P], qk_ps[:, s, :], FUNC.Identity,
+                                             bias=cols[:, COL_QKV_B + r:COL_QKV_B + r + 1],
+                                             accum_out=qk_sum[:, s, 2 * t + c:2 * t + c + 1])
             v_bias = qkv_b_sb[:].rearrange("p (t c u) -> p t c u", c=3, u=P)[:, :, 2, :]
             for s in range(PIECE_SAMPLES):
-                v_ps = psum.tile([P, HEADS, P], F32, tag="bank", bufs=3)
+                b = g * PIECE_SAMPLES + s
+                v_ps = psum_ring["bank"].tile([P, HEADS, P], F32, tag="bank")
                 for hb in range(HID_BLOCKS):
-                    nc.tensor.matmul(v_ps[:].rearrange("p t u -> p (t u)"), mem0_bf16[:, hb, s * SLOTS:(s + 1) * SLOTS],
+                    nc.tensor.matmul(v_ps[:].rearrange("p t u -> p (t u)"), mem0_bf16[:, hb, b * SLOTS:(b + 1) * SLOTS],
                                      w_v_sb[:, hb, :], start=(hb == 0), stop=(hb == HID_BLOCKS - 1))
-                nc.vector.tensor_tensor(y[:, s, :].rearrange("p (t c u) -> p t c u", c=3, u=P)[:, :, 2, :],
-                                        v_ps[:], v_bias, ALU.add)
+                nc.vector.scalar_tensor_tensor(y[:, s, :].rearrange("p (t c u) -> p t c u", c=3, u=P)[:, :, 2, :],
+                                               v_ps[:], 1.0, v_bias, ALU.mult, ALU.add,
+                                               accum_out=v_sum[:, s:s + 1])
+
+        def measure(g):
+            y = y_of_piece[g]
+            qk_sum, v_sum = sums_of_piece[g]
+            y_sum = ring["y_sum"].tile([P, PIECE_SAMPLES], F32)
+            nc.vector.tensor_reduce(y_sum[:], qk_sum[:], AXIS_X, ALU.add)
+            nc.vector.tensor_tensor(y_sum[:], y_sum[:], v_sum[:], ALU.add)
+            sq_sum = ring["sq_sum"].tile([P, PIECE_SAMPLES], F32)
+            for s in range(PIECE_SAMPLES):
+                squares = ring["squares"].tile([P, PROJ], BF16)
+                nc.scalar.activation(squares[:], y[:, s, :], FUNC.Square, accum_out=sq_sum[:, s:s + 1])
+            sample_ps = psum_ring["scores"].tile([P, 2, PIECE_SAMPLES], F32, tag="scores")
+            nc.tensor.matmul(sample_ps[:, 0, :], spread_mean[:], y_sum[:], start=True, stop=True)
+            nc.tensor.matmul(sample_ps[:, 1, :], spread_mean[:], sq_sum[:], start=True, stop=True)
+            sample_moments = ring["sample_moments"].tile([P, 2, PIECE_SAMPLES], F32)
+            nc.vector.tensor_copy(sample_moments[:], sample_ps[:])
+            mu_sq = ring["mu_sq"].tile([P, PIECE_SAMPLES], F32)
+            nc.vector.tensor_tensor(mu_sq[:], sample_moments[:, 0, :], sample_moments[:, 0, :], ALU.mult)
+            var = ring["var"].tile([P, PIECE_SAMPLES], F32)
+            nc.vector.tensor_tensor(var[:], sample_moments[:, 1, :], mu_sq[:], ALU.subtract)
+            nc.vector.tensor_scalar(var[:], var[:], 0.0, EPS, ALU.max, ALU.add)
+            rstd = ring["rstd"].tile([P, PIECE_SAMPLES], F32)
+            nc.gpsimd.tensor_tensor(rstd[:], var[:], minus_half[:], ALU.pow)
+            mu_rstd_of_piece[g] = (sample_moments, rstd)
 
         def normalise(g):
             y = y_of_piece[g]
-            chunk_stats = stats.tile([P, PIECE_SAMPLES, PROJ // STAT_CHUNK, 6], F32)
-            moments = stats.tile([P, PIECE_SAMPLES, 2], F32)
-            for s in range(PIECE_SAMPLES):
-                for k in range(PROJ // STAT_CHUNK):
-                    nc.vector.bn_stats(chunk_stats[:, s, k, :], y[:, s, k * STAT_CHUNK:(k + 1) * STAT_CHUNK])
-                nc.vector.bn_aggr(moments[:, s, :], chunk_stats[:, s, :, :].rearrange("p k f -> p (k f)"))
-            mean_sq = stats.tile([P, PIECE_SAMPLES], F32)
-            nc.vector.tensor_tensor(mean_sq[:], moments[:, :, 0], moments[:, :, 0], ALU.mult)
-            nc.vector.tensor_tensor(moments[:, :, 1], moments[:, :, 1], mean_sq[:], ALU.add)
-            sample_ps = psum.tile([P, PIECE_SAMPLES, 2], F32, tag="other")
-            nc.tensor.matmul(sample_ps[:].rearrange("p s m -> p (s m)"), mean_over_partitions[:],
-                             moments[:].rearrange("p s m -> p (s m)"), start=True, stop=True)
-            sample_moments = stats.tile([P, PIECE_SAMPLES, 2], F32)
-            nc.vector.tensor_copy(sample_moments[:], sample_ps[:])
-            mu_sq = stats.tile([P, PIECE_SAMPLES], F32)
-            nc.vector.tensor_tensor(mu_sq[:], sample_moments[:, :, 0], sample_moments[:, :, 0], ALU.mult)
-            var = stats.tile([P, PIECE_SAMPLES], F32)
-            nc.vector.tensor_tensor(var[:], sample_moments[:, :, 1], mu_sq[:], ALU.subtract)
-            nc.vector.tensor_scalar(var[:], var[:], 0.0, EPS, ALU.max, ALU.add)
-            rstd = stats.tile([P, PIECE_SAMPLES], F32)
-            nc.gpsimd.tensor_tensor(rstd[:], var[:], minus_half[:], ALU.pow)
-
-            z = by_piece.tile([P, PIECE_SAMPLES, PROJ], BF16)
+            sample_moments, rstd = mu_rstd_of_piece[g]
+            z = ring["z"].tile([P, PIECE_SAMPLES, PROJ], BF16)
             z_of_piece[g] = z
             for s in range(PIECE_SAMPLES):
-                centred = by_sample.tile([P, PROJ], F32, bufs=2)
-                nc.vector.scalar_tensor_tensor(centred[:], y[:, s, :], sample_moments[:, s, 0:1], ln_gain[:],
+                centred = ring["centred"].tile([P, PROJ], F32)
+                nc.vector.scalar_tensor_tensor(centred[:], y[:, s, :], sample_moments[:, 0, s:s + 1], ln_gain[:],
                                                ALU.subtract, ALU.mult)
                 nc.vector.scalar_tensor_tensor(z[:, s, :], centred[:], rstd[:, s:s + 1], ln_bias[:],
                                                ALU.mult, ALU.add)
@@ -253,71 +267,86 @@ def tile_rsaffdecoder_b_kernel(
             sample = slice(b * SLOTS, (b + 1) * SLOTS)
             q_k_v = z_of_piece[g][:, s, :].rearrange("p (t c n) -> p t c n", c=3, n=P)
 
-            scores = psum.tile([P, HEADS, SLOTS], F32, tag="scores")
+            scores = psum_ring["scores"].tile([P, HEADS, SLOTS], F32, tag="scores")
             for t in range(HEADS):
                 nc.tensor.matmul(scores[:, t, :], q_k_v[:, t, 0, :], q_k_v[:, t, 1, :], start=True, stop=True)
-            minus_max = stats.tile([P, HEADS], F32)
+            minus_max = ring["minus_max"].tile([P, HEADS], F32)
             nc.vector.tensor_reduce(minus_max[:], scores[:], AXIS_X, ALU.max, negate=True)
-            exp_scores = by_sample.tile([P, HEADS, SLOTS], F32)
-            exp_sum = stats.tile([P, HEADS], F32)
+            exp_scores = ring["exp_scores"].tile([P, HEADS, SLOTS], F32)
+            exp_sum = ring["exp_sum"].tile([P, HEADS], F32)
             for t in range(HEADS):
                 nc.scalar.activation(exp_scores[:, t, :], scores[:, t, :], FUNC.Exp,
                                      bias=minus_max[:, t:t + 1], accum_out=exp_sum[:, t:t + 1])
-            exp_rsum = stats.tile([P, HEADS], F32)
+            exp_rsum = ring["exp_rsum"].tile([P, HEADS], F32)
             nc.vector.reciprocal(exp_rsum[:], exp_sum[:])
-            att = by_sample.tile([P, HEADS, SLOTS], BF16)
+            att = ring["att"].tile([P, HEADS, SLOTS], BF16)
             for t in range(HEADS):
                 nc.scalar.activation(att[:, t, :], exp_scores[:, t, :], FUNC.Copy, scale=exp_rsum[:, t:t + 1])
-            att_flipped_ps = psum.tile([P, HEADS, SLOTS], BF16, tag="att_flipped")
+            att_flipped_ps = psum_ring["att_flipped"].tile([P, HEADS, SLOTS], BF16, tag="att_flipped")
             for t in range(HEADS):
                 nc.tensor.transpose(att_flipped_ps[:, t, :], att[:, t, :], identity_bf16[:])
-            att_flipped = by_sample.tile([P, HEADS, SLOTS], BF16)
+            att_flipped = ring["att_flipped"].tile([P, HEADS, SLOTS], BF16)
             nc.scalar.activation(att_flipped[:], att_flipped_ps[:], FUNC.Copy)
-            o_ps = psum.tile([P, HEADS, SLOTS], F32, tag="o")
+            o_ps = psum_ring["o"].tile([P, HEADS, SLOTS], F32, tag="o")
             for t in range(HEADS):
                 nc.tensor.matmul(o_ps[:, t, :], q_k_v[:, t, 2, :], att_flipped[:, t, :], start=True, stop=True)
 
-            mem1 = by_sample.tile([P, HID_BLOCKS, SLOTS], F32, bufs=4)
+            mem1 = ring["mem1"].tile([P, HID_BLOCKS, SLOTS], F32)
             nc.vector.tensor_tensor(mem1[:], o_ps[:], mem[:, :, sample], ALU.add)
 
-            relu_mem1 = by_sample.tile([P, HID_BLOCKS, SLOTS], BF16)
+            relu_mem1 = ring["relu_mem1"].tile([P, HID_BLOCKS, SLOTS], BF16)
             nc.scalar.activation(relu_mem1[:], mem1[:], FUNC.Relu)
-            f_ps = psum.tile([P, HID], F32, tag="f")
+            f_ps = psum_ring["f"].tile([P, HID], F32, tag="f")
             for hb in range(HID_BLOCKS):
                 nc.tensor.matmul(f_ps[:], relu_mem1[:, hb, :], mlp_w_sb[:, hb, :],
                                  start=(hb == 0), stop=(hb == HID_BLOCKS - 1))
-            f = by_sample.tile([P, HID], F32)
+            f = ring["f"].tile([P, HID], F32)
             nc.vector.tensor_tensor(f[:], f_ps[:], mlp_b_sb[:], ALU.add)
-            f_stats = stats.tile([P, 6], F32)
+            f_stats = ring["f_stats"].tile([P, 6], F32)
             nc.vector.bn_stats(f_stats[:], f[:])
-            f_moments = stats.tile([P, 2], F32)
+            f_moments = ring["f_moments"].tile([P, 2], F32)
             nc.vector.bn_aggr(f_moments[:], f_stats[:])
-            var2 = stats.tile([P, 1], F32)
+            var2 = ring["var2"].tile([P, 1], F32)
             nc.vector.tensor_scalar_add(var2[:], f_moments[:, 1:2], EPS)
-            rstd2 = stats.tile([P, 1], F32)
+            rstd2 = ring["rstd2"].tile([P, 1], F32)
             nc.gpsimd.tensor_tensor(rstd2[:], var2[:], minus_half[:, 0:1], ALU.pow)
-            shift2 = stats.tile([P, 1], F32)
-            nc.vector.scalar_tensor_tensor(shift2[:], f_moments[:, 0:1], -1.0, rstd2[:], ALU.mult, ALU.mult)
-            normed = by_sample.tile([P, HID], F32)
-            nc.scalar.activation(normed[:], f[:], FUNC.Identity, bias=shift2[:], scale=rstd2[:])
+            normed = ring["normed"].tile([P, HID], F32)
+            nc.vector.tensor_scalar(normed[:], f[:], f_moments[:, 0:1], rstd2[:], ALU.subtract, ALU.mult)
 
-            normed_flipped = psum.tile([P, HID_BLOCKS, SLOTS], F32, tag="other")
+            normed_flipped = psum_ring["flipped"].tile([P, HID_BLOCKS, SLOTS], F32, tag="flipped")
             for rb in range(HID_BLOCKS):
                 nc.tensor.transpose(normed_flipped[:, rb, :], normed[:, rb * P:(rb + 1) * P], identity_f32[:])
-            scaled = by_sample.tile([P, HID_BLOCKS, SLOTS], F32)
+            scaled = ring["scaled"].tile([P, HID_BLOCKS, SLOTS], F32)
             for rb in range(HID_BLOCKS):
                 nc.scalar.activation(scaled[:, rb, :], normed_flipped[:, rb, :], FUNC.Identity,
                                      bias=cols[:, COL_MLP_LN_B + rb:COL_MLP_LN_B + rb + 1],
                                      scale=cols[:, COL_MLP_LN_W + rb:COL_MLP_LN_W + rb + 1])
-            result = by_sample.tile([P, HID_BLOCKS, SLOTS], F32)
+            result = ring["result"].tile([P, HID_BLOCKS, SLOTS], F32)
             nc.gpsimd.tensor_tensor(result[:], scaled[:], mem1[:], ALU.add)
             nc.sync.dma_start(out_blocks[:, :, sample], result[:])
 
         for g in range(AHEAD):
             project(g)
+        add_emb(1, psum_ring["bank"], 3)
+        round_mem0(1)
+
+        for param in (ln_gain, ln_bias):
+            by_kind = param[:].rearrange("p (t c n) -> p t c n", c=3, n=SLOTS)
+            v_flipped = psum_ring["flipped"].tile([P, HEADS, P], F32, tag="flipped")
+            for t in range(HEADS):
+                nc.tensor.transpose(v_flipped[:, t, :], by_kind[:, t, 2, :], identity_f32[:])
+            nc.vector.tensor_copy(by_kind[:, :, 2, :], v_flipped[:])
+            nc.vector.tensor_scalar_mul(by_kind[:, :, 0, :], by_kind[:, :, 0, :], Q_SCALE)
+
+        measure(0)
         for g in range(PIECES):
             normalise(g)
+            if g + 1 < PIECES:
+                measure(g + 1)
             for s in range(PIECE_SAMPLES):
                 attend_and_mlp(g, s)
             if g + AHEAD < PIECES:
                 project(g + AHEAD)
+            if g % 2 == 0 and g // 2 + 2 < LOOKUPS:
+                add_emb(g // 2 + 2, psum_ring["bank"], 3)
+                round_mem0(g // 2 + 2)

@@ -28,6 +28,7 @@ PIECE = 256
 PIECES = N_TOK // PIECE
 PIECE_SAMPLES = PIECE // SLOTS
 AHEAD = 2
+STAT_CHUNK = 512
 EPS = 1e-5
 Q_SCALE = 128.0 ** -0.5
 
@@ -39,10 +40,10 @@ COL_QKV_B = 16
 N_COLS = 28
 
 SBUF_RINGS = (
-    ("y", 3), ("z", 3), ("centred", 2), ("qk_sum", 3), ("v_sum", 3), ("y_sum", 3), ("sq_sum", 3), ("squares", 1), ("sample_moments", 3),
+    ("y", 3), ("z", 3), ("centred", 2), ("chunk_stats", 3), ("moments", 3), ("mean_sq", 3), ("sample_moments", 3),
     ("mu_sq", 3), ("var", 3), ("rstd", 3), ("exp_scores", 2), ("att", 3), ("att_flipped", 3), ("mem1", 4),
     ("relu_mem1", 3), ("f", 2), ("normed", 2), ("scaled", 2), ("result", 3), ("minus_max", 3), ("exp_sum", 3),
-    ("exp_rsum", 3), ("f_stats", 3), ("f_moments", 3), ("var2", 3), ("rstd2", 3),
+    ("exp_rsum", 3), ("f_stats", 3), ("f_moments", 3), ("var2", 3), ("rstd2", 3), ("shift2", 3),
 )
 PSUM_RINGS = (("bank", 3), ("scores", 1), ("att_flipped", 1), ("o", 1), ("f", 1), ("flipped", 1))
 
@@ -114,7 +115,7 @@ def tile_rsaffdecoder_b_kernel(
         nc.sync.dma_start(mlp_w_sb[:], mlp_w.rearrange("(hb p) r -> p hb r", p=P))
 
         spread_mean = held.tile([P, P], F32)
-        nc.vector.memset(spread_mean[:], 1.0 / (P * PROJ))
+        nc.vector.memset(spread_mean[:], 1.0 / P)
         minus_half = held.tile([P, PIECE_SAMPLES], F32)
         nc.vector.memset(minus_half[:], -0.5)
         scratch = held.tile([P, 1], F32)
@@ -194,15 +195,11 @@ def tile_rsaffdecoder_b_kernel(
         y_of_piece = {}
         z_of_piece = {}
         mu_rstd_of_piece = {}
-        sums_of_piece = {}
 
         def project(g):
             piece = slice(g * PIECE, (g + 1) * PIECE)
             y = ring["y"].tile([P, PIECE_SAMPLES, PROJ], F32)
             y_of_piece[g] = y
-            qk_sum = ring["qk_sum"].tile([P, PIECE_SAMPLES, 2 * HEADS], F32)
-            v_sum = ring["v_sum"].tile([P, PIECE_SAMPLES], F32)
-            sums_of_piece[g] = (qk_sum, v_sum)
             for t in range(HEADS):
                 for c in range(2):
                     qk_ps = psum_ring["bank"].tile([P, PIECE_SAMPLES, SLOTS], F32, tag="bank")
@@ -211,10 +208,8 @@ def tile_rsaffdecoder_b_kernel(
                                          w_qk_sb[:, hb, (2 * t + c) * P:(2 * t + c + 1) * P],
                                          mem0_bf16[:, hb, piece], start=(hb == 0), stop=(hb == HID_BLOCKS - 1))
                     r = 3 * t + c
-                    for s in range(PIECE_SAMPLES):
-                        nc.scalar.activation(y[:, s, r * P:(r + 1) * P], qk_ps[:, s, :], FUNC.Identity,
-                                             bias=cols[:, COL_QKV_B + r:COL_QKV_B + r + 1],
-                                             accum_out=qk_sum[:, s, 2 * t + c:2 * t + c + 1])
+                    nc.scalar.activation(y[:, :, r * P:(r + 1) * P], qk_ps[:], FUNC.Identity,
+                                         bias=cols[:, COL_QKV_B + r:COL_QKV_B + r + 1])
             v_bias = qkv_b_sb[:].rearrange("p (t c u) -> p t c u", c=3, u=P)[:, :, 2, :]
             for s in range(PIECE_SAMPLES):
                 b = g * PIECE_SAMPLES + s
@@ -222,29 +217,29 @@ def tile_rsaffdecoder_b_kernel(
                 for hb in range(HID_BLOCKS):
                     nc.tensor.matmul(v_ps[:].rearrange("p t u -> p (t u)"), mem0_bf16[:, hb, b * SLOTS:(b + 1) * SLOTS],
                                      w_v_sb[:, hb, :], start=(hb == 0), stop=(hb == HID_BLOCKS - 1))
-                nc.vector.scalar_tensor_tensor(y[:, s, :].rearrange("p (t c u) -> p t c u", c=3, u=P)[:, :, 2, :],
-                                               v_ps[:], 1.0, v_bias, ALU.mult, ALU.add,
-                                               accum_out=v_sum[:, s:s + 1])
+                nc.vector.tensor_tensor(y[:, s, :].rearrange("p (t c u) -> p t c u", c=3, u=P)[:, :, 2, :],
+                                        v_ps[:], v_bias, ALU.add)
 
         def measure(g):
             y = y_of_piece[g]
-            qk_sum, v_sum = sums_of_piece[g]
-            y_sum = ring["y_sum"].tile([P, PIECE_SAMPLES], F32)
-            nc.vector.tensor_reduce(y_sum[:], qk_sum[:], AXIS_X, ALU.add)
-            nc.vector.tensor_tensor(y_sum[:], y_sum[:], v_sum[:], ALU.add)
-            sq_sum = ring["sq_sum"].tile([P, PIECE_SAMPLES], F32)
+            chunk_stats = ring["chunk_stats"].tile([P, PIECE_SAMPLES, PROJ // STAT_CHUNK, 6], F32)
+            moments = ring["moments"].tile([P, PIECE_SAMPLES, 2], F32)
             for s in range(PIECE_SAMPLES):
-                squares = ring["squares"].tile([P, PROJ], BF16)
-                nc.scalar.activation(squares[:], y[:, s, :], FUNC.Square, accum_out=sq_sum[:, s:s + 1])
-            sample_ps = psum_ring["scores"].tile([P, 2, PIECE_SAMPLES], F32, tag="scores")
-            nc.tensor.matmul(sample_ps[:, 0, :], spread_mean[:], y_sum[:], start=True, stop=True)
-            nc.tensor.matmul(sample_ps[:, 1, :], spread_mean[:], sq_sum[:], start=True, stop=True)
-            sample_moments = ring["sample_moments"].tile([P, 2, PIECE_SAMPLES], F32)
+                for k in range(PROJ // STAT_CHUNK):
+                    nc.vector.bn_stats(chunk_stats[:, s, k, :], y[:, s, k * STAT_CHUNK:(k + 1) * STAT_CHUNK])
+                nc.vector.bn_aggr(moments[:, s, :], chunk_stats[:, s, :, :].rearrange("p k f -> p (k f)"))
+            mean_sq = ring["mean_sq"].tile([P, PIECE_SAMPLES], F32)
+            nc.vector.tensor_tensor(mean_sq[:], moments[:, :, 0], moments[:, :, 0], ALU.mult)
+            nc.vector.tensor_tensor(moments[:, :, 1], moments[:, :, 1], mean_sq[:], ALU.add)
+            sample_ps = psum_ring["scores"].tile([P, PIECE_SAMPLES, 2], F32, tag="scores")
+            nc.tensor.matmul(sample_ps[:].rearrange("p s m -> p (s m)"), spread_mean[:],
+                             moments[:].rearrange("p s m -> p (s m)"), start=True, stop=True)
+            sample_moments = ring["sample_moments"].tile([P, PIECE_SAMPLES, 2], F32)
             nc.vector.tensor_copy(sample_moments[:], sample_ps[:])
             mu_sq = ring["mu_sq"].tile([P, PIECE_SAMPLES], F32)
-            nc.vector.tensor_tensor(mu_sq[:], sample_moments[:, 0, :], sample_moments[:, 0, :], ALU.mult)
+            nc.vector.tensor_tensor(mu_sq[:], sample_moments[:, :, 0], sample_moments[:, :, 0], ALU.mult)
             var = ring["var"].tile([P, PIECE_SAMPLES], F32)
-            nc.vector.tensor_tensor(var[:], sample_moments[:, 1, :], mu_sq[:], ALU.subtract)
+            nc.vector.tensor_tensor(var[:], sample_moments[:, :, 1], mu_sq[:], ALU.subtract)
             nc.vector.tensor_scalar(var[:], var[:], 0.0, EPS, ALU.max, ALU.add)
             rstd = ring["rstd"].tile([P, PIECE_SAMPLES], F32)
             nc.gpsimd.tensor_tensor(rstd[:], var[:], minus_half[:], ALU.pow)
@@ -257,7 +252,7 @@ def tile_rsaffdecoder_b_kernel(
             z_of_piece[g] = z
             for s in range(PIECE_SAMPLES):
                 centred = ring["centred"].tile([P, PROJ], F32)
-                nc.vector.scalar_tensor_tensor(centred[:], y[:, s, :], sample_moments[:, 0, s:s + 1], ln_gain[:],
+                nc.vector.scalar_tensor_tensor(centred[:], y[:, s, :], sample_moments[:, s, 0:1], ln_gain[:],
                                                ALU.subtract, ALU.mult)
                 nc.vector.scalar_tensor_tensor(z[:, s, :], centred[:], rstd[:, s:s + 1], ln_bias[:],
                                                ALU.mult, ALU.add)
@@ -310,8 +305,10 @@ def tile_rsaffdecoder_b_kernel(
             nc.vector.tensor_scalar_add(var2[:], f_moments[:, 1:2], EPS)
             rstd2 = ring["rstd2"].tile([P, 1], F32)
             nc.gpsimd.tensor_tensor(rstd2[:], var2[:], minus_half[:, 0:1], ALU.pow)
+            shift2 = ring["shift2"].tile([P, 1], F32)
+            nc.vector.scalar_tensor_tensor(shift2[:], f_moments[:, 0:1], -1.0, rstd2[:], ALU.mult, ALU.mult)
             normed = ring["normed"].tile([P, HID], F32)
-            nc.vector.tensor_scalar(normed[:], f[:], f_moments[:, 0:1], rstd2[:], ALU.subtract, ALU.mult)
+            nc.scalar.activation(normed[:], f[:], FUNC.Identity, bias=shift2[:], scale=rstd2[:])
 
             normed_flipped = psum_ring["flipped"].tile([P, HID_BLOCKS, SLOTS], F32, tag="flipped")
             for rb in range(HID_BLOCKS):

@@ -28,7 +28,6 @@ PIECE = 256
 PIECES = N_TOK // PIECE
 PIECE_SAMPLES = PIECE // SLOTS
 AHEAD = 2
-STAT_CHUNK = 512
 EPS = 1e-5
 Q_SCALE = 128.0 ** -0.5
 
@@ -40,10 +39,10 @@ COL_QKV_B = 16
 N_COLS = 28
 
 SBUF_RINGS = (
-    ("y", 3), ("z", 3), ("centred", 2), ("chunk_stats", 3), ("moments", 3), ("mean_sq", 3), ("sample_moments", 3),
-    ("mu_sq", 3), ("var", 3), ("rstd", 3), ("exp_scores", 2), ("att", 3), ("att_flipped", 3), ("mem1", 4),
-    ("relu_mem1", 3), ("f", 2), ("normed", 2), ("scaled", 2), ("result", 3), ("minus_max", 3), ("exp_sum", 3),
-    ("exp_rsum", 3), ("f_stats", 3), ("f_moments", 3), ("var2", 3), ("rstd2", 3), ("shift2", 3),
+    ("y", 3), ("z", 3), ("centred", 2), ("qk_sum", 3), ("v_sum", 3), ("y_sum", 3), ("sq_sum", 3), ("squares", 1), ("sample_moments", 3),
+    ("mu_sq", 3), ("var", 3), ("rstd", 3), ("exp_scores", 2), ("att", 3), ("att_flipped", 3), ("mem1", 3),
+    ("relu_mem1", 3), ("f", 2), ("normed", 2), ("mem1_and_bias", 4), ("result", 3), ("minus_max", 3), ("exp_sum", 3),
+    ("exp_rsum", 3), ("f_stats", 3), ("f_moments", 3), ("var2", 3), ("rstd2", 3),
 )
 PSUM_RINGS = (("bank", 3), ("scores", 1), ("att_flipped", 1), ("o", 1), ("f", 1), ("flipped", 1))
 
@@ -115,7 +114,7 @@ def tile_rsaffdecoder_b_kernel(
         nc.sync.dma_start(mlp_w_sb[:], mlp_w.rearrange("(hb p) r -> p hb r", p=P))
 
         spread_mean = held.tile([P, P], F32)
-        nc.vector.memset(spread_mean[:], 1.0 / P)
+        nc.vector.memset(spread_mean[:], 1.0 / (P * PROJ))
         minus_half = held.tile([P, PIECE_SAMPLES], F32)
         nc.vector.memset(minus_half[:], -0.5)
         scratch = held.tile([P, 1], F32)
@@ -195,11 +194,15 @@ def tile_rsaffdecoder_b_kernel(
         y_of_piece = {}
         z_of_piece = {}
         mu_rstd_of_piece = {}
+        sums_of_piece = {}
 
         def project(g):
             piece = slice(g * PIECE, (g + 1) * PIECE)
             y = ring["y"].tile([P, PIECE_SAMPLES, PROJ], F32)
             y_of_piece[g] = y
+            qk_sum = ring["qk_sum"].tile([P, PIECE_SAMPLES, 2 * HEADS], F32)
+            v_sum = ring["v_sum"].tile([P, PIECE_SAMPLES], F32)
+            sums_of_piece[g] = (qk_sum, v_sum)
             for t in range(HEADS):
                 for c in range(2):
                     qk_ps = psum_ring["bank"].tile([P, PIECE_SAMPLES, SLOTS], F32, tag="bank")
@@ -208,8 +211,10 @@ def tile_rsaffdecoder_b_kernel(
                                          w_qk_sb[:, hb, (2 * t + c) * P:(2 * t + c + 1) * P],
                                          mem0_bf16[:, hb, piece], start=(hb == 0), stop=(hb == HID_BLOCKS - 1))
                     r = 3 * t + c
-                    nc.scalar.activation(y[:, :, r * P:(r + 1) * P], qk_ps[:], FUNC.Identity,
-                                         bias=cols[:, COL_QKV_B + r:COL_QKV_B + r + 1])
+                    for s in range(PIECE_SAMPLES):
+                        nc.scalar.activation(y[:, s, r * P:(r + 1) * P], qk_ps[:, s, :], FUNC.Identity,
+                                             bias=cols[:, COL_QKV_B + r:COL_QKV_B + r + 1],
+                                             accum_out=qk_sum[:, s, 2 * t + c:2 * t + c + 1])
             v_bias = qkv_b_sb[:].rearrange("p (t c u) -> p t c u", c=3, u=P)[:, :, 2, :]
             for s in range(PIECE_SAMPLES):
                 b = g * PIECE_SAMPLES + s
@@ -217,29 +222,29 @@ def tile_rsaffdecoder_b_kernel(
                 for hb in range(HID_BLOCKS):
                     nc.tensor.matmul(v_ps[:].rearrange("p t u -> p (t u)"), mem0_bf16[:, hb, b * SLOTS:(b + 1) * SLOTS],
                                      w_v_sb[:, hb, :], start=(hb == 0), stop=(hb == HID_BLOCKS - 1))
-                nc.vector.tensor_tensor(y[:, s, :].rearrange("p (t c u) -> p t c u", c=3, u=P)[:, :, 2, :],
-                                        v_ps[:], v_bias, ALU.add)
+                nc.vector.scalar_tensor_tensor(y[:, s, :].rearrange("p (t c u) -> p t c u", c=3, u=P)[:, :, 2, :],
+                                               v_ps[:], 1.0, v_bias, ALU.mult, ALU.add,
+                                               accum_out=v_sum[:, s:s + 1])
 
         def measure(g):
             y = y_of_piece[g]
-            chunk_stats = ring["chunk_stats"].tile([P, PIECE_SAMPLES, PROJ // STAT_CHUNK, 6], F32)
-            moments = ring["moments"].tile([P, PIECE_SAMPLES, 2], F32)
+            qk_sum, v_sum = sums_of_piece[g]
+            y_sum = ring["y_sum"].tile([P, PIECE_SAMPLES], F32)
+            nc.vector.tensor_reduce(y_sum[:], qk_sum[:], AXIS_X, ALU.add)
+            nc.vector.tensor_tensor(y_sum[:], y_sum[:], v_sum[:], ALU.add)
+            sq_sum = ring["sq_sum"].tile([P, PIECE_SAMPLES], F32)
             for s in range(PIECE_SAMPLES):
-                for k in range(PROJ // STAT_CHUNK):
-                    nc.vector.bn_stats(chunk_stats[:, s, k, :], y[:, s, k * STAT_CHUNK:(k + 1) * STAT_CHUNK])
-                nc.vector.bn_aggr(moments[:, s, :], chunk_stats[:, s, :, :].rearrange("p k f -> p (k f)"))
-            mean_sq = ring["mean_sq"].tile([P, PIECE_SAMPLES], F32)
-            nc.vector.tensor_tensor(mean_sq[:], moments[:, :, 0], moments[:, :, 0], ALU.mult)
-            nc.vector.tensor_tensor(moments[:, :, 1], moments[:, :, 1], mean_sq[:], ALU.add)
-            sample_ps = psum_ring["scores"].tile([P, PIECE_SAMPLES, 2], F32, tag="scores")
-            nc.tensor.matmul(sample_ps[:].rearrange("p s m -> p (s m)"), spread_mean[:],
-                             moments[:].rearrange("p s m -> p (s m)"), start=True, stop=True)
-            sample_moments = ring["sample_moments"].tile([P, PIECE_SAMPLES, 2], F32)
+                squares = ring["squares"].tile([P, PROJ], BF16)
+                nc.scalar.activation(squares[:], y[:, s, :], FUNC.Square, accum_out=sq_sum[:, s:s + 1])
+            sample_ps = psum_ring["scores"].tile([P, 2, PIECE_SAMPLES], F32, tag="scores")
+            nc.tensor.matmul(sample_ps[:, 0, :], spread_mean[:], y_sum[:], start=True, stop=True)
+            nc.tensor.matmul(sample_ps[:, 1, :], spread_mean[:], sq_sum[:], start=True, stop=True)
+            sample_moments = ring["sample_moments"].tile([P, 2, PIECE_SAMPLES], F32)
             nc.vector.tensor_copy(sample_moments[:], sample_ps[:])
             mu_sq = ring["mu_sq"].tile([P, PIECE_SAMPLES], F32)
-            nc.vector.tensor_tensor(mu_sq[:], sample_moments[:, :, 0], sample_moments[:, :, 0], ALU.mult)
+            nc.vector.tensor_tensor(mu_sq[:], sample_moments[:, 0, :], sample_moments[:, 0, :], ALU.mult)
             var = ring["var"].tile([P, PIECE_SAMPLES], F32)
-            nc.vector.tensor_tensor(var[:], sample_moments[:, :, 1], mu_sq[:], ALU.subtract)
+            nc.vector.tensor_tensor(var[:], sample_moments[:, 1, :], mu_sq[:], ALU.subtract)
             nc.vector.tensor_scalar(var[:], var[:], 0.0, EPS, ALU.max, ALU.add)
             rstd = ring["rstd"].tile([P, PIECE_SAMPLES], F32)
             nc.gpsimd.tensor_tensor(rstd[:], var[:], minus_half[:], ALU.pow)
@@ -252,7 +257,7 @@ def tile_rsaffdecoder_b_kernel(
             z_of_piece[g] = z
             for s in range(PIECE_SAMPLES):
                 centred = ring["centred"].tile([P, PROJ], F32)
-                nc.vector.scalar_tensor_tensor(centred[:], y[:, s, :], sample_moments[:, s, 0:1], ln_gain[:],
+                nc.vector.scalar_tensor_tensor(centred[:], y[:, s, :], sample_moments[:, 0, s:s + 1], ln_gain[:],
                                                ALU.subtract, ALU.mult)
                 nc.vector.scalar_tensor_tensor(z[:, s, :], centred[:], rstd[:, s:s + 1], ln_bias[:],
                                                ALU.mult, ALU.add)
@@ -289,6 +294,11 @@ def tile_rsaffdecoder_b_kernel(
             mem1 = ring["mem1"].tile([P, HID_BLOCKS, SLOTS], F32)
             nc.vector.tensor_tensor(mem1[:], o_ps[:], mem[:, :, sample], ALU.add)
 
+            mem1_and_bias = ring["mem1_and_bias"].tile([P, HID_BLOCKS, SLOTS], F32)
+            for rb in range(HID_BLOCKS):
+                nc.scalar.activation(mem1_and_bias[:, rb, :], mem1[:, rb, :], FUNC.Identity,
+                                     bias=cols[:, COL_MLP_LN_B + rb:COL_MLP_LN_B + rb + 1])
+
             relu_mem1 = ring["relu_mem1"].tile([P, HID_BLOCKS, SLOTS], BF16)
             nc.scalar.activation(relu_mem1[:], mem1[:], FUNC.Relu)
             f_ps = psum_ring["f"].tile([P, HID], F32, tag="f")
@@ -305,21 +315,17 @@ def tile_rsaffdecoder_b_kernel(
             nc.vector.tensor_scalar_add(var2[:], f_moments[:, 1:2], EPS)
             rstd2 = ring["rstd2"].tile([P, 1], F32)
             nc.gpsimd.tensor_tensor(rstd2[:], var2[:], minus_half[:, 0:1], ALU.pow)
-            shift2 = ring["shift2"].tile([P, 1], F32)
-            nc.vector.scalar_tensor_tensor(shift2[:], f_moments[:, 0:1], -1.0, rstd2[:], ALU.mult, ALU.mult)
             normed = ring["normed"].tile([P, HID], F32)
-            nc.scalar.activation(normed[:], f[:], FUNC.Identity, bias=shift2[:], scale=rstd2[:])
+            nc.vector.tensor_scalar(normed[:], f[:], f_moments[:, 0:1], rstd2[:], ALU.subtract, ALU.mult)
 
             normed_flipped = psum_ring["flipped"].tile([P, HID_BLOCKS, SLOTS], F32, tag="flipped")
             for rb in range(HID_BLOCKS):
                 nc.tensor.transpose(normed_flipped[:, rb, :], normed[:, rb * P:(rb + 1) * P], identity_f32[:])
-            scaled = ring["scaled"].tile([P, HID_BLOCKS, SLOTS], F32)
-            for rb in range(HID_BLOCKS):
-                nc.scalar.activation(scaled[:, rb, :], normed_flipped[:, rb, :], FUNC.Identity,
-                                     bias=cols[:, COL_MLP_LN_B + rb:COL_MLP_LN_B + rb + 1],
-                                     scale=cols[:, COL_MLP_LN_W + rb:COL_MLP_LN_W + rb + 1])
             result = ring["result"].tile([P, HID_BLOCKS, SLOTS], F32)
-            nc.gpsimd.tensor_tensor(result[:], scaled[:], mem1[:], ALU.add)
+            for rb in range(HID_BLOCKS):
+                nc.vector.scalar_tensor_tensor(result[:, rb, :], normed_flipped[:, rb, :],
+                                               cols[:, COL_MLP_LN_W + rb:COL_MLP_LN_W + rb + 1], mem1_and_bias[:, rb, :],
+                                               ALU.mult, ALU.add)
             nc.sync.dma_start(out_blocks[:, :, sample], result[:])
 
         for g in range(AHEAD):

@@ -40,8 +40,8 @@ N_COLS = 28
 
 SBUF_RINGS = (
     ("y", 3), ("z", 3), ("centred", 2), ("qk_sum", 3), ("v_sum", 3), ("y_sum", 3), ("sq_sum", 3), ("squares", 1), ("sample_moments", 3),
-    ("mu_sq", 3), ("var", 3), ("rstd", 3), ("exp_scores", 2), ("att", 3), ("att_flipped", 3), ("mem1", 3),
-    ("relu_mem1", 3), ("f", 2), ("normed", 2), ("mem1_and_bias", 4), ("result", 3), ("minus_max", 3), ("exp_sum", 3),
+    ("mu_sq", 3), ("var", 3), ("rstd", 3), ("exp_scores", 2), ("att", 3), ("att_flipped", 3), ("mem1_biased", 4),
+    ("relu_mem1", 3), ("f", 2), ("normed", 2), ("result", 3), ("minus_max", 3), ("exp_sum", 3),
     ("exp_rsum", 3), ("f_stats", 3), ("f_moments", 3), ("var2", 3), ("rstd2", 3),
 )
 PSUM_RINGS = (("bank", 3), ("scores", 1), ("att_flipped", 1), ("o", 1), ("f", 1), ("flipped", 1))
@@ -95,14 +95,14 @@ def tile_rsaffdecoder_b_kernel(
             by_head = qkv_w[hb * P:(hb + 1) * P, :].rearrange("p (t r) -> p t r", t=HEADS)
             nc.sync.dma_start(w_qk_sb[:, hb, :].rearrange("p (t r) -> p t r", t=HEADS),
                               by_head[:, :, 0:2 * P])
-            nc.gpsimd.dma_start(w_v_sb[:, hb, :].rearrange("p (t r) -> p t r", t=HEADS),
+            nc.sync.dma_start(w_v_sb[:, hb, :].rearrange("p (t r) -> p t r", t=HEADS),
                                 by_head[:, :, 2 * P:3 * P])
         nc.sync.dma_start(emb_sb[:, :, LOOKUP:N_TOK], emb_blocks[:, :, LOOKUP:N_TOK])
 
         qkv_b_sb = held.tile([P, PROJ], F32)
-        nc.gpsimd.dma_start(qkv_b_sb[:], qkv_b.rearrange("r o -> (r o)").partition_broadcast(P))
+        nc.sync.dma_start(qkv_b_sb[:], qkv_b.rearrange("r o -> (r o)").partition_broadcast(P))
         mlp_b_sb = held.tile([P, HID], F32)
-        nc.gpsimd.dma_start(mlp_b_sb[:], mlp_b.rearrange("r o -> (r o)").partition_broadcast(P))
+        nc.sync.dma_start(mlp_b_sb[:], mlp_b.rearrange("r o -> (r o)").partition_broadcast(P))
 
         ln_gain = held.tile([P, PROJ], F32)
         nc.sync.dma_start(ln_gain[:].rearrange("p (r n) -> p r n", n=SLOTS),
@@ -124,6 +124,7 @@ def tile_rsaffdecoder_b_kernel(
         mem = held.tile([P, HID_BLOCKS, N_TOK], F32)
         mem0_bf16 = held.tile([P, HID_BLOCKS, N_TOK], BF16)
         cols = held.tile([P, N_COLS], F32)
+        minus_last_bias = held.tile([P, HID_BLOCKS], F32)
         query_term = held.tile([P, HID_BLOCKS, N_SAMPLES], F32)
         w_dist_scaled = held.tile([P, HID_BLOCKS, N_SAMPLES], F32)
         dist_min = held.tile([P, N_SAMPLES], F32)
@@ -142,7 +143,8 @@ def tile_rsaffdecoder_b_kernel(
         def round_mem0(u):
             lookup = slice(u * LOOKUP, (u + 1) * LOOKUP)
             for hb in range(HID_BLOCKS):
-                nc.scalar.activation(mem0_bf16[:, hb, lookup], mem[:, hb, lookup], FUNC.Copy)
+                nc.scalar.activation(mem0_bf16[:, hb, lookup], mem[:, hb, lookup], FUNC.Identity,
+                                     bias=minus_last_bias[:, hb:hb + 1])
 
         with tc.psum_pool(name="setup_psum", bufs=1) as setup_psum:
             cols_ps = setup_psum.tile([P, P], F32)
@@ -153,9 +155,12 @@ def tile_rsaffdecoder_b_kernel(
                 for kb in range(EMB_BLOCKS):
                     nc.tensor.matmul(query_ps[:, hb, :], w_qry_sb[:, kb, hb * P:(hb + 1) * P], query_sb[:, kb, :],
                                      start=(kb == 0), stop=(kb == EMB_BLOCKS - 1))
-            pre_b_cols = cols[:, COL_PRE_B:COL_PRE_B + HID_BLOCKS].unsqueeze(2)
+            last_bias = cols[:, COL_MLP_LN_B:COL_MLP_LN_B + HID_BLOCKS]
+            nc.vector.tensor_scalar_mul(minus_last_bias[:], last_bias, -1.0)
+            both_biases = held.tile([P, HID_BLOCKS], F32)
+            nc.vector.tensor_tensor(both_biases[:], cols[:, COL_PRE_B:COL_PRE_B + HID_BLOCKS], last_bias, ALU.add)
             nc.vector.tensor_tensor(query_term[:], query_ps[:],
-                                    pre_b_cols.to_broadcast([P, HID_BLOCKS, N_SAMPLES]), ALU.add)
+                                    both_biases[:].unsqueeze(2).to_broadcast([P, HID_BLOCKS, N_SAMPLES]), ALU.add)
 
             for u in range(LOOKUPS):
                 group = slice(u * LOOKUP_SAMPLES, (u + 1) * LOOKUP_SAMPLES)
@@ -291,16 +296,12 @@ def tile_rsaffdecoder_b_kernel(
             for t in range(HEADS):
                 nc.tensor.matmul(o_ps[:, t, :], q_k_v[:, t, 2, :], att_flipped[:, t, :], start=True, stop=True)
 
-            mem1 = ring["mem1"].tile([P, HID_BLOCKS, SLOTS], F32)
-            nc.vector.tensor_tensor(mem1[:], o_ps[:], mem[:, :, sample], ALU.add)
-
-            mem1_and_bias = ring["mem1_and_bias"].tile([P, HID_BLOCKS, SLOTS], F32)
-            for rb in range(HID_BLOCKS):
-                nc.scalar.activation(mem1_and_bias[:, rb, :], mem1[:, rb, :], FUNC.Identity,
-                                     bias=cols[:, COL_MLP_LN_B + rb:COL_MLP_LN_B + rb + 1])
+            mem1_biased = ring["mem1_biased"].tile([P, HID_BLOCKS, SLOTS], F32)
+            nc.vector.tensor_tensor(mem1_biased[:], o_ps[:], mem[:, :, sample], ALU.add)
 
             relu_mem1 = ring["relu_mem1"].tile([P, HID_BLOCKS, SLOTS], BF16)
-            nc.scalar.activation(relu_mem1[:], mem1[:], FUNC.Relu)
+            for hb in range(HID_BLOCKS):
+                nc.scalar.activation(relu_mem1[:, hb, :], mem1_biased[:, hb, :], FUNC.Relu, bias=minus_last_bias[:, hb:hb + 1])
             f_ps = psum_ring["f"].tile([P, HID], F32, tag="f")
             for hb in range(HID_BLOCKS):
                 nc.tensor.matmul(f_ps[:], relu_mem1[:, hb, :], mlp_w_sb[:, hb, :],
@@ -324,7 +325,7 @@ def tile_rsaffdecoder_b_kernel(
             result = ring["result"].tile([P, HID_BLOCKS, SLOTS], F32)
             for rb in range(HID_BLOCKS):
                 nc.vector.scalar_tensor_tensor(result[:, rb, :], normed_flipped[:, rb, :],
-                                               cols[:, COL_MLP_LN_W + rb:COL_MLP_LN_W + rb + 1], mem1_and_bias[:, rb, :],
+                                               cols[:, COL_MLP_LN_W + rb:COL_MLP_LN_W + rb + 1], mem1_biased[:, rb, :],
                                                ALU.mult, ALU.add)
             nc.sync.dma_start(out_blocks[:, :, sample], result[:])
 

@@ -64,6 +64,12 @@ def tile_rsaffdecoder_b_kernel(
         identity_bf16 = held.tile([P, P], BF16)
         nc.vector.tensor_copy(identity_bf16[:], identity_f32[:])
 
+        offsets = held.tile([P, N_TOK // 16], U16, name="offsets")
+        nc.sync.dma_start(offsets[:], offs)
+        table_sb = held.tile([P, TABLE_COLS], BF16)
+        nc.sync.dma_start(table_sb[:], table)
+        w_lab_sb = held.tile([P, HID], BF16)
+        nc.sync.dma_start(w_lab_sb[:], w_lab)
         edist = held.tile([P, N_TOK], F32)
         nc.sync.dma_start(edist[:], distances.rearrange("o n -> (o n)").partition_broadcast(P))
         w_qry_sb = held.tile([P, EMB_BLOCKS, HID], BF16)
@@ -73,12 +79,6 @@ def tile_rsaffdecoder_b_kernel(
         emb_sb = held.tile([P, EMB_BLOCKS, N_TOK], BF16)
         emb_blocks = emb.rearrange("(k p) n -> p k n", p=P)
         nc.sync.dma_start(emb_sb[:, :, 0:LOOKUP], emb_blocks[:, :, 0:LOOKUP])
-        offsets = held.tile([P, N_TOK // 16], U16, name="offsets")
-        nc.sync.dma_start(offsets[:], offs)
-        w_lab_sb = held.tile([P, HID], BF16)
-        nc.sync.dma_start(w_lab_sb[:], w_lab)
-        table_sb = held.tile([P, TABLE_COLS], BF16)
-        nc.sync.dma_start(table_sb[:], table)
 
         rows = held.tile([P, P], F32)
         nc.vector.memset(rows[:], 0.0)
@@ -97,12 +97,9 @@ def tile_rsaffdecoder_b_kernel(
                               by_head[:, :, 0:2 * P])
             nc.sync.dma_start(w_v_sb[:, hb, :].rearrange("p (t r) -> p t r", t=HEADS),
                                 by_head[:, :, 2 * P:3 * P])
-        nc.sync.dma_start(emb_sb[:, :, LOOKUP:N_TOK], emb_blocks[:, :, LOOKUP:N_TOK])
 
         qkv_b_sb = held.tile([P, PROJ], F32)
         nc.sync.dma_start(qkv_b_sb[:], qkv_b.rearrange("r o -> (r o)").partition_broadcast(P))
-        mlp_b_sb = held.tile([P, HID], F32)
-        nc.sync.dma_start(mlp_b_sb[:], mlp_b.rearrange("r o -> (r o)").partition_broadcast(P))
 
         ln_gain = held.tile([P, PROJ], F32)
         nc.sync.dma_start(ln_gain[:].rearrange("p (r n) -> p r n", n=SLOTS),
@@ -110,6 +107,9 @@ def tile_rsaffdecoder_b_kernel(
         ln_bias = held.tile([P, PROJ], F32)
         nc.sync.dma_start(ln_bias[:].rearrange("p (r n) -> p r n", n=SLOTS),
                           qkv_ln_b.rearrange("(r p) n -> p r n", p=P))
+        nc.sync.dma_start(emb_sb[:, :, LOOKUP:N_TOK], emb_blocks[:, :, LOOKUP:N_TOK])
+        mlp_b_sb = held.tile([P, HID], F32)
+        nc.sync.dma_start(mlp_b_sb[:], mlp_b.rearrange("r o -> (r o)").partition_broadcast(P))
         mlp_w_sb = held.tile([P, HID_BLOCKS, HID], BF16)
         nc.sync.dma_start(mlp_w_sb[:], mlp_w.rearrange("(hb p) r -> p hb r", p=P))
 
@@ -209,15 +209,16 @@ def tile_rsaffdecoder_b_kernel(
             v_sum = ring["v_sum"].tile([P, PIECE_SAMPLES], F32)
             sums_of_piece[g] = (qk_sum, v_sum)
             for t in range(HEADS):
+                qk_ps = psum_ring["bank"].tile([P, 2, PIECE_SAMPLES, SLOTS], F32, tag="bank")
                 for c in range(2):
-                    qk_ps = psum_ring["bank"].tile([P, PIECE_SAMPLES, SLOTS], F32, tag="bank")
                     for hb in range(HID_BLOCKS):
-                        nc.tensor.matmul(qk_ps[:].rearrange("p s n -> p (s n)"),
+                        nc.tensor.matmul(qk_ps[:, c, :, :].rearrange("p s n -> p (s n)"),
                                          w_qk_sb[:, hb, (2 * t + c) * P:(2 * t + c + 1) * P],
                                          mem0_bf16[:, hb, piece], start=(hb == 0), stop=(hb == HID_BLOCKS - 1))
+                for c in range(2):
                     r = 3 * t + c
                     for s in range(PIECE_SAMPLES):
-                        nc.scalar.activation(y[:, s, r * P:(r + 1) * P], qk_ps[:, s, :], FUNC.Identity,
+                        nc.scalar.activation(y[:, s, r * P:(r + 1) * P], qk_ps[:, c, s, :], FUNC.Identity,
                                              bias=cols[:, COL_QKV_B + r:COL_QKV_B + r + 1],
                                              accum_out=qk_sum[:, s, 2 * t + c:2 * t + c + 1])
             v_bias = qkv_b_sb[:].rearrange("p (t c u) -> p t c u", c=3, u=P)[:, :, 2, :]
@@ -329,10 +330,7 @@ def tile_rsaffdecoder_b_kernel(
                                                ALU.mult, ALU.add)
             nc.sync.dma_start(out_blocks[:, :, sample], result[:])
 
-        for g in range(AHEAD):
-            project(g)
-        add_emb(1, psum_ring["bank"], 3)
-        round_mem0(1)
+        project(0)
 
         for param in (ln_gain, ln_bias):
             by_kind = param[:].rearrange("p (t c n) -> p t c n", c=3, n=SLOTS)
@@ -345,12 +343,15 @@ def tile_rsaffdecoder_b_kernel(
         measure(0)
         for g in range(PIECES):
             normalise(g)
+            if g == 0:
+                project(1)
             if g + 1 < PIECES:
                 measure(g + 1)
             for s in range(PIECE_SAMPLES):
                 attend_and_mlp(g, s)
-            if g + AHEAD < PIECES:
-                project(g + AHEAD)
-            if g % 2 == 0 and g // 2 + 2 < LOOKUPS:
-                add_emb(g // 2 + 2, psum_ring["bank"], 3)
-                round_mem0(g // 2 + 2)
+            ahead = g + AHEAD
+            if ahead < PIECES:
+                if ahead % 2 == 0:
+                    add_emb(ahead // 2, psum_ring["bank"], 3)
+                    round_mem0(ahead // 2)
+                project(ahead)

@@ -33,10 +33,11 @@ Q_SCALE = 128.0 ** -0.5
 
 COL_W_DIST = 0
 COL_PRE_B = 4
-COL_MLP_LN_W = 8
-COL_MLP_LN_B = 12
-COL_QKV_B = 16
-N_COLS = 28
+COL_MLP_LN_B = 8
+N_COLS = 12
+LATE_COL_MLP_LN_W = 0
+LATE_COL_QKV_B = 4
+N_LATE_COLS = 16
 
 SBUF_RINGS = (
     ("y", 3), ("z", 3), ("centred", 2), ("qk_sum", 3), ("v_sum", 3), ("y_sum", 3), ("sq_sum", 3), ("squares", 1), ("sample_moments", 3),
@@ -64,54 +65,55 @@ def tile_rsaffdecoder_b_kernel(
         identity_bf16 = held.tile([P, P], BF16)
         nc.vector.tensor_copy(identity_bf16[:], identity_f32[:])
 
-        offsets = held.tile([P, N_TOK // 16], U16, name="offsets")
-        nc.sync.dma_start(offsets[:], offs)
+        def as_rows(vector):
+            return vector.rearrange("(k p) o -> k (p o)", p=P)
+
+        rows = held.tile([P, P], F32)
+        nc.vector.memset(rows[:], 0.0)
+        late_rows = held.tile([P, P], F32)
+        nc.vector.memset(late_rows[:], 0.0)
+
+        edist = held.tile([P, N_TOK], F32)
+        distance_row = distances.rearrange("o n -> (o n)")
+        nc.scalar.dma_start(edist[:, 0:LOOKUP], distance_row[0:LOOKUP].partition_broadcast(P))
+        nc.scalar.dma_start(rows[COL_W_DIST:COL_W_DIST + HID_BLOCKS, :], as_rows(w_dist))
+        query_sb = held.tile([P, EMB_BLOCKS, N_SAMPLES], BF16)
+        nc.scalar.dma_start(query_sb[:], query.rearrange("(k p) b -> p k b", p=P))
+
         table_sb = held.tile([P, TABLE_COLS], BF16)
         nc.sync.dma_start(table_sb[:], table)
+        offsets = held.tile([P, N_TOK // 16], U16, name="offsets")
+        nc.sync.dma_start(offsets[:], offs)
         w_lab_sb = held.tile([P, HID], BF16)
         nc.sync.dma_start(w_lab_sb[:], w_lab)
-        edist = held.tile([P, N_TOK], F32)
-        nc.sync.dma_start(edist[:], distances.rearrange("o n -> (o n)").partition_broadcast(P))
-        w_qry_sb = held.tile([P, EMB_BLOCKS, HID], BF16)
-        nc.sync.dma_start(w_qry_sb[:], w_qry.rearrange("(k p) h -> p k h", p=P))
         w_emb_sb = held.tile([P, EMB_BLOCKS, HID], BF16)
         nc.sync.dma_start(w_emb_sb[:], w_emb.rearrange("(k p) h -> p k h", p=P))
         emb_sb = held.tile([P, EMB_BLOCKS, N_TOK], BF16)
         emb_blocks = emb.rearrange("(k p) n -> p k n", p=P)
         nc.sync.dma_start(emb_sb[:, :, 0:LOOKUP], emb_blocks[:, :, 0:LOOKUP])
-
-        rows = held.tile([P, P], F32)
-        nc.vector.memset(rows[:], 0.0)
-        for vector, col in ((w_dist, COL_W_DIST), (pre_b, COL_PRE_B), (mlp_ln_w, COL_MLP_LN_W),
-                            (mlp_ln_b, COL_MLP_LN_B), (qkv_b, COL_QKV_B)):
-            as_rows = vector.rearrange("(k p) o -> k (p o)", p=P)
-            nc.scalar.dma_start(rows[col:col + as_rows.shape[0], :], as_rows)
-        query_sb = held.tile([P, EMB_BLOCKS, N_SAMPLES], BF16)
-        nc.scalar.dma_start(query_sb[:], query.rearrange("(k p) b -> p k b", p=P))
-
-        w_qk_sb = held.tile([P, HID_BLOCKS, 2 * HEADS * P], BF16)
-        w_v_sb = held.tile([P, HID_BLOCKS, HID], BF16)
-        for hb in range(HID_BLOCKS):
-            by_head = qkv_w[hb * P:(hb + 1) * P, :].rearrange("p (t r) -> p t r", t=HEADS)
-            nc.sync.dma_start(w_qk_sb[:, hb, :].rearrange("p (t r) -> p t r", t=HEADS),
-                              by_head[:, :, 0:2 * P])
-            nc.sync.dma_start(w_v_sb[:, hb, :].rearrange("p (t r) -> p t r", t=HEADS),
-                                by_head[:, :, 2 * P:3 * P])
-
+        nc.sync.dma_start(rows[COL_PRE_B:COL_PRE_B + HID_BLOCKS, :], as_rows(pre_b))
+        nc.sync.dma_start(rows[COL_MLP_LN_B:COL_MLP_LN_B + HID_BLOCKS, :], as_rows(mlp_ln_b))
+        w_qry_sb = held.tile([P, EMB_BLOCKS, HID], BF16)
+        nc.sync.dma_start(w_qry_sb[:], w_qry.rearrange("(k p) h -> p k h", p=P))
+        nc.sync.dma_start(edist[:, LOOKUP:N_TOK], distance_row[LOOKUP:N_TOK].partition_broadcast(P))
+        qkv_w_sb = held.tile([P, HID_BLOCKS, PROJ], BF16)
+        nc.sync.dma_start(qkv_w_sb[:], qkv_w.rearrange("(hb p) r -> p hb r", p=P))
+        nc.sync.dma_start(late_rows[LATE_COL_QKV_B:LATE_COL_QKV_B + PROJ // P, :], as_rows(qkv_b))
+        nc.sync.dma_start(late_rows[LATE_COL_MLP_LN_W:LATE_COL_MLP_LN_W + HID_BLOCKS, :], as_rows(mlp_ln_w))
         qkv_b_sb = held.tile([P, PROJ], F32)
         nc.sync.dma_start(qkv_b_sb[:], qkv_b.rearrange("r o -> (r o)").partition_broadcast(P))
 
         ln_gain = held.tile([P, PROJ], F32)
-        nc.sync.dma_start(ln_gain[:].rearrange("p (r n) -> p r n", n=SLOTS),
-                          qkv_ln_w.rearrange("(r p) n -> p r n", p=P))
+        nc.gpsimd.dma_start(ln_gain[:].rearrange("p (r n) -> p r n", n=SLOTS),
+                            qkv_ln_w.rearrange("(r p) n -> p r n", p=P))
         ln_bias = held.tile([P, PROJ], F32)
-        nc.sync.dma_start(ln_bias[:].rearrange("p (r n) -> p r n", n=SLOTS),
-                          qkv_ln_b.rearrange("(r p) n -> p r n", p=P))
-        nc.sync.dma_start(emb_sb[:, :, LOOKUP:N_TOK], emb_blocks[:, :, LOOKUP:N_TOK])
+        nc.gpsimd.dma_start(ln_bias[:].rearrange("p (r n) -> p r n", n=SLOTS),
+                            qkv_ln_b.rearrange("(r p) n -> p r n", p=P))
+        nc.gpsimd.dma_start(emb_sb[:, :, LOOKUP:N_TOK], emb_blocks[:, :, LOOKUP:N_TOK])
         mlp_b_sb = held.tile([P, HID], F32)
-        nc.sync.dma_start(mlp_b_sb[:], mlp_b.rearrange("r o -> (r o)").partition_broadcast(P))
+        nc.gpsimd.dma_start(mlp_b_sb[:], mlp_b.rearrange("r o -> (r o)").partition_broadcast(P))
         mlp_w_sb = held.tile([P, HID_BLOCKS, HID], BF16)
-        nc.sync.dma_start(mlp_w_sb[:], mlp_w.rearrange("(hb p) r -> p hb r", p=P))
+        nc.gpsimd.dma_start(mlp_w_sb[:], mlp_w.rearrange("(hb p) r -> p hb r", p=P))
 
         spread_mean = held.tile([P, P], F32)
         nc.vector.memset(spread_mean[:], 1.0 / (P * PROJ))
@@ -124,21 +126,53 @@ def tile_rsaffdecoder_b_kernel(
         mem = held.tile([P, HID_BLOCKS, N_TOK], F32)
         mem0_bf16 = held.tile([P, HID_BLOCKS, N_TOK], BF16)
         cols = held.tile([P, N_COLS], F32)
+        late_cols = held.tile([P, N_LATE_COLS], F32)
         minus_last_bias = held.tile([P, HID_BLOCKS], F32)
         query_term = held.tile([P, HID_BLOCKS, N_SAMPLES], F32)
-        w_dist_scaled = held.tile([P, HID_BLOCKS, N_SAMPLES], F32)
         dist_min = held.tile([P, N_SAMPLES], F32)
         edist_sum = held.tile([P, N_SAMPLES], F32)
         edist_rsum = held.tile([P, N_SAMPLES], F32)
 
-        def add_emb(u, banks, bufs):
+        def soften(u):
+            group = slice(u * LOOKUP_SAMPLES, (u + 1) * LOOKUP_SAMPLES)
+            samples = [(b, slice(b * SLOTS, (b + 1) * SLOTS)) for b in range(group.start, group.stop)]
+            nc.vector.tensor_reduce(dist_min[:, group],
+                                    edist[:, u * LOOKUP:(u + 1) * LOOKUP].rearrange("p (b n) -> p b n", n=SLOTS),
+                                    AXIS_X, ALU.min)
+            for b, sample in samples:
+                nc.scalar.activation(edist[:, sample], edist[:, sample], FUNC.Exp, bias=dist_min[:, b:b + 1],
+                                     scale=-1.0, accum_out=edist_sum[:, b:b + 1])
+            nc.vector.reciprocal(edist_rsum[:, group], edist_sum[:, group])
+            for b, sample in samples:
+                nc.scalar.activation(edist[:, sample], edist[:, sample], FUNC.Copy, scale=edist_rsum[:, b:b + 1])
+
+        def emb_product(u, hb, banks):
+            emb_ps = banks.tile([P, LOOKUP], F32, tag="bank")
+            for kb in range(EMB_BLOCKS):
+                nc.tensor.matmul(emb_ps[:], w_emb_sb[:, kb, hb * P:(hb + 1) * P],
+                                 emb_sb[:, kb, u * LOOKUP:(u + 1) * LOOKUP],
+                                 start=(kb == 0), stop=(kb == EMB_BLOCKS - 1))
+            return emb_ps
+
+        def label_product(u, hb, banks):
+            label_ps = banks.tile([P, LOOKUP], F32, tag="bank")
+            nc.tensor.matmul(label_ps[:], w_lab_sb[:, hb * P:(hb + 1) * P],
+                             table_sb[:].indirect(offsets[:, u * (LOOKUP // 16):(u + 1) * (LOOKUP // 16)]),
+                             start=True, stop=True)
+            return label_ps
+
+        def start_mem(u, hb, product_ps):
             lookup = slice(u * LOOKUP, (u + 1) * LOOKUP)
-            for hb in range(HID_BLOCKS):
-                emb_ps = banks.tile([P, LOOKUP], F32, tag="bank", bufs=bufs)
-                for kb in range(EMB_BLOCKS):
-                    nc.tensor.matmul(emb_ps[:], w_emb_sb[:, kb, hb * P:(hb + 1) * P], emb_sb[:, kb, lookup],
-                                     start=(kb == 0), stop=(kb == EMB_BLOCKS - 1))
-                nc.vector.tensor_tensor(mem[:, hb, lookup], emb_ps[:], mem[:, hb, lookup], ALU.add)
+            nc.vector.scalar_tensor_tensor(mem[:, hb, lookup], edist[:, lookup],
+                                           cols[:, COL_W_DIST + hb:COL_W_DIST + hb + 1], product_ps[:],
+                                           ALU.mult, ALU.add)
+
+        def finish_mem(u, hb, product_ps):
+            for k in range(LOOKUP_SAMPLES):
+                b = u * LOOKUP_SAMPLES + k
+                sample = slice(b * SLOTS, (b + 1) * SLOTS)
+                nc.vector.scalar_tensor_tensor(mem[:, hb, sample], product_ps[:, k * SLOTS:(k + 1) * SLOTS],
+                                               query_term[:, hb, b:b + 1], mem[:, hb, sample], ALU.add, ALU.add)
 
         def round_mem0(u):
             lookup = slice(u * LOOKUP, (u + 1) * LOOKUP)
@@ -146,11 +180,59 @@ def tile_rsaffdecoder_b_kernel(
                 nc.scalar.activation(mem0_bf16[:, hb, lookup], mem[:, hb, lookup], FUNC.Identity,
                                      bias=minus_last_bias[:, hb:hb + 1])
 
-        with tc.psum_pool(name="setup_psum", bufs=1) as setup_psum:
-            cols_ps = setup_psum.tile([P, P], F32)
+        out_blocks = out.rearrange("(rb p) n -> p rb n", p=P)
+        y_of_piece = {}
+        z_of_piece = {}
+        mu_rstd_of_piece = {}
+        sums_of_piece = {}
+
+        def project(g, banks):
+            piece = slice(g * PIECE, (g + 1) * PIECE)
+            y = ring["y"].tile([P, PIECE_SAMPLES, PROJ], F32)
+            y_of_piece[g] = y
+            qk_sum = ring["qk_sum"].tile([P, PIECE_SAMPLES, 2 * HEADS], F32)
+            v_sum = ring["v_sum"].tile([P, PIECE_SAMPLES], F32)
+            sums_of_piece[g] = (qk_sum, v_sum)
+            for t in range(HEADS):
+                qk_ps = banks.tile([P, 2, PIECE_SAMPLES, SLOTS], F32, tag="bank")
+                for c in range(2):
+                    r = 3 * t + c
+                    for hb in range(HID_BLOCKS):
+                        nc.tensor.matmul(qk_ps[:, c, :, :].rearrange("p s n -> p (s n)"),
+                                         qkv_w_sb[:, hb, r * P:(r + 1) * P],
+                                         mem0_bf16[:, hb, piece], start=(hb == 0), stop=(hb == HID_BLOCKS - 1))
+                for c in range(2):
+                    r = 3 * t + c
+                    for s in range(PIECE_SAMPLES):
+                        nc.scalar.activation(y[:, s, r * P:(r + 1) * P], qk_ps[:, c, s, :], FUNC.Identity,
+                                             bias=late_cols[:, LATE_COL_QKV_B + r:LATE_COL_QKV_B + r + 1],
+                                             accum_out=qk_sum[:, s, 2 * t + c:2 * t + c + 1])
+            v_bias = qkv_b_sb[:].rearrange("p (t c u) -> p t c u", c=3, u=P)[:, :, 2, :]
+            v_weights = qkv_w_sb[:].rearrange("p hb (t c u) -> p hb t c u", c=3, u=P)[:, :, :, 2, :]
+            for s in range(PIECE_SAMPLES):
+                b = g * PIECE_SAMPLES + s
+                v_ps = banks.tile([P, HEADS, P], F32, tag="bank")
+                for hb in range(HID_BLOCKS):
+                    nc.tensor.matmul(v_ps[:], mem0_bf16[:, hb, b * SLOTS:(b + 1) * SLOTS], v_weights[:, hb, :, :],
+                                     start=(hb == 0), stop=(hb == HID_BLOCKS - 1))
+                nc.vector.scalar_tensor_tensor(y[:, s, :].rearrange("p (t c u) -> p t c u", c=3, u=P)[:, :, 2, :],
+                                               v_ps[:], 1.0, v_bias, ALU.mult, ALU.add,
+                                               accum_out=v_sum[:, s:s + 1])
+
+        def flip_v_params(banks):
+            for param in (ln_gain, ln_bias):
+                by_kind = param[:].rearrange("p (t c n) -> p t c n", c=3, n=SLOTS)
+                v_flipped = banks.tile([P, HEADS, P], F32, tag="bank")
+                for t in range(HEADS):
+                    nc.tensor.transpose(v_flipped[:, t, :], by_kind[:, t, 2, :], identity_f32[:])
+                nc.vector.tensor_copy(by_kind[:, :, 2, :], v_flipped[:])
+                nc.vector.tensor_scalar_mul(by_kind[:, :, 0, :], by_kind[:, :, 0, :], Q_SCALE)
+
+        with tc.psum_pool(name="head_psum", bufs=8) as head_psum:
+            cols_ps = head_psum.tile([P, P], F32, tag="bank")
             nc.tensor.transpose(cols_ps[:], rows[:], identity_f32[:])
             nc.vector.tensor_copy(cols[:], cols_ps[:, 0:N_COLS])
-            query_ps = setup_psum.tile([P, HID_BLOCKS, N_SAMPLES], F32)
+            query_ps = head_psum.tile([P, HID_BLOCKS, N_SAMPLES], F32, tag="bank")
             for hb in range(HID_BLOCKS):
                 for kb in range(EMB_BLOCKS):
                     nc.tensor.matmul(query_ps[:, hb, :], w_qry_sb[:, kb, hb * P:(hb + 1) * P], query_sb[:, kb, :],
@@ -162,75 +244,31 @@ def tile_rsaffdecoder_b_kernel(
             nc.vector.tensor_tensor(query_term[:], query_ps[:],
                                     both_biases[:].unsqueeze(2).to_broadcast([P, HID_BLOCKS, N_SAMPLES]), ALU.add)
 
+            soften(0)
+            for hb in range(HID_BLOCKS):
+                start_mem(0, hb, emb_product(0, hb, head_psum))
+            for u in range(1, LOOKUPS):
+                soften(u)
             for u in range(LOOKUPS):
-                group = slice(u * LOOKUP_SAMPLES, (u + 1) * LOOKUP_SAMPLES)
-                nc.vector.tensor_reduce(
-                    dist_min[:, group],
-                    edist[:, u * LOOKUP:(u + 1) * LOOKUP].rearrange("p (b n) -> p b n", n=SLOTS), AXIS_X, ALU.min)
-                for b in range(u * LOOKUP_SAMPLES, (u + 1) * LOOKUP_SAMPLES):
-                    sample = slice(b * SLOTS, (b + 1) * SLOTS)
-                    nc.scalar.activation(edist[:, sample], edist[:, sample], FUNC.Exp, bias=dist_min[:, b:b + 1],
-                                         scale=-1.0, accum_out=edist_sum[:, b:b + 1])
-                nc.vector.reciprocal(edist_rsum[:, group], edist_sum[:, group])
                 for hb in range(HID_BLOCKS):
-                    nc.vector.tensor_scalar_mul(w_dist_scaled[:, hb, group], edist_rsum[:, group],
-                                                cols[:, COL_W_DIST + hb:COL_W_DIST + hb + 1])
-                    for b in range(u * LOOKUP_SAMPLES, (u + 1) * LOOKUP_SAMPLES):
-                        sample = slice(b * SLOTS, (b + 1) * SLOTS)
-                        nc.scalar.activation(mem[:, hb, sample], edist[:, sample], FUNC.Identity,
-                                             bias=query_term[:, hb, b:b + 1], scale=w_dist_scaled[:, hb, b:b + 1])
-                if u == 0:
-                    add_emb(0, setup_psum, 4)
-
-        with tc.psum_pool(name="label_psum", bufs=8) as label_psum:
-            for u in range(LOOKUPS):
-                lookup = slice(u * LOOKUP, (u + 1) * LOOKUP)
-                lookup_offsets = offsets[:, u * (LOOKUP // 16):(u + 1) * (LOOKUP // 16)]
-                for hb in range(HID_BLOCKS):
-                    label_ps = label_psum.tile([P, LOOKUP], F32)
-                    nc.tensor.matmul(label_ps[:], w_lab_sb[:, hb * P:(hb + 1) * P],
-                                     table_sb[:].indirect(lookup_offsets), start=True, stop=True)
-                    nc.vector.tensor_tensor(mem[:, hb, lookup], label_ps[:], mem[:, hb, lookup], ALU.add)
+                    label_ps = label_product(u, hb, head_psum)
+                    if u == 0:
+                        finish_mem(u, hb, label_ps)
+                    else:
+                        start_mem(u, hb, label_ps)
+            late_cols_ps = head_psum.tile([P, P], F32, tag="bank")
+            nc.tensor.transpose(late_cols_ps[:], late_rows[:], identity_f32[:])
+            nc.vector.tensor_copy(late_cols[:], late_cols_ps[:, 0:N_LATE_COLS])
             round_mem0(0)
+            project(0, head_psum)
+            flip_v_params(head_psum)
 
         psum_ring = {kind: ctx.enter_context(tc.psum_pool(name="psum_" + kind, bufs=bufs)) for kind, bufs in PSUM_RINGS}
 
-        out_blocks = out.rearrange("(rb p) n -> p rb n", p=P)
-        y_of_piece = {}
-        z_of_piece = {}
-        mu_rstd_of_piece = {}
-        sums_of_piece = {}
-
-        def project(g):
-            piece = slice(g * PIECE, (g + 1) * PIECE)
-            y = ring["y"].tile([P, PIECE_SAMPLES, PROJ], F32)
-            y_of_piece[g] = y
-            qk_sum = ring["qk_sum"].tile([P, PIECE_SAMPLES, 2 * HEADS], F32)
-            v_sum = ring["v_sum"].tile([P, PIECE_SAMPLES], F32)
-            sums_of_piece[g] = (qk_sum, v_sum)
-            for t in range(HEADS):
-                qk_ps = psum_ring["bank"].tile([P, 2, PIECE_SAMPLES, SLOTS], F32, tag="bank")
-                for c in range(2):
-                    for hb in range(HID_BLOCKS):
-                        nc.tensor.matmul(qk_ps[:, c, :, :].rearrange("p s n -> p (s n)"),
-                                         w_qk_sb[:, hb, (2 * t + c) * P:(2 * t + c + 1) * P],
-                                         mem0_bf16[:, hb, piece], start=(hb == 0), stop=(hb == HID_BLOCKS - 1))
-                for c in range(2):
-                    r = 3 * t + c
-                    for s in range(PIECE_SAMPLES):
-                        nc.scalar.activation(y[:, s, r * P:(r + 1) * P], qk_ps[:, c, s, :], FUNC.Identity,
-                                             bias=cols[:, COL_QKV_B + r:COL_QKV_B + r + 1],
-                                             accum_out=qk_sum[:, s, 2 * t + c:2 * t + c + 1])
-            v_bias = qkv_b_sb[:].rearrange("p (t c u) -> p t c u", c=3, u=P)[:, :, 2, :]
-            for s in range(PIECE_SAMPLES):
-                b = g * PIECE_SAMPLES + s
-                v_ps = psum_ring["bank"].tile([P, HEADS, P], F32, tag="bank")
-                for hb in range(HID_BLOCKS):
-                    nc.tensor.matmul(v_ps[:].rearrange("p t u -> p (t u)"), mem0_bf16[:, hb, b * SLOTS:(b + 1) * SLOTS],
-                                     w_v_sb[:, hb, :], start=(hb == 0), stop=(hb == HID_BLOCKS - 1))
-                nc.vector.scalar_tensor_tensor(y[:, s, :].rearrange("p (t c u) -> p t c u", c=3, u=P)[:, :, 2, :],
-                                               v_ps[:], 1.0, v_bias, ALU.mult, ALU.add,
-                                               accum_out=v_sum[:, s:s + 1])
+        def complete_mem0(u):
+            for hb in range(HID_BLOCKS):
+                finish_mem(u, hb, emb_product(u, hb, psum_ring["bank"]))
+            round_mem0(u)
 
         def measure(g):
             y = y_of_piece[g]
@@ -326,32 +364,23 @@ def tile_rsaffdecoder_b_kernel(
             result = ring["result"].tile([P, HID_BLOCKS, SLOTS], F32)
             for rb in range(HID_BLOCKS):
                 nc.vector.scalar_tensor_tensor(result[:, rb, :], normed_flipped[:, rb, :],
-                                               cols[:, COL_MLP_LN_W + rb:COL_MLP_LN_W + rb + 1], mem1_biased[:, rb, :],
+                                               late_cols[:, LATE_COL_MLP_LN_W + rb:LATE_COL_MLP_LN_W + rb + 1],
+                                               mem1_biased[:, rb, :],
                                                ALU.mult, ALU.add)
             nc.sync.dma_start(out_blocks[:, :, sample], result[:])
 
-        project(0)
-
-        for param in (ln_gain, ln_bias):
-            by_kind = param[:].rearrange("p (t c n) -> p t c n", c=3, n=SLOTS)
-            v_flipped = psum_ring["flipped"].tile([P, HEADS, P], F32, tag="flipped")
-            for t in range(HEADS):
-                nc.tensor.transpose(v_flipped[:, t, :], by_kind[:, t, 2, :], identity_f32[:])
-            nc.vector.tensor_copy(by_kind[:, :, 2, :], v_flipped[:])
-            nc.vector.tensor_scalar_mul(by_kind[:, :, 0, :], by_kind[:, :, 0, :], Q_SCALE)
-
         measure(0)
+        complete_mem0(1)
         for g in range(PIECES):
             normalise(g)
             if g == 0:
-                project(1)
+                project(1, psum_ring["bank"])
             if g + 1 < PIECES:
                 measure(g + 1)
             for s in range(PIECE_SAMPLES):
                 attend_and_mlp(g, s)
             ahead = g + AHEAD
             if ahead < PIECES:
-                if ahead % 2 == 0:
-                    add_emb(ahead // 2, psum_ring["bank"], 3)
-                    round_mem0(ahead // 2)
-                project(ahead)
+                project(ahead, psum_ring["bank"])
+                if ahead % 2 == 0 and ahead // 2 + 1 < LOOKUPS:
+                    complete_mem0(ahead // 2 + 1)

@@ -39,8 +39,12 @@ LATE_COL_MLP_LN_W = 0
 LATE_COL_QKV_B = 4
 N_LATE_COLS = 16
 
+SUM_V = 8
+SUM_SQ = 9
+N_SUMS = 13
+
 SBUF_RINGS = (
-    ("y", 3), ("z", 3), ("centred", 2), ("qk_sum", 3), ("v_sum", 3), ("y_sum", 3), ("sq_sum", 3), ("squares", 1), ("sample_moments", 3),
+    ("y", 3), ("z", 3), ("centred", 2), ("part_sums", 3), ("squares", 1), ("sample_moments", 3),
     ("mu_sq", 3), ("var", 3), ("rstd", 3), ("exp_scores", 2), ("att", 3), ("att_flipped", 3), ("mem1_biased", 4),
     ("relu_mem1", 3), ("f", 2), ("normed", 2), ("result", 3), ("minus_max", 3), ("exp_sum", 3),
     ("exp_rsum", 3), ("f_stats", 3), ("f_moments", 3), ("var2", 3), ("rstd2", 3),
@@ -73,28 +77,28 @@ def tile_rsaffdecoder_b_kernel(
         late_rows = held.tile([P, P], F32)
         nc.vector.memset(late_rows[:], 0.0)
 
+        table_sb = held.tile([P, TABLE_COLS], BF16)
+        nc.scalar.dma_start(table_sb[:], table)
         edist = held.tile([P, N_TOK], F32)
         distance_row = distances.rearrange("o n -> (o n)")
         nc.scalar.dma_start(edist[:, 0:LOOKUP], distance_row[0:LOOKUP].partition_broadcast(P))
         nc.scalar.dma_start(rows[COL_W_DIST:COL_W_DIST + HID_BLOCKS, :], as_rows(w_dist))
-        query_sb = held.tile([P, EMB_BLOCKS, N_SAMPLES], BF16)
-        nc.scalar.dma_start(query_sb[:], query.rearrange("(k p) b -> p k b", p=P))
+        nc.scalar.dma_start(rows[COL_PRE_B:COL_PRE_B + HID_BLOCKS, :], as_rows(pre_b))
+        nc.scalar.dma_start(rows[COL_MLP_LN_B:COL_MLP_LN_B + HID_BLOCKS, :], as_rows(mlp_ln_b))
 
-        table_sb = held.tile([P, TABLE_COLS], BF16)
-        nc.sync.dma_start(table_sb[:], table)
-        offsets = held.tile([P, N_TOK // 16], U16, name="offsets")
-        nc.sync.dma_start(offsets[:], offs)
-        w_lab_sb = held.tile([P, HID], BF16)
-        nc.sync.dma_start(w_lab_sb[:], w_lab)
         w_emb_sb = held.tile([P, EMB_BLOCKS, HID], BF16)
         nc.sync.dma_start(w_emb_sb[:], w_emb.rearrange("(k p) h -> p k h", p=P))
         emb_sb = held.tile([P, EMB_BLOCKS, N_TOK], BF16)
         emb_blocks = emb.rearrange("(k p) n -> p k n", p=P)
         nc.sync.dma_start(emb_sb[:, :, 0:LOOKUP], emb_blocks[:, :, 0:LOOKUP])
-        nc.sync.dma_start(rows[COL_PRE_B:COL_PRE_B + HID_BLOCKS, :], as_rows(pre_b))
-        nc.sync.dma_start(rows[COL_MLP_LN_B:COL_MLP_LN_B + HID_BLOCKS, :], as_rows(mlp_ln_b))
+        offsets = held.tile([P, N_TOK // 16], U16, name="offsets")
+        nc.sync.dma_start(offsets[:], offs)
+        w_lab_sb = held.tile([P, HID], BF16)
+        nc.sync.dma_start(w_lab_sb[:], w_lab)
         w_qry_sb = held.tile([P, EMB_BLOCKS, HID], BF16)
         nc.sync.dma_start(w_qry_sb[:], w_qry.rearrange("(k p) h -> p k h", p=P))
+        query_sb = held.tile([P, EMB_BLOCKS, N_SAMPLES], BF16)
+        nc.sync.dma_start(query_sb[:], query.rearrange("(k p) b -> p k b", p=P))
         nc.sync.dma_start(edist[:, LOOKUP:N_TOK], distance_row[LOOKUP:N_TOK].partition_broadcast(P))
         qkv_w_sb = held.tile([P, HID_BLOCKS, PROJ], BF16)
         nc.sync.dma_start(qkv_w_sb[:], qkv_w.rearrange("(hb p) r -> p hb r", p=P))
@@ -190,9 +194,19 @@ def tile_rsaffdecoder_b_kernel(
             piece = slice(g * PIECE, (g + 1) * PIECE)
             y = ring["y"].tile([P, PIECE_SAMPLES, PROJ], F32)
             y_of_piece[g] = y
-            qk_sum = ring["qk_sum"].tile([P, PIECE_SAMPLES, 2 * HEADS], F32)
-            v_sum = ring["v_sum"].tile([P, PIECE_SAMPLES], F32)
-            sums_of_piece[g] = (qk_sum, v_sum)
+            part_sums = ring["part_sums"].tile([P, PIECE_SAMPLES, N_SUMS], F32)
+            sums_of_piece[g] = part_sums
+            v_bias = qkv_b_sb[:].rearrange("p (t c u) -> p t c u", c=3, u=P)[:, :, 2, :]
+            v_weights = qkv_w_sb[:].rearrange("p hb (t c u) -> p hb t c u", c=3, u=P)[:, :, :, 2, :]
+            for s in range(PIECE_SAMPLES):
+                b = g * PIECE_SAMPLES + s
+                v_ps = banks.tile([P, HEADS, P], F32, tag="bank")
+                for hb in range(HID_BLOCKS):
+                    nc.tensor.matmul(v_ps[:], mem0_bf16[:, hb, b * SLOTS:(b + 1) * SLOTS], v_weights[:, hb, :, :],
+                                     start=(hb == 0), stop=(hb == HID_BLOCKS - 1))
+                nc.vector.scalar_tensor_tensor(y[:, s, :].rearrange("p (t c u) -> p t c u", c=3, u=P)[:, :, 2, :],
+                                               v_ps[:], 1.0, v_bias, ALU.mult, ALU.add,
+                                               accum_out=part_sums[:, s, SUM_V:SUM_V + 1])
             for t in range(HEADS):
                 qk_ps = banks.tile([P, 2, PIECE_SAMPLES, SLOTS], F32, tag="bank")
                 for c in range(2):
@@ -206,18 +220,28 @@ def tile_rsaffdecoder_b_kernel(
                     for s in range(PIECE_SAMPLES):
                         nc.scalar.activation(y[:, s, r * P:(r + 1) * P], qk_ps[:, c, s, :], FUNC.Identity,
                                              bias=late_cols[:, LATE_COL_QKV_B + r:LATE_COL_QKV_B + r + 1],
-                                             accum_out=qk_sum[:, s, 2 * t + c:2 * t + c + 1])
-            v_bias = qkv_b_sb[:].rearrange("p (t c u) -> p t c u", c=3, u=P)[:, :, 2, :]
-            v_weights = qkv_w_sb[:].rearrange("p hb (t c u) -> p hb t c u", c=3, u=P)[:, :, :, 2, :]
-            for s in range(PIECE_SAMPLES):
-                b = g * PIECE_SAMPLES + s
-                v_ps = banks.tile([P, HEADS, P], F32, tag="bank")
-                for hb in range(HID_BLOCKS):
-                    nc.tensor.matmul(v_ps[:], mem0_bf16[:, hb, b * SLOTS:(b + 1) * SLOTS], v_weights[:, hb, :, :],
-                                     start=(hb == 0), stop=(hb == HID_BLOCKS - 1))
-                nc.vector.scalar_tensor_tensor(y[:, s, :].rearrange("p (t c u) -> p t c u", c=3, u=P)[:, :, 2, :],
-                                               v_ps[:], 1.0, v_bias, ALU.mult, ALU.add,
-                                               accum_out=v_sum[:, s:s + 1])
+                                             accum_out=part_sums[:, s, 2 * t + c:2 * t + c + 1])
+                for s in range(PIECE_SAMPLES):
+                    squares = ring["squares"].tile([P, HEAD_ROWS], BF16)
+                    nc.scalar.activation(squares[:], y[:, s, t * HEAD_ROWS:(t + 1) * HEAD_ROWS], FUNC.Square,
+                                         accum_out=part_sums[:, s, SUM_SQ + t:SUM_SQ + t + 1])
+
+        def measure(g, banks, tag):
+            part_sums = sums_of_piece[g]
+            sample_ps = banks.tile([P, PIECE_SAMPLES, N_SUMS], F32, tag=tag)
+            nc.tensor.matmul(sample_ps[:].rearrange("p s k -> p (s k)"), spread_mean[:],
+                             part_sums[:].rearrange("p s k -> p (s k)"), start=True, stop=True)
+            sample_moments = ring["sample_moments"].tile([P, 2, PIECE_SAMPLES], F32)
+            nc.vector.tensor_reduce(sample_moments[:, 0, :], sample_ps[:, :, 0:SUM_SQ], AXIS_X, ALU.add)
+            nc.vector.tensor_reduce(sample_moments[:, 1, :], sample_ps[:, :, SUM_SQ:N_SUMS], AXIS_X, ALU.add)
+            mu_sq = ring["mu_sq"].tile([P, PIECE_SAMPLES], F32)
+            nc.vector.tensor_tensor(mu_sq[:], sample_moments[:, 0, :], sample_moments[:, 0, :], ALU.mult)
+            var = ring["var"].tile([P, PIECE_SAMPLES], F32)
+            nc.vector.tensor_tensor(var[:], sample_moments[:, 1, :], mu_sq[:], ALU.subtract)
+            nc.vector.tensor_scalar(var[:], var[:], 0.0, EPS, ALU.max, ALU.add)
+            rstd = ring["rstd"].tile([P, PIECE_SAMPLES], F32)
+            nc.gpsimd.tensor_tensor(rstd[:], var[:], minus_half[:], ALU.pow)
+            mu_rstd_of_piece[g] = (sample_moments, rstd)
 
         def flip_v_params(banks):
             for param in (ln_gain, ln_bias):
@@ -229,6 +253,7 @@ def tile_rsaffdecoder_b_kernel(
                 nc.vector.tensor_scalar_mul(by_kind[:, :, 0, :], by_kind[:, :, 0, :], Q_SCALE)
 
         with tc.psum_pool(name="head_psum", bufs=8) as head_psum:
+            first_emb_ps = [emb_product(0, hb, head_psum) for hb in range(HID_BLOCKS)]
             cols_ps = head_psum.tile([P, P], F32, tag="bank")
             nc.tensor.transpose(cols_ps[:], rows[:], identity_f32[:])
             nc.vector.tensor_copy(cols[:], cols_ps[:, 0:N_COLS])
@@ -243,24 +268,25 @@ def tile_rsaffdecoder_b_kernel(
             nc.vector.tensor_tensor(both_biases[:], cols[:, COL_PRE_B:COL_PRE_B + HID_BLOCKS], last_bias, ALU.add)
             nc.vector.tensor_tensor(query_term[:], query_ps[:],
                                     both_biases[:].unsqueeze(2).to_broadcast([P, HID_BLOCKS, N_SAMPLES]), ALU.add)
-
             soften(0)
             for hb in range(HID_BLOCKS):
-                start_mem(0, hb, emb_product(0, hb, head_psum))
-            for u in range(1, LOOKUPS):
-                soften(u)
-            for u in range(LOOKUPS):
-                for hb in range(HID_BLOCKS):
-                    label_ps = label_product(u, hb, head_psum)
-                    if u == 0:
-                        finish_mem(u, hb, label_ps)
-                    else:
-                        start_mem(u, hb, label_ps)
+                start_mem(0, hb, first_emb_ps[hb])
+            soften(1)
+            for hb in range(HID_BLOCKS):
+                finish_mem(0, hb, label_product(0, hb, head_psum))
+            for hb in range(HID_BLOCKS):
+                start_mem(1, hb, label_product(1, hb, head_psum))
             late_cols_ps = head_psum.tile([P, P], F32, tag="bank")
             nc.tensor.transpose(late_cols_ps[:], late_rows[:], identity_f32[:])
             nc.vector.tensor_copy(late_cols[:], late_cols_ps[:, 0:N_LATE_COLS])
             round_mem0(0)
             project(0, head_psum)
+            for u in (2, 3):
+                soften(u)
+                for hb in range(HID_BLOCKS):
+                    start_mem(u, hb, label_product(u, hb, head_psum))
+            measure(0, head_psum, "bank")
+            project(1, head_psum)
             flip_v_params(head_psum)
 
         psum_ring = {kind: ctx.enter_context(tc.psum_pool(name="psum_" + kind, bufs=bufs)) for kind, bufs in PSUM_RINGS}
@@ -269,30 +295,6 @@ def tile_rsaffdecoder_b_kernel(
             for hb in range(HID_BLOCKS):
                 finish_mem(u, hb, emb_product(u, hb, psum_ring["bank"]))
             round_mem0(u)
-
-        def measure(g):
-            y = y_of_piece[g]
-            qk_sum, v_sum = sums_of_piece[g]
-            y_sum = ring["y_sum"].tile([P, PIECE_SAMPLES], F32)
-            nc.vector.tensor_reduce(y_sum[:], qk_sum[:], AXIS_X, ALU.add)
-            nc.vector.tensor_tensor(y_sum[:], y_sum[:], v_sum[:], ALU.add)
-            sq_sum = ring["sq_sum"].tile([P, PIECE_SAMPLES], F32)
-            for s in range(PIECE_SAMPLES):
-                squares = ring["squares"].tile([P, PROJ], BF16)
-                nc.scalar.activation(squares[:], y[:, s, :], FUNC.Square, accum_out=sq_sum[:, s:s + 1])
-            sample_ps = psum_ring["scores"].tile([P, 2, PIECE_SAMPLES], F32, tag="scores")
-            nc.tensor.matmul(sample_ps[:, 0, :], spread_mean[:], y_sum[:], start=True, stop=True)
-            nc.tensor.matmul(sample_ps[:, 1, :], spread_mean[:], sq_sum[:], start=True, stop=True)
-            sample_moments = ring["sample_moments"].tile([P, 2, PIECE_SAMPLES], F32)
-            nc.vector.tensor_copy(sample_moments[:], sample_ps[:])
-            mu_sq = ring["mu_sq"].tile([P, PIECE_SAMPLES], F32)
-            nc.vector.tensor_tensor(mu_sq[:], sample_moments[:, 0, :], sample_moments[:, 0, :], ALU.mult)
-            var = ring["var"].tile([P, PIECE_SAMPLES], F32)
-            nc.vector.tensor_tensor(var[:], sample_moments[:, 1, :], mu_sq[:], ALU.subtract)
-            nc.vector.tensor_scalar(var[:], var[:], 0.0, EPS, ALU.max, ALU.add)
-            rstd = ring["rstd"].tile([P, PIECE_SAMPLES], F32)
-            nc.gpsimd.tensor_tensor(rstd[:], var[:], minus_half[:], ALU.pow)
-            mu_rstd_of_piece[g] = (sample_moments, rstd)
 
         def normalise(g):
             y = y_of_piece[g]
@@ -369,14 +371,11 @@ def tile_rsaffdecoder_b_kernel(
                                                ALU.mult, ALU.add)
             nc.sync.dma_start(out_blocks[:, :, sample], result[:])
 
-        measure(0)
         complete_mem0(1)
         for g in range(PIECES):
             normalise(g)
-            if g == 0:
-                project(1, psum_ring["bank"])
             if g + 1 < PIECES:
-                measure(g + 1)
+                measure(g + 1, psum_ring["scores"], "scores")
             for s in range(PIECE_SAMPLES):
                 attend_and_mlp(g, s)
             ahead = g + AHEAD

@@ -27,7 +27,6 @@ LOOKUP_SAMPLES = LOOKUP // SLOTS
 PIECE = 256
 PIECES = N_TOK // PIECE
 PIECE_SAMPLES = PIECE // SLOTS
-AHEAD = 2
 EPS = 1e-5
 Q_SCALE = 128.0 ** -0.5
 
@@ -44,7 +43,7 @@ SUM_SQ = 9
 N_SUMS = 13
 
 SBUF_RINGS = (
-    ("y", 3), ("z", 3), ("centred", 2), ("part_sums", 3), ("squares", 1), ("sample_moments", 3),
+    ("y", 3), ("z", 4), ("centred", 2), ("part_sums", 3), ("squares", 1), ("sample_moments", 3),
     ("mu_sq", 3), ("var", 3), ("rstd", 3), ("exp_scores", 2), ("att", 3), ("att_flipped", 3), ("mem1_biased", 4),
     ("relu_mem1", 3), ("f", 2), ("normed", 2), ("result", 3), ("minus_max", 3), ("exp_sum", 3),
     ("exp_rsum", 3), ("f_stats", 3), ("f_moments", 3), ("var2", 3), ("rstd2", 3),
@@ -186,7 +185,10 @@ def tile_rsaffdecoder_b_kernel(
 
         out_blocks = out.rearrange("(rb p) n -> p rb n", p=P)
         y_of_piece = {}
-        z_of_piece = {}
+        q_k_v_of_sample = {}
+        att_of_sample = {}
+        mem1_of_sample = {}
+        normed_of_sample = {}
         mu_rstd_of_piece = {}
         sums_of_piece = {}
 
@@ -296,23 +298,19 @@ def tile_rsaffdecoder_b_kernel(
                 finish_mem(u, hb, emb_product(u, hb, psum_ring["bank"]))
             round_mem0(u)
 
-        def normalise(g):
+        def normalise(b):
+            g, s = divmod(b, PIECE_SAMPLES)
             y = y_of_piece[g]
             sample_moments, rstd = mu_rstd_of_piece[g]
-            z = ring["z"].tile([P, PIECE_SAMPLES, PROJ], BF16)
-            z_of_piece[g] = z
-            for s in range(PIECE_SAMPLES):
-                centred = ring["centred"].tile([P, PROJ], F32)
-                nc.vector.scalar_tensor_tensor(centred[:], y[:, s, :], sample_moments[:, 0, s:s + 1], ln_gain[:],
-                                               ALU.subtract, ALU.mult)
-                nc.vector.scalar_tensor_tensor(z[:, s, :], centred[:], rstd[:, s:s + 1], ln_bias[:],
-                                               ALU.mult, ALU.add)
+            z = ring["z"].tile([P, PROJ], BF16)
+            q_k_v_of_sample[b] = z[:].rearrange("p (t c n) -> p t c n", c=3, n=P)
+            centred = ring["centred"].tile([P, PROJ], F32)
+            nc.vector.scalar_tensor_tensor(centred[:], y[:, s, :], sample_moments[:, 0, s:s + 1], ln_gain[:],
+                                           ALU.subtract, ALU.mult)
+            nc.vector.scalar_tensor_tensor(z[:], centred[:], rstd[:, s:s + 1], ln_bias[:], ALU.mult, ALU.add)
 
-        def attend_and_mlp(g, s):
-            b = g * PIECE_SAMPLES + s
-            sample = slice(b * SLOTS, (b + 1) * SLOTS)
-            q_k_v = z_of_piece[g][:, s, :].rearrange("p (t c n) -> p t c n", c=3, n=P)
-
+        def soft_max(b):
+            q_k_v = q_k_v_of_sample[b]
             scores = psum_ring["scores"].tile([P, HEADS, SLOTS], F32, tag="scores")
             for t in range(HEADS):
                 nc.tensor.matmul(scores[:, t, :], q_k_v[:, t, 0, :], q_k_v[:, t, 1, :], start=True, stop=True)
@@ -328,6 +326,12 @@ def tile_rsaffdecoder_b_kernel(
             att = ring["att"].tile([P, HEADS, SLOTS], BF16)
             for t in range(HEADS):
                 nc.scalar.activation(att[:, t, :], exp_scores[:, t, :], FUNC.Copy, scale=exp_rsum[:, t:t + 1])
+            att_of_sample[b] = att
+
+        def weighted_sum(b):
+            sample = slice(b * SLOTS, (b + 1) * SLOTS)
+            q_k_v = q_k_v_of_sample[b]
+            att = att_of_sample[b]
             att_flipped_ps = psum_ring["att_flipped"].tile([P, HEADS, SLOTS], BF16, tag="att_flipped")
             for t in range(HEADS):
                 nc.tensor.transpose(att_flipped_ps[:, t, :], att[:, t, :], identity_bf16[:])
@@ -343,6 +347,10 @@ def tile_rsaffdecoder_b_kernel(
             relu_mem1 = ring["relu_mem1"].tile([P, HID_BLOCKS, SLOTS], BF16)
             for hb in range(HID_BLOCKS):
                 nc.scalar.activation(relu_mem1[:, hb, :], mem1_biased[:, hb, :], FUNC.Relu, bias=minus_last_bias[:, hb:hb + 1])
+            mem1_of_sample[b] = (mem1_biased, relu_mem1)
+
+        def mlp(b):
+            relu_mem1 = mem1_of_sample[b][1]
             f_ps = psum_ring["f"].tile([P, HID], F32, tag="f")
             for hb in range(HID_BLOCKS):
                 nc.tensor.matmul(f_ps[:], relu_mem1[:, hb, :], mlp_w_sb[:, hb, :],
@@ -359,7 +367,12 @@ def tile_rsaffdecoder_b_kernel(
             nc.gpsimd.tensor_tensor(rstd2[:], var2[:], minus_half[:, 0:1], ALU.pow)
             normed = ring["normed"].tile([P, HID], F32)
             nc.vector.tensor_scalar(normed[:], f[:], f_moments[:, 0:1], rstd2[:], ALU.subtract, ALU.mult)
+            normed_of_sample[b] = normed
 
+        def finish(b):
+            sample = slice(b * SLOTS, (b + 1) * SLOTS)
+            mem1_biased = mem1_of_sample[b][0]
+            normed = normed_of_sample[b]
             normed_flipped = psum_ring["flipped"].tile([P, HID_BLOCKS, SLOTS], F32, tag="flipped")
             for rb in range(HID_BLOCKS):
                 nc.tensor.transpose(normed_flipped[:, rb, :], normed[:, rb * P:(rb + 1) * P], identity_f32[:])
@@ -372,14 +385,22 @@ def tile_rsaffdecoder_b_kernel(
             nc.sync.dma_start(out_blocks[:, :, sample], result[:])
 
         complete_mem0(1)
-        for g in range(PIECES):
-            normalise(g)
-            if g + 1 < PIECES:
-                measure(g + 1, psum_ring["scores"], "scores")
-            for s in range(PIECE_SAMPLES):
-                attend_and_mlp(g, s)
-            ahead = g + AHEAD
-            if ahead < PIECES:
-                project(ahead, psum_ring["bank"])
-                if ahead % 2 == 0 and ahead // 2 + 1 < LOOKUPS:
-                    complete_mem0(ahead // 2 + 1)
+        for tick in range(-1, N_SAMPLES + 3):
+            if 0 <= tick - 3 < N_SAMPLES:
+                finish(tick - 3)
+            if 0 <= tick - 2 < N_SAMPLES:
+                mlp(tick - 2)
+            if 0 <= tick - 1 < N_SAMPLES:
+                weighted_sum(tick - 1)
+            if 0 <= tick < N_SAMPLES:
+                soft_max(tick)
+            if tick + 1 < N_SAMPLES:
+                normalise(tick + 1)
+            g, s = divmod(tick + 3, PIECE_SAMPLES)
+            if s == 0 and g < PIECES:
+                measure(g, psum_ring["scores"], "scores")
+            g, s = divmod(tick + 5, PIECE_SAMPLES)
+            if s == 0 and g < PIECES:
+                project(g, psum_ring["bank"])
+                if g % 2 == 0 and g // 2 + 1 < LOOKUPS:
+                    complete_mem0(g // 2 + 1)

@@ -43,9 +43,9 @@ SUM_SQ = 9
 N_SUMS = 13
 
 SBUF_RINGS = (
-    ("y", 3), ("z", 4), ("centred", 2), ("part_sums", 3), ("squares", 1), ("sample_moments", 3),
-    ("mu_sq", 3), ("var", 3), ("rstd", 3), ("exp_scores", 2), ("att", 3), ("att_flipped", 3), ("mem1_biased", 4),
-    ("relu_mem1", 3), ("f", 2), ("normed", 2), ("result", 3), ("minus_max", 3), ("exp_sum", 3),
+    ("y", 3), ("z", 6), ("centred", 2), ("part_sums", 3), ("squares", 1), ("sample_moments", 3),
+    ("mu_sq", 3), ("var", 3), ("rstd", 3), ("exp_scores", 3), ("att", 3), ("att_flipped", 3), ("mem1_biased", 5),
+    ("relu_mem1", 3), ("f", 3), ("normed", 3), ("result", 3), ("minus_max", 3), ("exp_sum", 3),
     ("exp_rsum", 3), ("f_stats", 3), ("f_moments", 3), ("var2", 3), ("rstd2", 3),
 )
 PSUM_RINGS = (("bank", 3), ("scores", 1), ("att_flipped", 1), ("o", 1), ("f", 1), ("flipped", 1))
@@ -186,9 +186,6 @@ def tile_rsaffdecoder_b_kernel(
         out_blocks = out.rearrange("(rb p) n -> p rb n", p=P)
         y_of_piece = {}
         q_k_v_of_sample = {}
-        att_of_sample = {}
-        mem1_of_sample = {}
-        normed_of_sample = {}
         mu_rstd_of_piece = {}
         sums_of_piece = {}
 
@@ -309,13 +306,20 @@ def tile_rsaffdecoder_b_kernel(
                                            ALU.subtract, ALU.mult)
             nc.vector.scalar_tensor_tensor(z[:], centred[:], rstd[:, s:s + 1], ln_bias[:], ALU.mult, ALU.add)
 
-        def soft_max(b):
+        kept = {b: {} for b in range(N_SAMPLES)}
+
+        def score(b):
             q_k_v = q_k_v_of_sample[b]
             scores = psum_ring["scores"].tile([P, HEADS, SLOTS], F32, tag="scores")
             for t in range(HEADS):
                 nc.tensor.matmul(scores[:, t, :], q_k_v[:, t, 0, :], q_k_v[:, t, 1, :], start=True, stop=True)
             minus_max = ring["minus_max"].tile([P, HEADS], F32)
             nc.vector.tensor_reduce(minus_max[:], scores[:], AXIS_X, ALU.max, negate=True)
+            kept[b]["scores"] = scores
+            kept[b]["minus_max"] = minus_max
+
+        def exponentiate(b):
+            scores, minus_max = kept[b]["scores"], kept[b]["minus_max"]
             exp_scores = ring["exp_scores"].tile([P, HEADS, SLOTS], F32)
             exp_sum = ring["exp_sum"].tile([P, HEADS], F32)
             for t in range(HEADS):
@@ -323,34 +327,39 @@ def tile_rsaffdecoder_b_kernel(
                                      bias=minus_max[:, t:t + 1], accum_out=exp_sum[:, t:t + 1])
             exp_rsum = ring["exp_rsum"].tile([P, HEADS], F32)
             nc.vector.reciprocal(exp_rsum[:], exp_sum[:])
+            kept[b]["exp_scores"] = exp_scores
+            kept[b]["exp_rsum"] = exp_rsum
+
+        def divide_and_flip(b):
+            exp_scores, exp_rsum = kept[b]["exp_scores"], kept[b]["exp_rsum"]
             att = ring["att"].tile([P, HEADS, SLOTS], BF16)
             for t in range(HEADS):
                 nc.scalar.activation(att[:, t, :], exp_scores[:, t, :], FUNC.Copy, scale=exp_rsum[:, t:t + 1])
-            att_of_sample[b] = att
-
-        def weighted_sum(b):
-            sample = slice(b * SLOTS, (b + 1) * SLOTS)
-            q_k_v = q_k_v_of_sample[b]
-            att = att_of_sample[b]
             att_flipped_ps = psum_ring["att_flipped"].tile([P, HEADS, SLOTS], BF16, tag="att_flipped")
             for t in range(HEADS):
                 nc.tensor.transpose(att_flipped_ps[:, t, :], att[:, t, :], identity_bf16[:])
+            kept[b]["att_flipped_ps"] = att_flipped_ps
+
+        def weigh(b):
+            q_k_v = q_k_v_of_sample[b]
             att_flipped = ring["att_flipped"].tile([P, HEADS, SLOTS], BF16)
-            nc.scalar.activation(att_flipped[:], att_flipped_ps[:], FUNC.Copy)
+            nc.scalar.activation(att_flipped[:], kept[b]["att_flipped_ps"][:], FUNC.Copy)
             o_ps = psum_ring["o"].tile([P, HEADS, SLOTS], F32, tag="o")
             for t in range(HEADS):
                 nc.tensor.matmul(o_ps[:, t, :], q_k_v[:, t, 2, :], att_flipped[:, t, :], start=True, stop=True)
+            kept[b]["o_ps"] = o_ps
 
+        def add_and_relu(b):
             mem1_biased = ring["mem1_biased"].tile([P, HID_BLOCKS, SLOTS], F32)
-            nc.vector.tensor_tensor(mem1_biased[:], o_ps[:], mem[:, :, sample], ALU.add)
-
+            nc.vector.tensor_tensor(mem1_biased[:], kept[b]["o_ps"][:], mem[:, :, b * SLOTS:(b + 1) * SLOTS], ALU.add)
             relu_mem1 = ring["relu_mem1"].tile([P, HID_BLOCKS, SLOTS], BF16)
             for hb in range(HID_BLOCKS):
                 nc.scalar.activation(relu_mem1[:, hb, :], mem1_biased[:, hb, :], FUNC.Relu, bias=minus_last_bias[:, hb:hb + 1])
-            mem1_of_sample[b] = (mem1_biased, relu_mem1)
+            kept[b]["mem1_biased"] = mem1_biased
+            kept[b]["relu_mem1"] = relu_mem1
 
         def mlp(b):
-            relu_mem1 = mem1_of_sample[b][1]
+            relu_mem1 = kept[b]["relu_mem1"]
             f_ps = psum_ring["f"].tile([P, HID], F32, tag="f")
             for hb in range(HID_BLOCKS):
                 nc.tensor.matmul(f_ps[:], relu_mem1[:, hb, :], mlp_w_sb[:, hb, :],
@@ -363,16 +372,20 @@ def tile_rsaffdecoder_b_kernel(
             nc.vector.bn_aggr(f_moments[:], f_stats[:])
             var2 = ring["var2"].tile([P, 1], F32)
             nc.vector.tensor_scalar_add(var2[:], f_moments[:, 1:2], EPS)
+            kept[b]["f"] = f
+            kept[b]["f_moments"] = f_moments
+            kept[b]["var2"] = var2
+
+        def normalise_mlp(b):
             rstd2 = ring["rstd2"].tile([P, 1], F32)
-            nc.gpsimd.tensor_tensor(rstd2[:], var2[:], minus_half[:, 0:1], ALU.pow)
+            nc.gpsimd.tensor_tensor(rstd2[:], kept[b]["var2"][:], minus_half[:, 0:1], ALU.pow)
             normed = ring["normed"].tile([P, HID], F32)
-            nc.vector.tensor_scalar(normed[:], f[:], f_moments[:, 0:1], rstd2[:], ALU.subtract, ALU.mult)
-            normed_of_sample[b] = normed
+            nc.vector.tensor_scalar(normed[:], kept[b]["f"][:], kept[b]["f_moments"][:, 0:1], rstd2[:],
+                                    ALU.subtract, ALU.mult)
+            kept[b]["normed"] = normed
 
         def finish(b):
-            sample = slice(b * SLOTS, (b + 1) * SLOTS)
-            mem1_biased = mem1_of_sample[b][0]
-            normed = normed_of_sample[b]
+            mem1_biased, normed = kept[b]["mem1_biased"], kept[b]["normed"]
             normed_flipped = psum_ring["flipped"].tile([P, HID_BLOCKS, SLOTS], F32, tag="flipped")
             for rb in range(HID_BLOCKS):
                 nc.tensor.transpose(normed_flipped[:, rb, :], normed[:, rb * P:(rb + 1) * P], identity_f32[:])
@@ -382,23 +395,20 @@ def tile_rsaffdecoder_b_kernel(
                                                late_cols[:, LATE_COL_MLP_LN_W + rb:LATE_COL_MLP_LN_W + rb + 1],
                                                mem1_biased[:, rb, :],
                                                ALU.mult, ALU.add)
-            nc.sync.dma_start(out_blocks[:, :, sample], result[:])
+            nc.sync.dma_start(out_blocks[:, :, b * SLOTS:(b + 1) * SLOTS], result[:])
 
+        stages = (score, exponentiate, divide_and_flip, weigh, add_and_relu, mlp, normalise_mlp, finish)
         complete_mem0(1)
-        for tick in range(-1, N_SAMPLES + 3):
-            if 0 <= tick - 3 < N_SAMPLES:
-                finish(tick - 3)
-            if 0 <= tick - 2 < N_SAMPLES:
-                mlp(tick - 2)
-            if 0 <= tick - 1 < N_SAMPLES:
-                weighted_sum(tick - 1)
-            if 0 <= tick < N_SAMPLES:
-                soft_max(tick)
+        for tick in range(-1, N_SAMPLES + len(stages) - 1):
+            for lag in reversed(range(len(stages))):
+                if lag == 0:
+                    g, s = divmod(tick + 3, PIECE_SAMPLES)
+                    if s == 0 and g < PIECES:
+                        measure(g, psum_ring["scores"], "scores")
+                if 0 <= tick - lag < N_SAMPLES:
+                    stages[lag](tick - lag)
             if tick + 1 < N_SAMPLES:
                 normalise(tick + 1)
-            g, s = divmod(tick + 3, PIECE_SAMPLES)
-            if s == 0 and g < PIECES:
-                measure(g, psum_ring["scores"], "scores")
             g, s = divmod(tick + 5, PIECE_SAMPLES)
             if s == 0 and g < PIECES:
                 project(g, psum_ring["bank"])

@@ -313,9 +313,11 @@ def tile_rsaffdecoder_b_kernel(
             scores = psum_ring["scores"].tile([P, HEADS, SLOTS], F32, tag="scores")
             for t in range(HEADS):
                 nc.tensor.matmul(scores[:, t, :], q_k_v[:, t, 0, :], q_k_v[:, t, 1, :], start=True, stop=True)
-            minus_max = ring["minus_max"].tile([P, HEADS], F32)
-            nc.vector.tensor_reduce(minus_max[:], scores[:], AXIS_X, ALU.max, negate=True)
             kept[b]["scores"] = scores
+
+        def find_max(b):
+            minus_max = ring["minus_max"].tile([P, HEADS], F32)
+            nc.vector.tensor_reduce(minus_max[:], kept[b]["scores"][:], AXIS_X, ALU.max, negate=True)
             kept[b]["minus_max"] = minus_max
 
         def exponentiate(b):
@@ -325,47 +327,61 @@ def tile_rsaffdecoder_b_kernel(
             for t in range(HEADS):
                 nc.scalar.activation(exp_scores[:, t, :], scores[:, t, :], FUNC.Exp,
                                      bias=minus_max[:, t:t + 1], accum_out=exp_sum[:, t:t + 1])
-            exp_rsum = ring["exp_rsum"].tile([P, HEADS], F32)
-            nc.vector.reciprocal(exp_rsum[:], exp_sum[:])
             kept[b]["exp_scores"] = exp_scores
+            kept[b]["exp_sum"] = exp_sum
+
+        def invert_sum(b):
+            exp_rsum = ring["exp_rsum"].tile([P, HEADS], F32)
+            nc.vector.reciprocal(exp_rsum[:], kept[b]["exp_sum"][:])
             kept[b]["exp_rsum"] = exp_rsum
 
-        def divide_and_flip(b):
+        def divide(b):
             exp_scores, exp_rsum = kept[b]["exp_scores"], kept[b]["exp_rsum"]
             att = ring["att"].tile([P, HEADS, SLOTS], BF16)
             for t in range(HEADS):
                 nc.scalar.activation(att[:, t, :], exp_scores[:, t, :], FUNC.Copy, scale=exp_rsum[:, t:t + 1])
+            kept[b]["att"] = att
+
+        def flip_att(b):
             att_flipped_ps = psum_ring["att_flipped"].tile([P, HEADS, SLOTS], BF16, tag="att_flipped")
             for t in range(HEADS):
-                nc.tensor.transpose(att_flipped_ps[:, t, :], att[:, t, :], identity_bf16[:])
+                nc.tensor.transpose(att_flipped_ps[:, t, :], kept[b]["att"][:, t, :], identity_bf16[:])
             kept[b]["att_flipped_ps"] = att_flipped_ps
+
+        def copy_att(b):
+            att_flipped = ring["att_flipped"].tile([P, HEADS, SLOTS], BF16)
+            nc.scalar.activation(att_flipped[:], kept[b]["att_flipped_ps"][:], FUNC.Copy)
+            kept[b]["att_flipped"] = att_flipped
 
         def weigh(b):
             q_k_v = q_k_v_of_sample[b]
-            att_flipped = ring["att_flipped"].tile([P, HEADS, SLOTS], BF16)
-            nc.scalar.activation(att_flipped[:], kept[b]["att_flipped_ps"][:], FUNC.Copy)
             o_ps = psum_ring["o"].tile([P, HEADS, SLOTS], F32, tag="o")
             for t in range(HEADS):
-                nc.tensor.matmul(o_ps[:, t, :], q_k_v[:, t, 2, :], att_flipped[:, t, :], start=True, stop=True)
+                nc.tensor.matmul(o_ps[:, t, :], q_k_v[:, t, 2, :], kept[b]["att_flipped"][:, t, :], start=True, stop=True)
             kept[b]["o_ps"] = o_ps
 
-        def add_and_relu(b):
+        def add_residual(b):
             mem1_biased = ring["mem1_biased"].tile([P, HID_BLOCKS, SLOTS], F32)
             nc.vector.tensor_tensor(mem1_biased[:], kept[b]["o_ps"][:], mem[:, :, b * SLOTS:(b + 1) * SLOTS], ALU.add)
+            kept[b]["mem1_biased"] = mem1_biased
+
+        def rectify(b):
             relu_mem1 = ring["relu_mem1"].tile([P, HID_BLOCKS, SLOTS], BF16)
             for hb in range(HID_BLOCKS):
-                nc.scalar.activation(relu_mem1[:, hb, :], mem1_biased[:, hb, :], FUNC.Relu, bias=minus_last_bias[:, hb:hb + 1])
-            kept[b]["mem1_biased"] = mem1_biased
+                nc.scalar.activation(relu_mem1[:, hb, :], kept[b]["mem1_biased"][:, hb, :], FUNC.Relu,
+                                     bias=minus_last_bias[:, hb:hb + 1])
             kept[b]["relu_mem1"] = relu_mem1
 
-        def mlp(b):
-            relu_mem1 = kept[b]["relu_mem1"]
+        def mlp_product(b):
             f_ps = psum_ring["f"].tile([P, HID], F32, tag="f")
             for hb in range(HID_BLOCKS):
-                nc.tensor.matmul(f_ps[:], relu_mem1[:, hb, :], mlp_w_sb[:, hb, :],
+                nc.tensor.matmul(f_ps[:], kept[b]["relu_mem1"][:, hb, :], mlp_w_sb[:, hb, :],
                                  start=(hb == 0), stop=(hb == HID_BLOCKS - 1))
+            kept[b]["f_ps"] = f_ps
+
+        def mlp_moments(b):
             f = ring["f"].tile([P, HID], F32)
-            nc.vector.tensor_tensor(f[:], f_ps[:], mlp_b_sb[:], ALU.add)
+            nc.vector.tensor_tensor(f[:], kept[b]["f_ps"][:], mlp_b_sb[:], ALU.add)
             f_stats = ring["f_stats"].tile([P, 6], F32)
             nc.vector.bn_stats(f_stats[:], f[:])
             f_moments = ring["f_moments"].tile([P, 2], F32)
@@ -376,37 +392,44 @@ def tile_rsaffdecoder_b_kernel(
             kept[b]["f_moments"] = f_moments
             kept[b]["var2"] = var2
 
-        def normalise_mlp(b):
+        def mlp_rstd(b):
             rstd2 = ring["rstd2"].tile([P, 1], F32)
             nc.gpsimd.tensor_tensor(rstd2[:], kept[b]["var2"][:], minus_half[:, 0:1], ALU.pow)
+            kept[b]["rstd2"] = rstd2
+
+        def mlp_normalise(b):
             normed = ring["normed"].tile([P, HID], F32)
-            nc.vector.tensor_scalar(normed[:], kept[b]["f"][:], kept[b]["f_moments"][:, 0:1], rstd2[:],
+            nc.vector.tensor_scalar(normed[:], kept[b]["f"][:], kept[b]["f_moments"][:, 0:1], kept[b]["rstd2"][:],
                                     ALU.subtract, ALU.mult)
             kept[b]["normed"] = normed
 
-        def finish(b):
-            mem1_biased, normed = kept[b]["mem1_biased"], kept[b]["normed"]
+        def flip_back(b):
             normed_flipped = psum_ring["flipped"].tile([P, HID_BLOCKS, SLOTS], F32, tag="flipped")
             for rb in range(HID_BLOCKS):
-                nc.tensor.transpose(normed_flipped[:, rb, :], normed[:, rb * P:(rb + 1) * P], identity_f32[:])
+                nc.tensor.transpose(normed_flipped[:, rb, :], kept[b]["normed"][:, rb * P:(rb + 1) * P], identity_f32[:])
+            kept[b]["normed_flipped"] = normed_flipped
+
+        def finish(b):
             result = ring["result"].tile([P, HID_BLOCKS, SLOTS], F32)
             for rb in range(HID_BLOCKS):
-                nc.vector.scalar_tensor_tensor(result[:, rb, :], normed_flipped[:, rb, :],
+                nc.vector.scalar_tensor_tensor(result[:, rb, :], kept[b]["normed_flipped"][:, rb, :],
                                                late_cols[:, LATE_COL_MLP_LN_W + rb:LATE_COL_MLP_LN_W + rb + 1],
-                                               mem1_biased[:, rb, :],
-                                               ALU.mult, ALU.add)
+                                               kept[b]["mem1_biased"][:, rb, :], ALU.mult, ALU.add)
             nc.sync.dma_start(out_blocks[:, :, b * SLOTS:(b + 1) * SLOTS], result[:])
 
-        stages = (score, exponentiate, divide_and_flip, weigh, add_and_relu, mlp, normalise_mlp, finish)
+        links = (score, find_max, exponentiate, invert_sum, divide, flip_att, copy_att, weigh,
+                 add_residual, rectify, mlp_product, mlp_moments, mlp_rstd, mlp_normalise, flip_back, finish)
+        under_way = len(links) // 2
         complete_mem0(1)
-        for tick in range(-1, N_SAMPLES + len(stages) - 1):
-            for lag in reversed(range(len(stages))):
-                if lag == 0:
-                    g, s = divmod(tick + 3, PIECE_SAMPLES)
-                    if s == 0 and g < PIECES:
-                        measure(g, psum_ring["scores"], "scores")
-                if 0 <= tick - lag < N_SAMPLES:
-                    stages[lag](tick - lag)
+        for tick in range(-1, N_SAMPLES + under_way - 1):
+            for odd in (0, 1):
+                for lag in reversed(range(under_way)):
+                    if lag == 0 and odd == 0:
+                        g, s = divmod(tick + 3, PIECE_SAMPLES)
+                        if s == 0 and g < PIECES:
+                            measure(g, psum_ring["scores"], "scores")
+                    if 0 <= tick - lag < N_SAMPLES:
+                        links[2 * lag + odd](tick - lag)
             if tick + 1 < N_SAMPLES:
                 normalise(tick + 1)
             g, s = divmod(tick + 5, PIECE_SAMPLES)

@@ -43,10 +43,10 @@ SUM_SQ = 9
 N_SUMS = 13
 
 SBUF_RINGS = (
-    ("y", 3), ("z", 6), ("centred", 2), ("part_sums", 3), ("squares", 1), ("sample_moments", 3),
-    ("mu_sq", 3), ("var", 3), ("rstd", 3), ("exp_scores", 3), ("att", 3), ("att_flipped", 3), ("mem1_biased", 5),
-    ("relu_mem1", 3), ("f", 3), ("normed", 3), ("result", 3), ("minus_max", 3), ("exp_sum", 3),
-    ("exp_rsum", 3), ("f_stats", 3), ("f_moments", 3), ("var2", 3), ("rstd2", 3),
+    ("y", 3), ("z", 8), ("centred", 1), ("part_sums", 3), ("squares", 1), ("sample_moments", 3),
+    ("mu_sq", 3), ("var", 3), ("rstd", 3), ("exp_scores", 3), ("att", 3), ("att_flipped", 3), ("mem1_biased", 8),
+    ("relu_mem1", 3), ("f", 3), ("normed", 3), ("result", 2), ("minus_max", 3), ("exp_sum", 3),
+    ("exp_rsum", 3), ("f_stats", 3), ("f_moments", 4), ("var2", 3), ("rstd2", 3),
 )
 PSUM_RINGS = (("bank", 3), ("scores", 1), ("att_flipped", 1), ("o", 1), ("f", 1), ("flipped", 1))
 
@@ -417,19 +417,21 @@ def tile_rsaffdecoder_b_kernel(
                                                kept[b]["mem1_biased"][:, rb, :], ALU.mult, ALU.add)
             nc.sync.dma_start(out_blocks[:, :, b * SLOTS:(b + 1) * SLOTS], result[:])
 
-        links = (score, find_max, exponentiate, invert_sum, divide, flip_att, copy_att, weigh,
-                 add_residual, rectify, mlp_product, mlp_moments, mlp_rstd, mlp_normalise, flip_back, finish)
-        under_way = len(links) // 2
+        def score_and_max(b):
+            score(b)
+            find_max(b)
+
+        stages = (score_and_max, exponentiate, invert_sum, divide, flip_att, copy_att, weigh, add_residual, rectify,
+                  mlp_product, mlp_moments, mlp_rstd, mlp_normalise, flip_back, finish)
         complete_mem0(1)
-        for tick in range(-1, N_SAMPLES + under_way - 1):
-            for odd in (0, 1):
-                for lag in reversed(range(under_way)):
-                    if lag == 0 and odd == 0:
-                        g, s = divmod(tick + 3, PIECE_SAMPLES)
-                        if s == 0 and g < PIECES:
-                            measure(g, psum_ring["scores"], "scores")
-                    if 0 <= tick - lag < N_SAMPLES:
-                        links[2 * lag + odd](tick - lag)
+        for tick in range(-1, N_SAMPLES + len(stages) - 1):
+            for lag in reversed(range(len(stages))):
+                if lag == 0:
+                    g, s = divmod(tick + 3, PIECE_SAMPLES)
+                    if s == 0 and g < PIECES:
+                        measure(g, psum_ring["scores"], "scores")
+                if 0 <= tick - lag < N_SAMPLES:
+                    stages[lag](tick - lag)
             if tick + 1 < N_SAMPLES:
                 normalise(tick + 1)
             g, s = divmod(tick + 5, PIECE_SAMPLES)

@@ -350,7 +350,7 @@ def tile_rsaffdecoder_b_kernel(
 
         def copy_att(b):
             att_flipped = ring["att_flipped"].tile([P, HEADS, SLOTS], BF16)
-            nc.scalar.activation(att_flipped[:], kept[b]["att_flipped_ps"][:], FUNC.Copy)
+            nc.scalar.copy(att_flipped[:], kept[b]["att_flipped_ps"][:])
             kept[b]["att_flipped"] = att_flipped
 
         def weigh(b):

@@ -9,6 +9,7 @@ U16 = mybir.dt.uint16
 FUNC = mybir.ActivationFunctionType
 ALU = mybir.AluOpType
 AXIS_X = mybir.AxisListType.X
+AXIS_XY = mybir.AxisListType.XY
 
 P = 128
 TABLE_COLS = 4096
@@ -27,28 +28,32 @@ LOOKUP_SAMPLES = LOOKUP // SLOTS
 PIECE = 256
 PIECES = N_TOK // PIECE
 PIECE_SAMPLES = PIECE // SLOTS
+PARTS = PIECE_SAMPLES + HEADS
+NORMALISE_LEAD = 1
+MEASURE_LEAD = 3
+PROJECT_LEAD = 5
+QUADRANT = 32
 EPS = 1e-5
 Q_SCALE = 128.0 ** -0.5
 
-COL_W_DIST = 0
-COL_PRE_B = 4
-COL_MLP_LN_B = 8
-N_COLS = 12
+COL_PRE_B = 0
+COL_MLP_LN_B = 4
+N_COLS = 8
 LATE_COL_MLP_LN_W = 0
 LATE_COL_QKV_B = 4
 N_LATE_COLS = 16
 
 SUM_V = 8
-SUM_SQ = 9
-N_SUMS = 13
+SUM_EPS = 9
+N_SUMS = 10
 
 SBUF_RINGS = (
-    ("y", 3), ("z", 8), ("centred", 1), ("part_sums", 3), ("squares", 1), ("sample_moments", 3),
-    ("mu_sq", 3), ("var", 3), ("rstd", 3), ("exp_scores", 3), ("att", 3), ("att_flipped", 3), ("mem1_biased", 8),
+    ("scaled", 3), ("z", 8), ("squares", 2), ("var_eps", 3), ("rstd", 3), ("exp_scores", 3), ("att", 3), ("att_flipped", 3), ("mem1_biased", 8),
     ("relu_mem1", 3), ("f", 3), ("normed", 3), ("result", 2), ("minus_max", 3), ("exp_sum", 3),
-    ("exp_rsum", 3), ("f_stats", 3), ("f_moments", 4), ("var2", 3), ("rstd2", 3),
+    ("exp_rsum", 3), ("f_sum", 3), ("minus_mu2", 4), ("f_squares", 2),
+    ("f_square_sum", 3), ("var2", 3), ("rstd2", 3),
 )
-PSUM_RINGS = (("bank", 3), ("scores", 1), ("att_flipped", 1), ("o", 1), ("f", 1), ("flipped", 1))
+PSUM_RINGS = (("bank", 4), ("scores", 1), ("short", 3))
 
 FLOPS = 2 * (128 + 256) * HID * N_TOK + 2 * 256 * HID * N_SAMPLES + 2 * HID * PROJ * N_TOK \
     + 2 * 2 * HEADS * N_SAMPLES * SLOTS * SLOTS * P + 2 * HID * HID * N_TOK
@@ -61,250 +66,328 @@ def tile_rsaffdecoder_b_kernel(
     nc = tc.nc
     with ExitStack() as ctx:
         held = ctx.enter_context(tc.tile_pool(name="held", bufs=1))
-        ring = {kind: ctx.enter_context(tc.tile_pool(name=kind, bufs=bufs)) for kind, bufs in SBUF_RINGS}
-
         identity_f32 = held.tile([P, P], F32)
         make_identity(nc, identity_f32[:])
         identity_bf16 = held.tile([P, P], BF16)
         nc.vector.tensor_copy(identity_bf16[:], identity_f32[:])
 
-        def as_rows(vector):
-            return vector.rearrange("(k p) o -> k (p o)", p=P)
+        def split(pool, engine, value, shape, name):
+            terms = []
+            for k in range(3):
+                term = pool.tile(shape, BF16, name=f"{name}_term{k}")
+                engine.tensor_copy(term[:], value[:])
+                terms.append(term)
+                if k < 2:
+                    rest = pool.tile(shape, F32, name=f"{name}_rest{k}")
+                    engine.tensor_tensor(rest[:], value[:], term[:], ALU.subtract)
+                    value = rest
+            return terms
 
-        rows = held.tile([P, P], F32)
-        nc.vector.memset(rows[:], 0.0)
-        late_rows = held.tile([P, P], F32)
-        nc.vector.memset(late_rows[:], 0.0)
+        psum_ring = {kind: ctx.enter_context(tc.psum_pool(name="psum_" + kind, bufs=bufs)) for kind, bufs in PSUM_RINGS}
+        bank = psum_ring["bank"]
 
-        table_sb = held.tile([P, TABLE_COLS], BF16)
-        nc.scalar.dma_start(table_sb[:], table)
-        edist = held.tile([P, N_TOK], F32)
-        distance_row = distances.rearrange("o n -> (o n)")
-        nc.scalar.dma_start(edist[:, 0:LOOKUP], distance_row[0:LOOKUP].partition_broadcast(P))
-        nc.scalar.dma_start(rows[COL_W_DIST:COL_W_DIST + HID_BLOCKS, :], as_rows(w_dist))
-        nc.scalar.dma_start(rows[COL_PRE_B:COL_PRE_B + HID_BLOCKS, :], as_rows(pre_b))
-        nc.scalar.dma_start(rows[COL_MLP_LN_B:COL_MLP_LN_B + HID_BLOCKS, :], as_rows(mlp_ln_b))
+        with tc.tile_pool(name="setup", bufs=1) as setup:
+            def as_rows(vector):
+                return vector.rearrange("(k p) o -> k (p o)", p=P)
 
-        w_emb_sb = held.tile([P, EMB_BLOCKS, HID], BF16)
-        nc.sync.dma_start(w_emb_sb[:], w_emb.rearrange("(k p) h -> p k h", p=P))
-        emb_sb = held.tile([P, EMB_BLOCKS, N_TOK], BF16)
-        emb_blocks = emb.rearrange("(k p) n -> p k n", p=P)
-        nc.sync.dma_start(emb_sb[:, :, 0:LOOKUP], emb_blocks[:, :, 0:LOOKUP])
-        offsets = held.tile([P, N_TOK // 16], U16, name="offsets")
-        nc.sync.dma_start(offsets[:], offs)
-        w_lab_sb = held.tile([P, HID], BF16)
-        nc.sync.dma_start(w_lab_sb[:], w_lab)
-        w_qry_sb = held.tile([P, EMB_BLOCKS, HID], BF16)
-        nc.sync.dma_start(w_qry_sb[:], w_qry.rearrange("(k p) h -> p k h", p=P))
-        query_sb = held.tile([P, EMB_BLOCKS, N_SAMPLES], BF16)
-        nc.sync.dma_start(query_sb[:], query.rearrange("(k p) b -> p k b", p=P))
-        nc.sync.dma_start(edist[:, LOOKUP:N_TOK], distance_row[LOOKUP:N_TOK].partition_broadcast(P))
-        qkv_w_sb = held.tile([P, HID_BLOCKS, PROJ], BF16)
-        nc.sync.dma_start(qkv_w_sb[:], qkv_w.rearrange("(hb p) r -> p hb r", p=P))
-        nc.sync.dma_start(late_rows[LATE_COL_QKV_B:LATE_COL_QKV_B + PROJ // P, :], as_rows(qkv_b))
-        nc.sync.dma_start(late_rows[LATE_COL_MLP_LN_W:LATE_COL_MLP_LN_W + HID_BLOCKS, :], as_rows(mlp_ln_w))
-        qkv_b_sb = held.tile([P, PROJ], F32)
-        nc.sync.dma_start(qkv_b_sb[:], qkv_b.rearrange("r o -> (r o)").partition_broadcast(P))
+            rows = held.tile([P, P], F32)
+            nc.vector.memset(rows[:], 0.0)
+            late_rows = held.tile([P, P], F32)
+            nc.vector.memset(late_rows[:], 0.0)
 
-        ln_gain = held.tile([P, PROJ], F32)
-        nc.gpsimd.dma_start(ln_gain[:].rearrange("p (r n) -> p r n", n=SLOTS),
-                            qkv_ln_w.rearrange("(r p) n -> p r n", p=P))
-        ln_bias = held.tile([P, PROJ], F32)
-        nc.gpsimd.dma_start(ln_bias[:].rearrange("p (r n) -> p r n", n=SLOTS),
-                            qkv_ln_b.rearrange("(r p) n -> p r n", p=P))
-        nc.gpsimd.dma_start(emb_sb[:, :, LOOKUP:N_TOK], emb_blocks[:, :, LOOKUP:N_TOK])
-        mlp_b_sb = held.tile([P, HID], F32)
-        nc.gpsimd.dma_start(mlp_b_sb[:], mlp_b.rearrange("r o -> (r o)").partition_broadcast(P))
-        mlp_w_sb = held.tile([P, HID_BLOCKS, HID], BF16)
-        nc.gpsimd.dma_start(mlp_w_sb[:], mlp_w.rearrange("(hb p) r -> p hb r", p=P))
+            dist = held.tile([P, SLOTS], F32)
+            nc.vector.memset(dist[:], 0.0)
+            nc.sync.dma_start(dist[0:N_SAMPLES, :], distances.rearrange("o (b n) -> (o b) n", n=SLOTS))
+            table_sb = held.tile([P, TABLE_COLS], BF16)
+            nc.scalar.dma_start(table_sb[:], table)
+            w_qry_sb = held.tile([P, EMB_BLOCKS, HID], BF16)
+            nc.scalar.dma_start(w_qry_sb[:], w_qry.rearrange("(k p) h -> p k h", p=P))
+            qkv_w_sb = held.tile([P, HID_BLOCKS, PROJ], BF16)
+            nc.gpsimd.dma_start(qkv_w_sb[:], qkv_w.rearrange("(hb p) r -> p hb r", p=P))
+            ln_gain = held.tile([P, PROJ], F32)
+            nc.gpsimd.dma_start(ln_gain[:].rearrange("p (r n) -> p r n", n=SLOTS),
+                                qkv_ln_w.rearrange("(r p) n -> p r n", p=P))
 
-        spread_mean = held.tile([P, P], F32)
-        nc.vector.memset(spread_mean[:], 1.0 / (P * PROJ))
-        minus_half = held.tile([P, PIECE_SAMPLES], F32)
-        nc.vector.memset(minus_half[:], -0.5)
-        scratch = held.tile([P, 1], F32)
-        nc.vector.memset(scratch[:], 0.0)
-        nc.scalar.activation(scratch[:], scratch[:], FUNC.Exp)
+            w_dist_row = setup.tile([P, HID], F32)
+            nc.sync.dma_start(w_dist_row[:], w_dist.rearrange("h o -> (h o)").partition_broadcast(P))
+            w_emb_sb = held.tile([P, EMB_BLOCKS, HID], BF16)
+            nc.sync.dma_start(w_emb_sb[:], w_emb.rearrange("(k p) h -> p k h", p=P))
+            emb_sb = [held.tile([P, EMB_BLOCKS, LOOKUP], BF16, name=f"emb{u}") for u in range(LOOKUPS)]
+            emb_blocks = emb.rearrange("(k p) n -> p k n", p=P)
+            nc.sync.dma_start(emb_sb[0][:], emb_blocks[:, :, 0:LOOKUP])
+            v_bias = setup.tile([P, HEADS, P], F32)
+            nc.sync.dma_start(v_bias[:], qkv_b.rearrange("(t c u) o -> t c (u o)", c=3, u=P)[:, 2, :].partition_broadcast(P))
+            offsets = held.tile([P, N_TOK // 16], U16, name="offsets")
+            nc.sync.dma_start(offsets[:], offs)
+            w_lab_sb = held.tile([P, HID], BF16)
+            nc.sync.dma_start(w_lab_sb[:], w_lab)
+            query_sb = held.tile([P, EMB_BLOCKS, N_SAMPLES], BF16)
+            nc.sync.dma_start(query_sb[:], query.rearrange("(k p) b -> p k b", p=P))
+            nc.sync.dma_start(rows[COL_PRE_B:COL_PRE_B + HID_BLOCKS, :], as_rows(pre_b))
+            nc.sync.dma_start(rows[COL_MLP_LN_B:COL_MLP_LN_B + HID_BLOCKS, :], as_rows(mlp_ln_b))
+            nc.sync.dma_start(emb_sb[1][:], emb_blocks[:, :, LOOKUP:2 * LOOKUP])
+            nc.sync.dma_start(late_rows[LATE_COL_QKV_B:LATE_COL_QKV_B + PROJ // P, :], as_rows(qkv_b))
+            nc.sync.dma_start(late_rows[LATE_COL_MLP_LN_W:LATE_COL_MLP_LN_W + HID_BLOCKS, :], as_rows(mlp_ln_w))
 
-        mem = held.tile([P, HID_BLOCKS, N_TOK], F32)
-        mem0_bf16 = held.tile([P, HID_BLOCKS, N_TOK], BF16)
+            ln_bias = held.tile([P, PROJ], F32)
+            nc.gpsimd.dma_start(ln_bias[:].rearrange("p (r n) -> p r n", n=SLOTS),
+                                qkv_ln_b.rearrange("(r p) n -> p r n", p=P))
+            for u in (2, 3):
+                nc.gpsimd.dma_start(emb_sb[u][:], emb_blocks[:, :, u * LOOKUP:(u + 1) * LOOKUP])
+            mlp_b_sb = held.tile([P, HID], F32)
+            nc.gpsimd.dma_start(mlp_b_sb[:], mlp_b.rearrange("r o -> (r o)").partition_broadcast(P))
+            mlp_w_sb = held.tile([P, HID_BLOCKS, HID], BF16)
+            nc.gpsimd.dma_start(mlp_w_sb[:], mlp_w.rearrange("(hb p) r -> p hb r", p=P))
+
+            spread_mean = held.tile([P, P], F32)
+            nc.vector.memset(spread_mean[:], 1.0 / (P * PROJ))
+            spread_bias = held.tile([P, P], F32)
+            nc.vector.memset(spread_bias[:], 1.0 / PROJ)
+            ones = held.tile([P, P], F32)
+            nc.vector.memset(ones[:], 1.0)
+            minus_half = held.tile([P, PIECE_SAMPLES], F32)
+            nc.vector.memset(minus_half[:], -0.5)
+
+            repeat_rows = held.tile([P, P], F32)
+            nc.vector.tensor_copy(repeat_rows[:].rearrange("p (g b) -> p g b", b=N_SAMPLES),
+                                  identity_f32[:, 0:N_SAMPLES].unsqueeze(1).to_broadcast([P, P // N_SAMPLES, N_SAMPLES]))
+            dist_ps = psum_ring["short"].tile([P, SLOTS], F32, tag="short")
+            nc.tensor.matmul(dist_ps[:], repeat_rows[:], dist[:], start=True, stop=True)
+            d_min = setup.tile([P, 1], F32)
+            nc.vector.tensor_reduce(d_min[:], dist_ps[:], AXIS_X, ALU.min)
+            e_dist = setup.tile([P, SLOTS], F32)
+            d_sum = setup.tile([P, 1], F32)
+            nc.scalar.activation(e_dist[:], dist_ps[:], FUNC.Exp, bias=d_min[:], scale=-1.0, accum_out=d_sum[:])
+            d_rsum = setup.tile([P, 1], F32)
+            nc.vector.reciprocal(d_rsum[:], d_sum[:])
+            d = setup.tile([P, SLOTS], F32)
+            nc.vector.tensor_scalar_mul(d[:], e_dist[:], d_rsum[:])
+            d_terms = split(setup, nc.vector, d, [P, SLOTS], "d")
+            d_of_row = held.tile([P, SLOTS], BF16)
+            for q, k in enumerate((0, 1, 2, 0)):
+                quadrant = slice(QUADRANT * q, QUADRANT * (q + 1))
+                nc.vector.tensor_copy(d_of_row[quadrant, :], d_terms[k][quadrant, :])
+            sample_of_row = held.tile([P, N_SAMPLES], BF16)
+            with nc.allow_low_precision(reason="each sum has one term that is not 0"):
+                nc.vector.tensor_reduce(sample_of_row[:], identity_f32[:].rearrange("p (g b) -> p b g", b=N_SAMPLES),
+                                        AXIS_X, ALU.add)
+            d_rows = [held.tile([P, LOOKUP_SAMPLES, SLOTS], BF16, name=f"d_rows{u}") for u in range(LOOKUPS)]
+            for u in range(LOOKUPS):
+                group = slice(u * LOOKUP_SAMPLES, (u + 1) * LOOKUP_SAMPLES)
+                shape = [P, LOOKUP_SAMPLES, SLOTS]
+                nc.vector.tensor_tensor(d_rows[u][:], sample_of_row[:, group].unsqueeze(2).to_broadcast(shape),
+                                        d_of_row[:].unsqueeze(1).to_broadcast(shape), ALU.mult)
+
+            halves = identity_f32[:].rearrange("p (q h b) -> p q h b", h=2, b=N_SAMPLES)
+            term_of_row = setup.tile([P, 3], F32)
+            nc.vector.tensor_reduce(term_of_row[:, 0:1], halves[:, 0:3, 0, :], AXIS_XY, ALU.add)
+            nc.vector.tensor_reduce(term_of_row[:, 1:2], halves[:, 0:2, 1, :], AXIS_XY, ALU.add)
+            nc.vector.tensor_reduce(term_of_row[:, 2:3], halves[:, 3, 0, :], AXIS_X, ALU.add)
+            w_dist_rows = held.tile([P, HID], BF16)
+            w_terms = split(setup, nc.vector, w_dist_row, [P, HID], "w_dist")
+            w_first = setup.tile([P, HID], BF16)
+            w_second = setup.tile([P, HID], BF16)
+            nc.vector.tensor_scalar_mul(w_first[:], w_terms[0][:], term_of_row[:, 0:1])
+            nc.vector.scalar_tensor_tensor(w_second[:], w_terms[1][:], term_of_row[:, 1:2], w_first[:], ALU.mult, ALU.add)
+            nc.vector.scalar_tensor_tensor(w_dist_rows[:], w_terms[2][:], term_of_row[:, 2:3], w_second[:], ALU.mult, ALU.add)
+
+            pick_rows = held.tile([P, P], BF16)
+            nc.vector.memset(pick_rows[:], 0.0)
+            v_bias_rows = held.tile([P, HEADS, P], BF16)
+            nc.vector.memset(v_bias_rows[:], 0.0)
+            for k, term in enumerate(split(setup, nc.vector, v_bias, [P, HEADS, P], "v_bias")):
+                quadrant = slice(QUADRANT * k, QUADRANT * (k + 1))
+                nc.vector.memset(pick_rows[QUADRANT * k:QUADRANT * k + 1, :], 1.0)
+                nc.vector.tensor_copy(v_bias_rows[quadrant, :, :], term[quadrant, :, :])
+
+        ring = {kind: ctx.enter_context(tc.tile_pool(name=kind, bufs=bufs)) for kind, bufs in SBUF_RINGS}
+
+        mem = [held.tile([P, HID_BLOCKS, LOOKUP], F32, name=f"mem{u}") for u in range(LOOKUPS)]
+        mem0_bf16 = [held.tile([P, HID_BLOCKS, LOOKUP], BF16, name=f"mem0_bf16_{u}") for u in range(LOOKUPS)]
+        mem_sums = held.tile([P, HID_BLOCKS, N_SAMPLES], F32)
         cols = held.tile([P, N_COLS], F32)
         late_cols = held.tile([P, N_LATE_COLS], F32)
         minus_last_bias = held.tile([P, HID_BLOCKS], F32)
         query_term = held.tile([P, HID_BLOCKS, N_SAMPLES], F32)
-        dist_min = held.tile([P, N_SAMPLES], F32)
-        edist_sum = held.tile([P, N_SAMPLES], F32)
-        edist_rsum = held.tile([P, N_SAMPLES], F32)
 
-        def soften(u):
-            group = slice(u * LOOKUP_SAMPLES, (u + 1) * LOOKUP_SAMPLES)
-            samples = [(b, slice(b * SLOTS, (b + 1) * SLOTS)) for b in range(group.start, group.stop)]
-            nc.vector.tensor_reduce(dist_min[:, group],
-                                    edist[:, u * LOOKUP:(u + 1) * LOOKUP].rearrange("p (b n) -> p b n", n=SLOTS),
-                                    AXIS_X, ALU.min)
-            for b, sample in samples:
-                nc.scalar.activation(edist[:, sample], edist[:, sample], FUNC.Exp, bias=dist_min[:, b:b + 1],
-                                     scale=-1.0, accum_out=edist_sum[:, b:b + 1])
-            nc.vector.reciprocal(edist_rsum[:, group], edist_sum[:, group])
-            for b, sample in samples:
-                nc.scalar.activation(edist[:, sample], edist[:, sample], FUNC.Copy, scale=edist_rsum[:, b:b + 1])
-
-        def emb_product(u, hb, banks):
-            emb_ps = banks.tile([P, LOOKUP], F32, tag="bank")
+        def open_mem(u, hb, kind):
+            mem_ps = psum_ring[kind].tile([P, LOOKUP], F32, tag=kind)
             for kb in range(EMB_BLOCKS):
-                nc.tensor.matmul(emb_ps[:], w_emb_sb[:, kb, hb * P:(hb + 1) * P],
-                                 emb_sb[:, kb, u * LOOKUP:(u + 1) * LOOKUP],
-                                 start=(kb == 0), stop=(kb == EMB_BLOCKS - 1))
-            return emb_ps
+                nc.tensor.matmul(mem_ps[:], w_emb_sb[:, kb, hb * P:(hb + 1) * P], emb_sb[u][:, kb, :],
+                                 start=(kb == 0), stop=False)
+            return mem_ps
 
-        def label_product(u, hb, banks):
-            label_ps = banks.tile([P, LOOKUP], F32, tag="bank")
-            nc.tensor.matmul(label_ps[:], w_lab_sb[:, hb * P:(hb + 1) * P],
+        def add_dist(u, hb, mem_ps):
+            nc.tensor.matmul(mem_ps[:], w_dist_rows[:, hb * P:(hb + 1) * P], d_rows[u][:].rearrange("p b n -> p (b n)"),
+                             start=False, stop=False)
+
+        def close_mem(u, hb, mem_ps):
+            nc.tensor.matmul(mem_ps[:], w_lab_sb[:, hb * P:(hb + 1) * P],
                              table_sb[:].indirect(offsets[:, u * (LOOKUP // 16):(u + 1) * (LOOKUP // 16)]),
-                             start=True, stop=True)
-            return label_ps
-
-        def start_mem(u, hb, product_ps):
-            lookup = slice(u * LOOKUP, (u + 1) * LOOKUP)
-            nc.vector.scalar_tensor_tensor(mem[:, hb, lookup], edist[:, lookup],
-                                           cols[:, COL_W_DIST + hb:COL_W_DIST + hb + 1], product_ps[:],
-                                           ALU.mult, ALU.add)
-
-        def finish_mem(u, hb, product_ps):
+                             start=False, stop=True)
             for k in range(LOOKUP_SAMPLES):
                 b = u * LOOKUP_SAMPLES + k
-                sample = slice(b * SLOTS, (b + 1) * SLOTS)
-                nc.vector.scalar_tensor_tensor(mem[:, hb, sample], product_ps[:, k * SLOTS:(k + 1) * SLOTS],
-                                               query_term[:, hb, b:b + 1], mem[:, hb, sample], ALU.add, ALU.add)
+                sample = slice(k * SLOTS, (k + 1) * SLOTS)
+                nc.scalar.activation(mem[u][:, hb, sample], mem_ps[:, sample],
+                                     FUNC.Identity, bias=query_term[:, hb, b:b + 1], accum_out=mem_sums[:, hb, b:b + 1])
+            nc.vector.tensor_scalar_add(mem0_bf16[u][:, hb, :], mem[u][:, hb, :], minus_last_bias[:, hb:hb + 1])
 
-        def round_mem0(u):
-            lookup = slice(u * LOOKUP, (u + 1) * LOOKUP)
+        def sum_weights():
+            half = HID_BLOCKS // 2
+            w_copy = held.tile([P, PROJ], BF16)
+            for hb in range(half):
+                nc.scalar.activation(w_copy[:], qkv_w_sb[:, hb, :], FUNC.Copy, accum_out=w_sums[:, hb:hb + 1])
+            nc.vector.tensor_reduce(w_sums[:, half:HID_BLOCKS], qkv_w_sb[:, half:HID_BLOCKS, :], AXIS_X, ALU.add)
             for hb in range(HID_BLOCKS):
-                nc.scalar.activation(mem0_bf16[:, hb, lookup], mem[:, hb, lookup], FUNC.Identity,
-                                     bias=minus_last_bias[:, hb:hb + 1])
+                nc.vector.tensor_scalar(mean_weights[:, hb, :], ones[:], w_sums[:, hb:hb + 1], 1.0 / (P * PROJ),
+                                        ALU.mult, ALU.mult)
 
-        out_blocks = out.rearrange("(rb p) n -> p rb n", p=P)
-        y_of_piece = {}
+        def centre_bias():
+            qkv_b_cols = late_cols[:, LATE_COL_QKV_B:LATE_COL_QKV_B + PROJ // P]
+            bias_sum = held.tile([P, 2], F32)
+            nc.vector.tensor_reduce(bias_sum[:, 0:1], qkv_b_cols, AXIS_X, ALU.add)
+            extra = held.tile([P, HID_BLOCKS], F32)
+            nc.vector.tensor_tensor(extra[:], w_sums[:], minus_last_bias[:], ALU.mult)
+            nc.vector.tensor_reduce(bias_sum[:, 1:2], extra[:], AXIS_X, ALU.add)
+            bias_ps = bank.tile([P, 2], F32, tag="bank")
+            nc.tensor.matmul(bias_ps[:], spread_bias[:], bias_sum[:], start=True, stop=True)
+            bias_mean = held.tile([P, 1], F32)
+            nc.vector.tensor_reduce(bias_mean[:], bias_ps[:], AXIS_X, ALU.add)
+            nc.vector.memset(centred_bias[:], 0.0)
+            by_kind = centred_bias[:].rearrange("p (t c) -> p t c", c=3)
+            nc.vector.tensor_copy(by_kind[:, :, 0:2], qkv_b_cols.rearrange("p (t c) -> p t c", c=3)[:, :, 0:2])
+            nc.vector.tensor_scalar(centred_bias[:], centred_bias[:], bias_mean[:], None, ALU.subtract)
+
+        def find_mean(u):
+            group = slice(u * LOOKUP_SAMPLES, (u + 1) * LOOKUP_SAMPLES)
+            mean_ps = bank.tile([P, LOOKUP_SAMPLES], F32, tag="bank")
+            for hb in range(HID_BLOCKS):
+                nc.tensor.matmul(mean_ps[:], mean_weights[:, hb, :], mem_sums[:, hb, group],
+                                 start=(hb == 0), stop=(hb == HID_BLOCKS - 1))
+            shape = [P, LOOKUP_SAMPLES, PROJ // P]
+            nc.vector.tensor_tensor(shift[:, group, :], centred_bias[:].unsqueeze(1).to_broadcast(shape),
+                                    mean_ps[:].unsqueeze(2).to_broadcast(shape), ALU.subtract)
+
+        w_sums = held.tile([P, HID_BLOCKS], F32)
+        mean_weights = held.tile([P, HID_BLOCKS, P], F32)
+        centred_bias = held.tile([P, PROJ // P], F32)
+        shift = held.tile([P, N_SAMPLES, PROJ // P], F32)
+        square_sums = held.tile([P, N_SAMPLES, N_SUMS], F32)
+        nc.vector.memset(square_sums[:], EPS * PROJ)
+        scaled_of_piece = {}
         q_k_v_of_sample = {}
-        mu_rstd_of_piece = {}
-        sums_of_piece = {}
+        rstd_of_piece = {}
 
-        def project(g, banks):
-            piece = slice(g * PIECE, (g + 1) * PIECE)
-            y = ring["y"].tile([P, PIECE_SAMPLES, PROJ], F32)
-            y_of_piece[g] = y
-            part_sums = ring["part_sums"].tile([P, PIECE_SAMPLES, N_SUMS], F32)
-            sums_of_piece[g] = part_sums
-            v_bias = qkv_b_sb[:].rearrange("p (t c u) -> p t c u", c=3, u=P)[:, :, 2, :]
-            v_weights = qkv_w_sb[:].rearrange("p hb (t c u) -> p hb t c u", c=3, u=P)[:, :, :, 2, :]
-            for s in range(PIECE_SAMPLES):
-                b = g * PIECE_SAMPLES + s
-                v_ps = banks.tile([P, HEADS, P], F32, tag="bank")
+        gain_by_kind = ln_gain[:].rearrange("p (t c n) -> p t c n", c=3, n=SLOTS)
+        v_weights = qkv_w_sb[:].rearrange("p hb (t c u) -> p hb t c u", c=3, u=P)[:, :, :, 2, :]
+
+        def start_piece(g):
+            scaled = ring["scaled"].tile([P, PIECE_SAMPLES, PROJ], F32)
+            scaled_of_piece[g] = scaled
+
+        def project_v(g, s):
+            u, start = divmod(g * PIECE, LOOKUP)
+            b = g * PIECE_SAMPLES + s
+            v_shift = shift[:, b, 2:3]
+            v_ps = bank.tile([P, HEADS, P], F32, tag="bank")
+            for hb in range(HID_BLOCKS):
+                nc.tensor.matmul(v_ps[:], mem0_bf16[u][:, hb, start + s * SLOTS:start + (s + 1) * SLOTS], v_weights[:, hb, :, :],
+                                 start=(hb == 0), stop=False)
+            nc.tensor.matmul(v_ps[:], pick_rows[:], v_bias_rows[:], start=False, stop=True)
+            nc.vector.scalar_tensor_tensor(scaled_of_piece[g][:, s, :].rearrange("p (t c u) -> p t c u", c=3, u=P)[:, :, 2, :],
+                                           v_ps[:], v_shift, gain_by_kind[:, :, 2, :], ALU.add, ALU.mult)
+            squares = ring["squares"].tile([P, HEADS, P], BF16)
+            nc.scalar.activation(squares[:], v_ps[:], FUNC.Square, bias=v_shift,
+                                 accum_out=square_sums[:, b, SUM_V:SUM_V + 1])
+
+        def project_qk(g, t):
+            u, start = divmod(g * PIECE, LOOKUP)
+            qk_ps = bank.tile([P, 2, PIECE_SAMPLES, SLOTS], F32, tag="bank")
+            for c in range(2):
+                r = 3 * t + c
                 for hb in range(HID_BLOCKS):
-                    nc.tensor.matmul(v_ps[:], mem0_bf16[:, hb, b * SLOTS:(b + 1) * SLOTS], v_weights[:, hb, :, :],
-                                     start=(hb == 0), stop=(hb == HID_BLOCKS - 1))
-                nc.vector.scalar_tensor_tensor(y[:, s, :].rearrange("p (t c u) -> p t c u", c=3, u=P)[:, :, 2, :],
-                                               v_ps[:], 1.0, v_bias, ALU.mult, ALU.add,
-                                               accum_out=part_sums[:, s, SUM_V:SUM_V + 1])
-            for t in range(HEADS):
-                qk_ps = banks.tile([P, 2, PIECE_SAMPLES, SLOTS], F32, tag="bank")
-                for c in range(2):
-                    r = 3 * t + c
-                    for hb in range(HID_BLOCKS):
-                        nc.tensor.matmul(qk_ps[:, c, :, :].rearrange("p s n -> p (s n)"),
-                                         qkv_w_sb[:, hb, r * P:(r + 1) * P],
-                                         mem0_bf16[:, hb, piece], start=(hb == 0), stop=(hb == HID_BLOCKS - 1))
-                for c in range(2):
-                    r = 3 * t + c
-                    for s in range(PIECE_SAMPLES):
-                        nc.scalar.activation(y[:, s, r * P:(r + 1) * P], qk_ps[:, c, s, :], FUNC.Identity,
-                                             bias=late_cols[:, LATE_COL_QKV_B + r:LATE_COL_QKV_B + r + 1],
-                                             accum_out=part_sums[:, s, 2 * t + c:2 * t + c + 1])
-                for s in range(PIECE_SAMPLES):
-                    squares = ring["squares"].tile([P, HEAD_ROWS], BF16)
-                    nc.scalar.activation(squares[:], y[:, s, t * HEAD_ROWS:(t + 1) * HEAD_ROWS], FUNC.Square,
-                                         accum_out=part_sums[:, s, SUM_SQ + t:SUM_SQ + t + 1])
+                    nc.tensor.matmul(qk_ps[:, c, :, :].rearrange("p s n -> p (s n)"),
+                                     qkv_w_sb[:, hb, r * P:(r + 1) * P],
+                                     mem0_bf16[u][:, hb, start:start + PIECE], start=(hb == 0), stop=(hb == HID_BLOCKS - 1))
+            blocks = [(c, s, 3 * t + c, g * PIECE_SAMPLES + s) for c in range(2) for s in range(PIECE_SAMPLES)]
+            for c, s, r, b in blocks:
+                nc.vector.scalar_tensor_tensor(scaled_of_piece[g][:, s, r * P:(r + 1) * P], qk_ps[:, c, s, :],
+                                               shift[:, b, r:r + 1], ln_gain[:, r * P:(r + 1) * P],
+                                               ALU.add, ALU.mult)
+            for c, s, r, b in blocks:
+                squares = ring["squares"].tile([P, HEADS, P], BF16)
+                nc.scalar.activation(squares[:, 0, :], qk_ps[:, c, s, :], FUNC.Square, bias=shift[:, b, r:r + 1],
+                                     accum_out=square_sums[:, b, 2 * t + c:2 * t + c + 1])
 
-        def measure(g, banks, tag):
-            part_sums = sums_of_piece[g]
-            sample_ps = banks.tile([P, PIECE_SAMPLES, N_SUMS], F32, tag=tag)
+        def project_part(g, part):
+            if part == 0:
+                start_piece(g)
+            if part < PIECE_SAMPLES:
+                project_v(g, part)
+            else:
+                project_qk(g, part - PIECE_SAMPLES)
+
+        def measure(g):
+            samples = slice(g * PIECE_SAMPLES, (g + 1) * PIECE_SAMPLES)
+            sample_ps = psum_ring["short"].tile([P, PIECE_SAMPLES, N_SUMS], F32, tag="short")
             nc.tensor.matmul(sample_ps[:].rearrange("p s k -> p (s k)"), spread_mean[:],
-                             part_sums[:].rearrange("p s k -> p (s k)"), start=True, stop=True)
-            sample_moments = ring["sample_moments"].tile([P, 2, PIECE_SAMPLES], F32)
-            nc.vector.tensor_reduce(sample_moments[:, 0, :], sample_ps[:, :, 0:SUM_SQ], AXIS_X, ALU.add)
-            nc.vector.tensor_reduce(sample_moments[:, 1, :], sample_ps[:, :, SUM_SQ:N_SUMS], AXIS_X, ALU.add)
-            mu_sq = ring["mu_sq"].tile([P, PIECE_SAMPLES], F32)
-            nc.vector.tensor_tensor(mu_sq[:], sample_moments[:, 0, :], sample_moments[:, 0, :], ALU.mult)
-            var = ring["var"].tile([P, PIECE_SAMPLES], F32)
-            nc.vector.tensor_tensor(var[:], sample_moments[:, 1, :], mu_sq[:], ALU.subtract)
-            nc.vector.tensor_scalar(var[:], var[:], 0.0, EPS, ALU.max, ALU.add)
+                             square_sums[:, samples, :].rearrange("p s k -> p (s k)"), start=True, stop=True)
+            var_eps = ring["var_eps"].tile([P, PIECE_SAMPLES], F32)
+            nc.vector.tensor_reduce(var_eps[:], sample_ps[:], AXIS_X, ALU.add)
             rstd = ring["rstd"].tile([P, PIECE_SAMPLES], F32)
-            nc.gpsimd.tensor_tensor(rstd[:], var[:], minus_half[:], ALU.pow)
-            mu_rstd_of_piece[g] = (sample_moments, rstd)
+            nc.gpsimd.tensor_tensor(rstd[:], var_eps[:], minus_half[:], ALU.pow)
+            rstd_of_piece[g] = rstd
 
-        def flip_v_params(banks):
-            for param in (ln_gain, ln_bias):
-                by_kind = param[:].rearrange("p (t c n) -> p t c n", c=3, n=SLOTS)
-                v_flipped = banks.tile([P, HEADS, P], F32, tag="bank")
-                for t in range(HEADS):
-                    nc.tensor.transpose(v_flipped[:, t, :], by_kind[:, t, 2, :], identity_f32[:])
-                nc.vector.tensor_copy(by_kind[:, :, 2, :], v_flipped[:])
-                nc.vector.tensor_scalar_mul(by_kind[:, :, 0, :], by_kind[:, :, 0, :], Q_SCALE)
+        def prepare_param(param):
+            by_kind = param[:].rearrange("p (t c n) -> p t c n", c=3, n=SLOTS)
+            v_flipped = bank.tile([P, HEADS, P], F32, tag="bank")
+            for t in range(HEADS):
+                nc.tensor.transpose(v_flipped[:, t, :], by_kind[:, t, 2, :], identity_f32[:])
+            nc.vector.tensor_copy(by_kind[:, :, 2, :], v_flipped[:])
+            nc.vector.tensor_scalar_mul(by_kind[:, :, 0, :], by_kind[:, :, 0, :], Q_SCALE)
 
-        with tc.psum_pool(name="head_psum", bufs=8) as head_psum:
-            first_emb_ps = [emb_product(0, hb, head_psum) for hb in range(HID_BLOCKS)]
-            cols_ps = head_psum.tile([P, P], F32, tag="bank")
-            nc.tensor.transpose(cols_ps[:], rows[:], identity_f32[:])
-            nc.vector.tensor_copy(cols[:], cols_ps[:, 0:N_COLS])
-            query_ps = head_psum.tile([P, HID_BLOCKS, N_SAMPLES], F32, tag="bank")
-            for hb in range(HID_BLOCKS):
-                for kb in range(EMB_BLOCKS):
-                    nc.tensor.matmul(query_ps[:, hb, :], w_qry_sb[:, kb, hb * P:(hb + 1) * P], query_sb[:, kb, :],
-                                     start=(kb == 0), stop=(kb == EMB_BLOCKS - 1))
-            last_bias = cols[:, COL_MLP_LN_B:COL_MLP_LN_B + HID_BLOCKS]
-            nc.vector.tensor_scalar_mul(minus_last_bias[:], last_bias, -1.0)
-            both_biases = held.tile([P, HID_BLOCKS], F32)
-            nc.vector.tensor_tensor(both_biases[:], cols[:, COL_PRE_B:COL_PRE_B + HID_BLOCKS], last_bias, ALU.add)
-            nc.vector.tensor_tensor(query_term[:], query_ps[:],
-                                    both_biases[:].unsqueeze(2).to_broadcast([P, HID_BLOCKS, N_SAMPLES]), ALU.add)
-            soften(0)
-            for hb in range(HID_BLOCKS):
-                start_mem(0, hb, first_emb_ps[hb])
-            soften(1)
-            for hb in range(HID_BLOCKS):
-                finish_mem(0, hb, label_product(0, hb, head_psum))
-            for hb in range(HID_BLOCKS):
-                start_mem(1, hb, label_product(1, hb, head_psum))
-            late_cols_ps = head_psum.tile([P, P], F32, tag="bank")
-            nc.tensor.transpose(late_cols_ps[:], late_rows[:], identity_f32[:])
-            nc.vector.tensor_copy(late_cols[:], late_cols_ps[:, 0:N_LATE_COLS])
-            round_mem0(0)
-            project(0, head_psum)
-            for u in (2, 3):
-                soften(u)
+        def make_mem(*lookups):
+            opened = []
+            for u in lookups:
                 for hb in range(HID_BLOCKS):
-                    start_mem(u, hb, label_product(u, hb, head_psum))
-            measure(0, head_psum, "bank")
-            project(1, head_psum)
-            flip_v_params(head_psum)
+                    kind = "bank" if u == 0 else "scores" if hb == 0 else "short"
+                    opened.append((u, hb, open_mem(u, hb, kind)))
+            for u, hb, mem_ps in opened:
+                add_dist(u, hb, mem_ps)
+            for u, hb, mem_ps in opened:
+                close_mem(u, hb, mem_ps)
 
-        psum_ring = {kind: ctx.enter_context(tc.psum_pool(name="psum_" + kind, bufs=bufs)) for kind, bufs in PSUM_RINGS}
-
-        def complete_mem0(u):
-            for hb in range(HID_BLOCKS):
-                finish_mem(u, hb, emb_product(u, hb, psum_ring["bank"]))
-            round_mem0(u)
+        cols_ps = psum_ring["short"].tile([P, P], F32, tag="short")
+        nc.tensor.transpose(cols_ps[:], rows[:], identity_f32[:])
+        nc.vector.tensor_copy(cols[:], cols_ps[:, 0:N_COLS])
+        query_ps = psum_ring["short"].tile([P, HID_BLOCKS, N_SAMPLES], F32, tag="short")
+        for hb in range(HID_BLOCKS):
+            for kb in range(EMB_BLOCKS):
+                nc.tensor.matmul(query_ps[:, hb, :], w_qry_sb[:, kb, hb * P:(hb + 1) * P], query_sb[:, kb, :],
+                                 start=(kb == 0), stop=(kb == EMB_BLOCKS - 1))
+        last_bias = cols[:, COL_MLP_LN_B:COL_MLP_LN_B + HID_BLOCKS]
+        nc.vector.tensor_scalar_mul(minus_last_bias[:], last_bias, -1.0)
+        both_biases = held.tile([P, HID_BLOCKS], F32)
+        nc.vector.tensor_tensor(both_biases[:], cols[:, COL_PRE_B:COL_PRE_B + HID_BLOCKS], last_bias, ALU.add)
+        nc.vector.tensor_tensor(query_term[:], query_ps[:],
+                                both_biases[:].unsqueeze(2).to_broadcast([P, HID_BLOCKS, N_SAMPLES]), ALU.add)
+        make_mem(0, 1)
+        late_cols_ps = bank.tile([P, P], F32, tag="bank")
+        nc.tensor.transpose(late_cols_ps[:], late_rows[:], identity_f32[:])
+        nc.vector.tensor_copy(late_cols[:], late_cols_ps[:, 0:N_LATE_COLS])
+        sum_weights()
+        centre_bias()
+        find_mean(0)
+        prepare_param(ln_gain)
+        find_mean(1)
+        prepare_param(ln_bias)
 
         def normalise(b):
             g, s = divmod(b, PIECE_SAMPLES)
-            y = y_of_piece[g]
-            sample_moments, rstd = mu_rstd_of_piece[g]
             z = ring["z"].tile([P, PROJ], BF16)
             q_k_v_of_sample[b] = z[:].rearrange("p (t c n) -> p t c n", c=3, n=P)
-            centred = ring["centred"].tile([P, PROJ], F32)
-            nc.vector.scalar_tensor_tensor(centred[:], y[:, s, :], sample_moments[:, 0, s:s + 1], ln_gain[:],
-                                           ALU.subtract, ALU.mult)
-            nc.vector.scalar_tensor_tensor(z[:], centred[:], rstd[:, s:s + 1], ln_bias[:], ALU.mult, ALU.add)
+            nc.vector.scalar_tensor_tensor(z[:], scaled_of_piece[g][:, s, :], rstd_of_piece[g][:, s:s + 1], ln_bias[:],
+                                           ALU.mult, ALU.add)
 
         kept = {b: {} for b in range(N_SAMPLES)}
 
@@ -343,7 +426,7 @@ def tile_rsaffdecoder_b_kernel(
             kept[b]["att"] = att
 
         def flip_att(b):
-            att_flipped_ps = psum_ring["att_flipped"].tile([P, HEADS, SLOTS], BF16, tag="att_flipped")
+            att_flipped_ps = psum_ring["short"].tile([P, HEADS, SLOTS], BF16, tag="short")
             for t in range(HEADS):
                 nc.tensor.transpose(att_flipped_ps[:, t, :], kept[b]["att"][:, t, :], identity_bf16[:])
             kept[b]["att_flipped_ps"] = att_flipped_ps
@@ -355,14 +438,15 @@ def tile_rsaffdecoder_b_kernel(
 
         def weigh(b):
             q_k_v = q_k_v_of_sample[b]
-            o_ps = psum_ring["o"].tile([P, HEADS, SLOTS], F32, tag="o")
+            o_ps = psum_ring["short"].tile([P, HEADS, SLOTS], F32, tag="short")
             for t in range(HEADS):
                 nc.tensor.matmul(o_ps[:, t, :], q_k_v[:, t, 2, :], kept[b]["att_flipped"][:, t, :], start=True, stop=True)
             kept[b]["o_ps"] = o_ps
 
         def add_residual(b):
             mem1_biased = ring["mem1_biased"].tile([P, HID_BLOCKS, SLOTS], F32)
-            nc.vector.tensor_tensor(mem1_biased[:], kept[b]["o_ps"][:], mem[:, :, b * SLOTS:(b + 1) * SLOTS], ALU.add)
+            u, start = divmod(b * SLOTS, LOOKUP)
+            nc.vector.tensor_tensor(mem1_biased[:], kept[b]["o_ps"][:], mem[u][:, :, start:start + SLOTS], ALU.add)
             kept[b]["mem1_biased"] = mem1_biased
 
         def rectify(b):
@@ -373,38 +457,46 @@ def tile_rsaffdecoder_b_kernel(
             kept[b]["relu_mem1"] = relu_mem1
 
         def mlp_product(b):
-            f_ps = psum_ring["f"].tile([P, HID], F32, tag="f")
+            f_ps = psum_ring["short"].tile([P, HID], F32, tag="short")
             for hb in range(HID_BLOCKS):
                 nc.tensor.matmul(f_ps[:], kept[b]["relu_mem1"][:, hb, :], mlp_w_sb[:, hb, :],
                                  start=(hb == 0), stop=(hb == HID_BLOCKS - 1))
             kept[b]["f_ps"] = f_ps
 
-        def mlp_moments(b):
+        def mlp_bias(b):
             f = ring["f"].tile([P, HID], F32)
-            nc.vector.tensor_tensor(f[:], kept[b]["f_ps"][:], mlp_b_sb[:], ALU.add)
-            f_stats = ring["f_stats"].tile([P, 6], F32)
-            nc.vector.bn_stats(f_stats[:], f[:])
-            f_moments = ring["f_moments"].tile([P, 2], F32)
-            nc.vector.bn_aggr(f_moments[:], f_stats[:])
-            var2 = ring["var2"].tile([P, 1], F32)
-            nc.vector.tensor_scalar_add(var2[:], f_moments[:, 1:2], EPS)
+            f_sum = ring["f_sum"].tile([P, 1], F32)
+            nc.vector.scalar_tensor_tensor(f[:], kept[b]["f_ps"][:], 1.0, mlp_b_sb[:], ALU.mult, ALU.add, accum_out=f_sum[:])
             kept[b]["f"] = f
-            kept[b]["f_moments"] = f_moments
-            kept[b]["var2"] = var2
+            kept[b]["f_sum"] = f_sum
+
+        def mlp_mean(b):
+            minus_mu2 = ring["minus_mu2"].tile([P, 1], F32)
+            nc.gpsimd.tensor_scalar(minus_mu2[:], kept[b]["f_sum"][:], -1.0 / HID, None, ALU.mult)
+            kept[b]["minus_mu2"] = minus_mu2
+
+        def mlp_square(b):
+            f_squares = ring["f_squares"].tile([P, HID], BF16)
+            f_square_sum = ring["f_square_sum"].tile([P, 1], F32)
+            nc.scalar.activation(f_squares[:], kept[b]["f"][:], FUNC.Square, bias=kept[b]["minus_mu2"][:],
+                                 accum_out=f_square_sum[:])
+            kept[b]["f_square_sum"] = f_square_sum
 
         def mlp_rstd(b):
+            var2 = ring["var2"].tile([P, 1], F32)
+            nc.gpsimd.tensor_scalar(var2[:], kept[b]["f_square_sum"][:], 1.0 / HID, EPS, ALU.mult, ALU.add)
             rstd2 = ring["rstd2"].tile([P, 1], F32)
-            nc.gpsimd.tensor_tensor(rstd2[:], kept[b]["var2"][:], minus_half[:, 0:1], ALU.pow)
+            nc.gpsimd.tensor_tensor(rstd2[:], var2[:], minus_half[:, 0:1], ALU.pow)
             kept[b]["rstd2"] = rstd2
 
         def mlp_normalise(b):
             normed = ring["normed"].tile([P, HID], F32)
-            nc.vector.tensor_scalar(normed[:], kept[b]["f"][:], kept[b]["f_moments"][:, 0:1], kept[b]["rstd2"][:],
-                                    ALU.subtract, ALU.mult)
+            nc.vector.tensor_scalar(normed[:], kept[b]["f"][:], kept[b]["minus_mu2"][:], kept[b]["rstd2"][:],
+                                    ALU.add, ALU.mult)
             kept[b]["normed"] = normed
 
         def flip_back(b):
-            normed_flipped = psum_ring["flipped"].tile([P, HID_BLOCKS, SLOTS], F32, tag="flipped")
+            normed_flipped = psum_ring["short"].tile([P, HID_BLOCKS, SLOTS], F32, tag="short")
             for rb in range(HID_BLOCKS):
                 nc.tensor.transpose(normed_flipped[:, rb, :], kept[b]["normed"][:, rb * P:(rb + 1) * P], identity_f32[:])
             kept[b]["normed_flipped"] = normed_flipped
@@ -417,25 +509,28 @@ def tile_rsaffdecoder_b_kernel(
                                                kept[b]["mem1_biased"][:, rb, :], ALU.mult, ALU.add)
             nc.sync.dma_start(out_blocks[:, :, b * SLOTS:(b + 1) * SLOTS], result[:])
 
-        def score_and_max(b):
-            score(b)
-            find_max(b)
+        def in_turn(*links):
+            def stage(b):
+                for link in links:
+                    link(b)
+            return stage
 
-        stages = (score_and_max, exponentiate, invert_sum, divide, flip_att, copy_att, weigh, add_residual, rectify,
-                  mlp_product, mlp_moments, mlp_rstd, mlp_normalise, flip_back, finish)
-        complete_mem0(1)
-        for tick in range(-1, N_SAMPLES + len(stages) - 1):
+        stages = (in_turn(score, find_max), exponentiate, invert_sum, divide, flip_att, copy_att, weigh, add_residual, rectify,
+                  mlp_product, in_turn(mlp_bias, mlp_mean), in_turn(mlp_square, mlp_rstd), mlp_normalise, flip_back, finish)
+        out_blocks = out.rearrange("(rb p) n -> p rb n", p=P)
+        for tick in range(-PROJECT_LEAD, N_SAMPLES + len(stages) - 1):
             for lag in reversed(range(len(stages))):
-                if lag == 0:
-                    g, s = divmod(tick + 3, PIECE_SAMPLES)
-                    if s == 0 and g < PIECES:
-                        measure(g, psum_ring["scores"], "scores")
                 if 0 <= tick - lag < N_SAMPLES:
                     stages[lag](tick - lag)
-            if tick + 1 < N_SAMPLES:
-                normalise(tick + 1)
-            g, s = divmod(tick + 5, PIECE_SAMPLES)
+            if 0 <= tick + NORMALISE_LEAD < N_SAMPLES:
+                normalise(tick + NORMALISE_LEAD)
+            g, s = divmod(tick + MEASURE_LEAD, PIECE_SAMPLES)
+            if s == 0 and 0 <= g < PIECES:
+                measure(g)
+            g, s = divmod(tick + PROJECT_LEAD, PIECE_SAMPLES)
             if s == 0 and g < PIECES:
-                project(g, psum_ring["bank"])
-                if g % 2 == 0 and g // 2 + 1 < LOOKUPS:
-                    complete_mem0(g // 2 + 1)
+                for part in range(PARTS):
+                    project_part(g, part)
+                if g < 2:
+                    make_mem(g + 2)
+                    find_mean(g + 2)

@@ -28,10 +28,11 @@ LOOKUP_SAMPLES = LOOKUP // SLOTS
 PIECE = 256
 PIECES = N_TOK // PIECE
 PIECE_SAMPLES = PIECE // SLOTS
-PARTS = PIECE_SAMPLES + HEADS
 NORMALISE_LEAD = 1
 MEASURE_LEAD = 3
 PROJECT_LEAD = 5
+EARLY_BLOCKS = 6
+TERM_GROUPS = 6
 QUADRANT = 32
 EPS = 1e-5
 Q_SCALE = 128.0 ** -0.5
@@ -66,22 +67,11 @@ def tile_rsaffdecoder_b_kernel(
     nc = tc.nc
     with ExitStack() as ctx:
         held = ctx.enter_context(tc.tile_pool(name="held", bufs=1))
+        in_order = ctx.enter_context(tc.tile_pool(name="in_order", bufs=1))
         identity_f32 = held.tile([P, P], F32)
         make_identity(nc, identity_f32[:])
         identity_bf16 = held.tile([P, P], BF16)
         nc.vector.tensor_copy(identity_bf16[:], identity_f32[:])
-
-        def split(pool, engine, value, shape, name):
-            terms = []
-            for k in range(3):
-                term = pool.tile(shape, BF16, name=f"{name}_term{k}")
-                engine.tensor_copy(term[:], value[:])
-                terms.append(term)
-                if k < 2:
-                    rest = pool.tile(shape, F32, name=f"{name}_rest{k}")
-                    engine.tensor_tensor(rest[:], value[:], term[:], ALU.subtract)
-                    value = rest
-            return terms
 
         psum_ring = {kind: ctx.enter_context(tc.psum_pool(name="psum_" + kind, bufs=bufs)) for kind, bufs in PSUM_RINGS}
         bank = psum_ring["bank"]
@@ -97,38 +87,39 @@ def tile_rsaffdecoder_b_kernel(
 
             dist = held.tile([P, SLOTS], F32)
             nc.vector.memset(dist[:], 0.0)
-            nc.sync.dma_start(dist[0:N_SAMPLES, :], distances.rearrange("o (b n) -> (o b) n", n=SLOTS))
+            for g in range(TERM_GROUPS):
+                queue = nc.sync if g % 2 == 0 else nc.scalar
+                queue.dma_start(dist[g * N_SAMPLES:(g + 1) * N_SAMPLES, :], distances.rearrange("o (b n) -> (o b) n", n=SLOTS))
             table_sb = held.tile([P, TABLE_COLS], BF16)
             nc.scalar.dma_start(table_sb[:], table)
+            w_emb_sb = held.tile([P, EMB_BLOCKS, HID], BF16)
+            nc.sync.dma_start(w_emb_sb[:], w_emb.rearrange("(k p) h -> p k h", p=P))
+            emb_sb = [held.tile([P, EMB_BLOCKS, LOOKUP], BF16, name=f"emb{u}") for u in range(LOOKUPS)]
+            emb_blocks = emb.rearrange("(k p) n -> p k n", p=P)
+            for u in (0, 1):
+                nc.sync.dma_start(emb_sb[u][:], emb_blocks[:, :, u * LOOKUP:(u + 1) * LOOKUP])
+            w_dist_row = setup.tile([P, HID], F32)
+            nc.sync.dma_start(w_dist_row[:], w_dist.rearrange("h o -> (h o)").partition_broadcast(P))
+            offsets = held.tile([P, N_TOK // 16], U16, name="offsets")
+            nc.sync.dma_start(offsets[:], offs)
+            w_lab_sb = held.tile([P, HID], BF16)
+            nc.sync.dma_start(w_lab_sb[:], w_lab)
+            nc.sync.dma_start(rows[COL_PRE_B:COL_PRE_B + HID_BLOCKS, :], as_rows(pre_b))
+            nc.sync.dma_start(rows[COL_MLP_LN_B:COL_MLP_LN_B + HID_BLOCKS, :], as_rows(mlp_ln_b))
+            v_bias = setup.tile([P, HEADS, P], F32)
+            nc.sync.dma_start(v_bias[:], qkv_b.rearrange("(t c u) o -> t c (u o)", c=3, u=P)[:, 2, :].partition_broadcast(P))
+            nc.sync.dma_start(late_rows[LATE_COL_QKV_B:LATE_COL_QKV_B + PROJ // P, :], as_rows(qkv_b))
+            nc.sync.dma_start(late_rows[LATE_COL_MLP_LN_W:LATE_COL_MLP_LN_W + HID_BLOCKS, :], as_rows(mlp_ln_w))
+
             w_qry_sb = held.tile([P, EMB_BLOCKS, HID], BF16)
-            nc.scalar.dma_start(w_qry_sb[:], w_qry.rearrange("(k p) h -> p k h", p=P))
+            nc.gpsimd.dma_start(w_qry_sb[:], w_qry.rearrange("(k p) h -> p k h", p=P))
+            query_sb = held.tile([P, EMB_BLOCKS, N_SAMPLES], BF16)
+            nc.gpsimd.dma_start(query_sb[:], query.rearrange("(k p) b -> p k b", p=P))
             qkv_w_sb = held.tile([P, HID_BLOCKS, PROJ], BF16)
             nc.gpsimd.dma_start(qkv_w_sb[:], qkv_w.rearrange("(hb p) r -> p hb r", p=P))
             ln_gain = held.tile([P, PROJ], F32)
             nc.gpsimd.dma_start(ln_gain[:].rearrange("p (r n) -> p r n", n=SLOTS),
                                 qkv_ln_w.rearrange("(r p) n -> p r n", p=P))
-
-            w_dist_row = setup.tile([P, HID], F32)
-            nc.sync.dma_start(w_dist_row[:], w_dist.rearrange("h o -> (h o)").partition_broadcast(P))
-            w_emb_sb = held.tile([P, EMB_BLOCKS, HID], BF16)
-            nc.sync.dma_start(w_emb_sb[:], w_emb.rearrange("(k p) h -> p k h", p=P))
-            emb_sb = [held.tile([P, EMB_BLOCKS, LOOKUP], BF16, name=f"emb{u}") for u in range(LOOKUPS)]
-            emb_blocks = emb.rearrange("(k p) n -> p k n", p=P)
-            nc.sync.dma_start(emb_sb[0][:], emb_blocks[:, :, 0:LOOKUP])
-            v_bias = setup.tile([P, HEADS, P], F32)
-            nc.sync.dma_start(v_bias[:], qkv_b.rearrange("(t c u) o -> t c (u o)", c=3, u=P)[:, 2, :].partition_broadcast(P))
-            offsets = held.tile([P, N_TOK // 16], U16, name="offsets")
-            nc.sync.dma_start(offsets[:], offs)
-            w_lab_sb = held.tile([P, HID], BF16)
-            nc.sync.dma_start(w_lab_sb[:], w_lab)
-            query_sb = held.tile([P, EMB_BLOCKS, N_SAMPLES], BF16)
-            nc.sync.dma_start(query_sb[:], query.rearrange("(k p) b -> p k b", p=P))
-            nc.sync.dma_start(rows[COL_PRE_B:COL_PRE_B + HID_BLOCKS, :], as_rows(pre_b))
-            nc.sync.dma_start(rows[COL_MLP_LN_B:COL_MLP_LN_B + HID_BLOCKS, :], as_rows(mlp_ln_b))
-            nc.sync.dma_start(emb_sb[1][:], emb_blocks[:, :, LOOKUP:2 * LOOKUP])
-            nc.sync.dma_start(late_rows[LATE_COL_QKV_B:LATE_COL_QKV_B + PROJ // P, :], as_rows(qkv_b))
-            nc.sync.dma_start(late_rows[LATE_COL_MLP_LN_W:LATE_COL_MLP_LN_W + HID_BLOCKS, :], as_rows(mlp_ln_w))
-
             ln_bias = held.tile([P, PROJ], F32)
             nc.gpsimd.dma_start(ln_bias[:].rearrange("p (r n) -> p r n", n=SLOTS),
                                 qkv_ln_b.rearrange("(r p) n -> p r n", p=P))
@@ -148,57 +139,57 @@ def tile_rsaffdecoder_b_kernel(
             minus_half = held.tile([P, PIECE_SAMPLES], F32)
             nc.vector.memset(minus_half[:], -0.5)
 
-            repeat_rows = held.tile([P, P], F32)
-            nc.vector.tensor_copy(repeat_rows[:].rearrange("p (g b) -> p g b", b=N_SAMPLES),
-                                  identity_f32[:, 0:N_SAMPLES].unsqueeze(1).to_broadcast([P, P // N_SAMPLES, N_SAMPLES]))
-            dist_ps = psum_ring["short"].tile([P, SLOTS], F32, tag="short")
-            nc.tensor.matmul(dist_ps[:], repeat_rows[:], dist[:], start=True, stop=True)
+            in_group = setup.tile([P, P // N_SAMPLES], F32)
+            nc.vector.tensor_reduce(in_group[:], identity_f32[:].rearrange("p (g b) -> p g b", b=N_SAMPLES), AXIS_X, ALU.add)
+            sample_of_row = held.tile([P, N_SAMPLES], BF16)
+            with nc.allow_low_precision(reason="no sum has more than one term that is not 0"):
+                nc.vector.tensor_reduce(sample_of_row[:], identity_f32[:].rearrange("p (g b) -> p b g", b=N_SAMPLES)[:, :, 0:TERM_GROUPS],
+                                        AXIS_X, ALU.add)
+            later_d = setup.tile([P, 1], F32)
+            nc.vector.tensor_reduce(later_d[:], in_group[:, 3:6], AXIS_X, ALU.add)
+            third_d = in_group[:, 5:6]
+            later_w = setup.tile([P, 1], F32)
+            second_w = setup.tile([P, 1], F32)
+            nc.vector.tensor_tensor(second_w[:], in_group[:, 1:2], in_group[:, 4:5], ALU.add)
+            nc.vector.tensor_tensor(later_w[:], second_w[:], in_group[:, 2:3], ALU.add)
+            third_w = in_group[:, 2:3]
+
+            def take_terms(out, value, later, third, shape, name):
+                first = in_order.tile(shape, BF16, tag="slot", name=f"{name}_first")
+                nc.vector.tensor_copy(first[:], value[:])
+                minus_rest = setup.tile(shape, F32, name=f"{name}_minus_rest")
+                nc.vector.scalar_tensor_tensor(minus_rest[:], first[:], later, value[:], ALU.mult, ALU.subtract)
+                minus_second = setup.tile(shape, BF16, name=f"{name}_minus_second")
+                nc.vector.tensor_copy(minus_second[:], minus_rest[:])
+                nc.vector.scalar_tensor_tensor(out[:], minus_second[:], third, minus_rest[:], ALU.mult, ALU.subtract)
+
             d_min = setup.tile([P, 1], F32)
-            nc.vector.tensor_reduce(d_min[:], dist_ps[:], AXIS_X, ALU.min)
+            nc.vector.tensor_reduce(d_min[:], dist[:], AXIS_X, ALU.min)
             e_dist = setup.tile([P, SLOTS], F32)
             d_sum = setup.tile([P, 1], F32)
-            nc.scalar.activation(e_dist[:], dist_ps[:], FUNC.Exp, bias=d_min[:], scale=-1.0, accum_out=d_sum[:])
+            nc.scalar.activation(e_dist[:], dist[:], FUNC.Exp, bias=d_min[:], scale=-1.0, accum_out=d_sum[:])
             d_rsum = setup.tile([P, 1], F32)
             nc.vector.reciprocal(d_rsum[:], d_sum[:])
             d = setup.tile([P, SLOTS], F32)
             nc.vector.tensor_scalar_mul(d[:], e_dist[:], d_rsum[:])
-            d_terms = split(setup, nc.vector, d, [P, SLOTS], "d")
-            d_of_row = held.tile([P, SLOTS], BF16)
-            for q, k in enumerate((0, 1, 2, 0)):
-                quadrant = slice(QUADRANT * q, QUADRANT * (q + 1))
-                nc.vector.tensor_copy(d_of_row[quadrant, :], d_terms[k][quadrant, :])
-            sample_of_row = held.tile([P, N_SAMPLES], BF16)
-            with nc.allow_low_precision(reason="each sum has one term that is not 0"):
-                nc.vector.tensor_reduce(sample_of_row[:], identity_f32[:].rearrange("p (g b) -> p b g", b=N_SAMPLES),
-                                        AXIS_X, ALU.add)
+            d_of_row = setup.tile([P, SLOTS], BF16)
+            take_terms(d_of_row, d, later_d[:], third_d, [P, SLOTS], "d")
+            w_dist_rows = held.tile([P, HID], BF16)
+            take_terms(w_dist_rows, w_dist_row, later_w[:], third_w, [P, HID], "w_dist")
             d_rows = [held.tile([P, LOOKUP_SAMPLES, SLOTS], BF16, name=f"d_rows{u}") for u in range(LOOKUPS)]
             for u in range(LOOKUPS):
                 group = slice(u * LOOKUP_SAMPLES, (u + 1) * LOOKUP_SAMPLES)
                 shape = [P, LOOKUP_SAMPLES, SLOTS]
-                nc.vector.tensor_tensor(d_rows[u][:], sample_of_row[:, group].unsqueeze(2).to_broadcast(shape),
+                engine = nc.vector if u < 2 else nc.gpsimd
+                engine.tensor_tensor(d_rows[u][:], sample_of_row[:, group].unsqueeze(2).to_broadcast(shape),
                                         d_of_row[:].unsqueeze(1).to_broadcast(shape), ALU.mult)
 
-            halves = identity_f32[:].rearrange("p (q h b) -> p q h b", h=2, b=N_SAMPLES)
-            term_of_row = setup.tile([P, 3], F32)
-            nc.vector.tensor_reduce(term_of_row[:, 0:1], halves[:, 0:3, 0, :], AXIS_XY, ALU.add)
-            nc.vector.tensor_reduce(term_of_row[:, 1:2], halves[:, 0:2, 1, :], AXIS_XY, ALU.add)
-            nc.vector.tensor_reduce(term_of_row[:, 2:3], halves[:, 3, 0, :], AXIS_X, ALU.add)
-            w_dist_rows = held.tile([P, HID], BF16)
-            w_terms = split(setup, nc.vector, w_dist_row, [P, HID], "w_dist")
-            w_first = setup.tile([P, HID], BF16)
-            w_second = setup.tile([P, HID], BF16)
-            nc.vector.tensor_scalar_mul(w_first[:], w_terms[0][:], term_of_row[:, 0:1])
-            nc.vector.scalar_tensor_tensor(w_second[:], w_terms[1][:], term_of_row[:, 1:2], w_first[:], ALU.mult, ALU.add)
-            nc.vector.scalar_tensor_tensor(w_dist_rows[:], w_terms[2][:], term_of_row[:, 2:3], w_second[:], ALU.mult, ALU.add)
-
+            picked = setup.tile([P, 1], F32)
+            nc.vector.tensor_reduce(picked[:], identity_f32[:, 0:3 * N_SAMPLES:N_SAMPLES], AXIS_X, ALU.add)
             pick_rows = held.tile([P, P], BF16)
-            nc.vector.memset(pick_rows[:], 0.0)
+            nc.vector.tensor_scalar_mul(pick_rows[:], ones[:], picked[:])
             v_bias_rows = held.tile([P, HEADS, P], BF16)
-            nc.vector.memset(v_bias_rows[:], 0.0)
-            for k, term in enumerate(split(setup, nc.vector, v_bias, [P, HEADS, P], "v_bias")):
-                quadrant = slice(QUADRANT * k, QUADRANT * (k + 1))
-                nc.vector.memset(pick_rows[QUADRANT * k:QUADRANT * k + 1, :], 1.0)
-                nc.vector.tensor_copy(v_bias_rows[quadrant, :, :], term[quadrant, :, :])
+            take_terms(v_bias_rows, v_bias, later_w[:], third_w, [P, HEADS, P], "v_bias")
 
         ring = {kind: ctx.enter_context(tc.tile_pool(name=kind, bufs=bufs)) for kind, bufs in SBUF_RINGS}
 
@@ -233,34 +224,33 @@ def tile_rsaffdecoder_b_kernel(
             nc.vector.tensor_scalar_add(mem0_bf16[u][:, hb, :], mem[u][:, hb, :], minus_last_bias[:, hb:hb + 1])
 
         def sum_weights():
-            half = HID_BLOCKS // 2
             w_copy = held.tile([P, PROJ], BF16)
-            for hb in range(half):
-                nc.scalar.activation(w_copy[:], qkv_w_sb[:, hb, :], FUNC.Copy, accum_out=w_sums[:, hb:hb + 1])
-            nc.vector.tensor_reduce(w_sums[:, half:HID_BLOCKS], qkv_w_sb[:, half:HID_BLOCKS, :], AXIS_X, ALU.add)
+            nc.scalar.activation(w_copy[:], qkv_w_sb[:, 0, :], FUNC.Copy, accum_out=first_w_sum[:])
+            for hb in range(1, HID_BLOCKS):
+                nc.vector.tensor_reduce(later_w_sums[:, hb - 1:hb], qkv_w_sb[:, hb, :], AXIS_X, ALU.add)
             for hb in range(HID_BLOCKS):
-                nc.vector.tensor_scalar(mean_weights[:, hb, :], ones[:], w_sums[:, hb:hb + 1], 1.0 / (P * PROJ),
-                                        ALU.mult, ALU.mult)
+                w_sum = first_w_sum[:] if hb == 0 else later_w_sums[:, hb - 1:hb]
+                nc.vector.tensor_scalar(mean_weights[:, hb, :], ones[:], w_sum, 1.0 / (P * PROJ), ALU.mult, ALU.mult)
 
         def centre_bias():
             qkv_b_cols = late_cols[:, LATE_COL_QKV_B:LATE_COL_QKV_B + PROJ // P]
-            bias_sum = held.tile([P, 2], F32)
-            nc.vector.tensor_reduce(bias_sum[:, 0:1], qkv_b_cols, AXIS_X, ALU.add)
-            extra = held.tile([P, HID_BLOCKS], F32)
-            nc.vector.tensor_tensor(extra[:], w_sums[:], minus_last_bias[:], ALU.mult)
-            nc.vector.tensor_reduce(bias_sum[:, 1:2], extra[:], AXIS_X, ALU.add)
-            bias_ps = bank.tile([P, 2], F32, tag="bank")
-            nc.tensor.matmul(bias_ps[:], spread_bias[:], bias_sum[:], start=True, stop=True)
+            addends = held.tile([P, PROJ // P + HID_BLOCKS], F32)
+            nc.gpsimd.tensor_copy(addends[:, 0:PROJ // P], qkv_b_cols)
+            nc.gpsimd.tensor_tensor(addends[:, PROJ // P:PROJ // P + 1], first_w_sum[:], minus_last_bias[:, 0:1], ALU.mult)
+            nc.gpsimd.tensor_tensor(addends[:, PROJ // P + 1:PROJ // P + HID_BLOCKS], later_w_sums[:],
+                                    minus_last_bias[:, 1:HID_BLOCKS], ALU.mult)
+            bias_ps = psum_ring["scores"].tile([P, PROJ // P + HID_BLOCKS], F32, tag="scores")
+            nc.tensor.matmul(bias_ps[:], spread_bias[:], addends[:], start=True, stop=True)
             bias_mean = held.tile([P, 1], F32)
             nc.vector.tensor_reduce(bias_mean[:], bias_ps[:], AXIS_X, ALU.add)
-            nc.vector.memset(centred_bias[:], 0.0)
+            nc.gpsimd.memset(centred_bias[:], 0.0)
             by_kind = centred_bias[:].rearrange("p (t c) -> p t c", c=3)
-            nc.vector.tensor_copy(by_kind[:, :, 0:2], qkv_b_cols.rearrange("p (t c) -> p t c", c=3)[:, :, 0:2])
+            nc.gpsimd.tensor_copy(by_kind[:, :, 0:2], qkv_b_cols.rearrange("p (t c) -> p t c", c=3)[:, :, 0:2])
             nc.vector.tensor_scalar(centred_bias[:], centred_bias[:], bias_mean[:], None, ALU.subtract)
 
-        def find_mean(u):
+        def find_mean(u, kind):
             group = slice(u * LOOKUP_SAMPLES, (u + 1) * LOOKUP_SAMPLES)
-            mean_ps = bank.tile([P, LOOKUP_SAMPLES], F32, tag="bank")
+            mean_ps = psum_ring[kind].tile([P, LOOKUP_SAMPLES], F32, tag=kind)
             for hb in range(HID_BLOCKS):
                 nc.tensor.matmul(mean_ps[:], mean_weights[:, hb, :], mem_sums[:, hb, group],
                                  start=(hb == 0), stop=(hb == HID_BLOCKS - 1))
@@ -268,7 +258,8 @@ def tile_rsaffdecoder_b_kernel(
             nc.vector.tensor_tensor(shift[:, group, :], centred_bias[:].unsqueeze(1).to_broadcast(shape),
                                     mean_ps[:].unsqueeze(2).to_broadcast(shape), ALU.subtract)
 
-        w_sums = held.tile([P, HID_BLOCKS], F32)
+        first_w_sum = held.tile([P, 1], F32)
+        later_w_sums = in_order.tile([P, HID_BLOCKS - 1], F32, tag="slot")
         mean_weights = held.tile([P, HID_BLOCKS, P], F32)
         centred_bias = held.tile([P, PROJ // P], F32)
         shift = held.tile([P, N_SAMPLES, PROJ // P], F32)
@@ -319,13 +310,24 @@ def tile_rsaffdecoder_b_kernel(
                 nc.scalar.activation(squares[:, 0, :], qk_ps[:, c, s, :], FUNC.Square, bias=shift[:, b, r:r + 1],
                                      accum_out=square_sums[:, b, 2 * t + c:2 * t + c + 1])
 
-        def project_part(g, part):
-            if part == 0:
-                start_piece(g)
-            if part < PIECE_SAMPLES:
-                project_v(g, part)
-            else:
-                project_qk(g, part - PIECE_SAMPLES)
+        parts_of_piece = [lambda g: project_v(g, 0), lambda g: project_qk(g, 0), lambda g: project_qk(g, 1),
+                          lambda g: project_v(g, 1), lambda g: project_qk(g, 2), lambda g: project_qk(g, 3)]
+        parts_done = []
+
+        def project(g):
+            start_piece(g)
+            for project_part in parts_of_piece:
+                project_part(g)
+                parts_done.append(g)
+                n = len(parts_done)
+                turn = n // 4 if n <= 16 else 4 + (n - 16) // 3
+                if (n % 4 == 0 if n <= 16 else (n - 16) % 3 == 0) and turn <= len(later_blocks):
+                    u, hb = later_blocks[turn - 1]
+                    mem_ps = open_mem(u, hb, "bank")
+                    add_dist(u, hb, mem_ps)
+                    close_mem(u, hb, mem_ps)
+                    if hb == HID_BLOCKS - 1:
+                        find_mean(u, "bank")
 
         def measure(g):
             samples = slice(g * PIECE_SAMPLES, (g + 1) * PIECE_SAMPLES)
@@ -338,49 +340,42 @@ def tile_rsaffdecoder_b_kernel(
             nc.gpsimd.tensor_tensor(rstd[:], var_eps[:], minus_half[:], ALU.pow)
             rstd_of_piece[g] = rstd
 
-        def prepare_param(param):
+        def prepare_param(param, engine):
             by_kind = param[:].rearrange("p (t c n) -> p t c n", c=3, n=SLOTS)
-            v_flipped = bank.tile([P, HEADS, P], F32, tag="bank")
+            v_flipped = psum_ring["short"].tile([P, HEADS, P], F32, tag="short")
             for t in range(HEADS):
                 nc.tensor.transpose(v_flipped[:, t, :], by_kind[:, t, 2, :], identity_f32[:])
             nc.vector.tensor_copy(by_kind[:, :, 2, :], v_flipped[:])
-            nc.vector.tensor_scalar_mul(by_kind[:, :, 0, :], by_kind[:, :, 0, :], Q_SCALE)
-
-        def make_mem(*lookups):
-            opened = []
-            for u in lookups:
-                for hb in range(HID_BLOCKS):
-                    kind = "bank" if u == 0 else "scores" if hb == 0 else "short"
-                    opened.append((u, hb, open_mem(u, hb, kind)))
-            for u, hb, mem_ps in opened:
-                add_dist(u, hb, mem_ps)
-            for u, hb, mem_ps in opened:
-                close_mem(u, hb, mem_ps)
+            engine.mul(by_kind[:, :, 0, :], by_kind[:, :, 0, :], Q_SCALE)
 
         cols_ps = psum_ring["short"].tile([P, P], F32, tag="short")
         nc.tensor.transpose(cols_ps[:], rows[:], identity_f32[:])
-        nc.vector.tensor_copy(cols[:], cols_ps[:, 0:N_COLS])
+        nc.scalar.copy(cols[:], cols_ps[:, 0:N_COLS])
         query_ps = psum_ring["short"].tile([P, HID_BLOCKS, N_SAMPLES], F32, tag="short")
         for hb in range(HID_BLOCKS):
             for kb in range(EMB_BLOCKS):
                 nc.tensor.matmul(query_ps[:, hb, :], w_qry_sb[:, kb, hb * P:(hb + 1) * P], query_sb[:, kb, :],
                                  start=(kb == 0), stop=(kb == EMB_BLOCKS - 1))
         last_bias = cols[:, COL_MLP_LN_B:COL_MLP_LN_B + HID_BLOCKS]
-        nc.vector.tensor_scalar_mul(minus_last_bias[:], last_bias, -1.0)
+        nc.gpsimd.tensor_scalar(minus_last_bias[:], last_bias, -1.0, None, ALU.mult)
         both_biases = held.tile([P, HID_BLOCKS], F32)
-        nc.vector.tensor_tensor(both_biases[:], cols[:, COL_PRE_B:COL_PRE_B + HID_BLOCKS], last_bias, ALU.add)
-        nc.vector.tensor_tensor(query_term[:], query_ps[:],
-                                both_biases[:].unsqueeze(2).to_broadcast([P, HID_BLOCKS, N_SAMPLES]), ALU.add)
-        make_mem(0, 1)
-        late_cols_ps = bank.tile([P, P], F32, tag="bank")
+        nc.gpsimd.tensor_tensor(both_biases[:], cols[:, COL_PRE_B:COL_PRE_B + HID_BLOCKS], last_bias, ALU.add)
+        for hb in range(HID_BLOCKS):
+            nc.scalar.activation(query_term[:, hb, :], query_ps[:, hb, :], FUNC.Identity, bias=both_biases[:, hb:hb + 1])
+        blocks = [(u, hb) for u in range(LOOKUPS) for hb in range(HID_BLOCKS)]
+        early_blocks, later_blocks = blocks[:EARLY_BLOCKS], blocks[EARLY_BLOCKS:]
+        opened = [(u, hb, open_mem(u, hb, "bank" if u == 0 else "short")) for u, hb in early_blocks]
+        for u, hb, mem_ps in opened:
+            add_dist(u, hb, mem_ps)
+        for u, hb, mem_ps in opened:
+            close_mem(u, hb, mem_ps)
+        late_cols_ps = psum_ring["short"].tile([P, P], F32, tag="short")
         nc.tensor.transpose(late_cols_ps[:], late_rows[:], identity_f32[:])
-        nc.vector.tensor_copy(late_cols[:], late_cols_ps[:, 0:N_LATE_COLS])
+        nc.scalar.copy(late_cols[:], late_cols_ps[:, 0:N_LATE_COLS])
+        prepare_param(ln_gain, nc.scalar)
         sum_weights()
         centre_bias()
-        find_mean(0)
-        prepare_param(ln_gain)
-        find_mean(1)
-        prepare_param(ln_bias)
+        find_mean(0, "scores")
 
         def normalise(b):
             g, s = divmod(b, PIECE_SAMPLES)
@@ -472,7 +467,7 @@ def tile_rsaffdecoder_b_kernel(
 
         def mlp_mean(b):
             minus_mu2 = ring["minus_mu2"].tile([P, 1], F32)
-            nc.gpsimd.tensor_scalar(minus_mu2[:], kept[b]["f_sum"][:], -1.0 / HID, None, ALU.mult)
+            nc.vector.tensor_scalar_mul(minus_mu2[:], kept[b]["f_sum"][:], -1.0 / HID)
             kept[b]["minus_mu2"] = minus_mu2
 
         def mlp_square(b):
@@ -515,8 +510,9 @@ def tile_rsaffdecoder_b_kernel(
                     link(b)
             return stage
 
-        stages = (in_turn(score, find_max), exponentiate, invert_sum, divide, flip_att, copy_att, weigh, add_residual, rectify,
-                  mlp_product, in_turn(mlp_bias, mlp_mean), in_turn(mlp_square, mlp_rstd), mlp_normalise, flip_back, finish)
+        stages = (in_turn(score, find_max), in_turn(exponentiate, invert_sum), in_turn(divide, flip_att), in_turn(copy_att, weigh),
+                  in_turn(add_residual, rectify), in_turn(mlp_product, mlp_bias), in_turn(mlp_mean, mlp_square), mlp_rstd,
+                  in_turn(mlp_normalise, flip_back), finish)
         out_blocks = out.rearrange("(rb p) n -> p rb n", p=P)
         for tick in range(-PROJECT_LEAD, N_SAMPLES + len(stages) - 1):
             for lag in reversed(range(len(stages))):
@@ -529,8 +525,6 @@ def tile_rsaffdecoder_b_kernel(
                 measure(g)
             g, s = divmod(tick + PROJECT_LEAD, PIECE_SAMPLES)
             if s == 0 and g < PIECES:
-                for part in range(PARTS):
-                    project_part(g, part)
-                if g < 2:
-                    make_mem(g + 2)
-                    find_mean(g + 2)
+                project(g)
+                if g == 0:
+                    prepare_param(ln_bias, nc.scalar)

@@ -479,7 +479,7 @@ def tile_rsaffdecoder_b_kernel(
 
         def mlp_rstd(b):
             var2 = ring["var2"].tile([P, 1], F32)
-            nc.gpsimd.tensor_scalar(var2[:], kept[b]["f_square_sum"][:], 1.0 / HID, EPS, ALU.mult, ALU.add)
+            nc.vector.tensor_scalar(var2[:], kept[b]["f_square_sum"][:], 1.0 / HID, EPS, ALU.mult, ALU.add)
             rstd2 = ring["rstd2"].tile([P, 1], F32)
             nc.gpsimd.tensor_tensor(rstd2[:], var2[:], minus_half[:, 0:1], ALU.pow)
             kept[b]["rstd2"] = rstd2

@@ -172,17 +172,20 @@ def tile_rsaffdecoder_b_kernel(
             nc.vector.reciprocal(d_rsum[:], d_sum[:])
             d = setup.tile([P, SLOTS], F32)
             nc.vector.tensor_scalar_mul(d[:], e_dist[:], d_rsum[:])
-            d_of_row = setup.tile([P, SLOTS], BF16)
+            d_of_row = held.tile([P, SLOTS], BF16)
             take_terms(d_of_row, d, later_d[:], third_d, [P, SLOTS], "d")
             w_dist_rows = held.tile([P, HID], BF16)
             take_terms(w_dist_rows, w_dist_row, later_w[:], third_w, [P, HID], "w_dist")
             d_rows = [held.tile([P, LOOKUP_SAMPLES, SLOTS], BF16, name=f"d_rows{u}") for u in range(LOOKUPS)]
-            for u in range(LOOKUPS):
-                group = slice(u * LOOKUP_SAMPLES, (u + 1) * LOOKUP_SAMPLES)
-                shape = [P, LOOKUP_SAMPLES, SLOTS]
-                engine = nc.vector if u < 2 else nc.gpsimd
-                engine.tensor_tensor(d_rows[u][:], sample_of_row[:, group].unsqueeze(2).to_broadcast(shape),
-                                        d_of_row[:].unsqueeze(1).to_broadcast(shape), ALU.mult)
+
+            def make_d_rows(engine, *lookups):
+                for u in lookups:
+                    group = slice(u * LOOKUP_SAMPLES, (u + 1) * LOOKUP_SAMPLES)
+                    shape = [P, LOOKUP_SAMPLES, SLOTS]
+                    engine.tensor_tensor(d_rows[u][:], sample_of_row[:, group].unsqueeze(2).to_broadcast(shape),
+                                         d_of_row[:].unsqueeze(1).to_broadcast(shape), ALU.mult)
+
+            make_d_rows(nc.vector, 0, 1)
 
             picked = setup.tile([P, 1], F32)
             nc.vector.tensor_reduce(picked[:], identity_f32[:, 0:3 * N_SAMPLES:N_SAMPLES], AXIS_X, ALU.add)
@@ -369,6 +372,7 @@ def tile_rsaffdecoder_b_kernel(
             add_dist(u, hb, mem_ps)
         for u, hb, mem_ps in opened:
             close_mem(u, hb, mem_ps)
+        make_d_rows(nc.gpsimd, 2, 3)
         late_cols_ps = psum_ring["short"].tile([P, P], F32, tag="short")
         nc.tensor.transpose(late_cols_ps[:], late_rows[:], identity_f32[:])
         nc.scalar.copy(late_cols[:], late_cols_ps[:, 0:N_LATE_COLS])
@@ -381,8 +385,10 @@ def tile_rsaffdecoder_b_kernel(
             g, s = divmod(b, PIECE_SAMPLES)
             z = ring["z"].tile([P, PROJ], BF16)
             q_k_v_of_sample[b] = z[:].rearrange("p (t c n) -> p t c n", c=3, n=P)
-            nc.vector.scalar_tensor_tensor(z[:], scaled_of_piece[g][:, s, :], rstd_of_piece[g][:, s:s + 1], ln_bias[:],
-                                           ALU.mult, ALU.add)
+            for third in range(3):
+                columns = slice(third * HID, (third + 1) * HID)
+                nc.vector.scalar_tensor_tensor(z[:, columns], scaled_of_piece[g][:, s, columns], rstd_of_piece[g][:, s:s + 1],
+                                               ln_bias[:, columns], ALU.mult, ALU.add)
 
         kept = {b: {} for b in range(N_SAMPLES)}
 

@@ -28,9 +28,9 @@ LOOKUP_SAMPLES = LOOKUP // SLOTS
 PIECE = 256
 PIECES = N_TOK // PIECE
 PIECE_SAMPLES = PIECE // SLOTS
-NORMALISE_LEAD = 1
-MEASURE_LEAD = 3
-PROJECT_LEAD = 5
+NORMALISE_LEAD = 2
+MEASURE_LEAD = 4
+PROJECT_LEAD = 6
 EARLY_BLOCKS = 6
 TERM_GROUPS = 6
 QUADRANT = 32
@@ -516,9 +516,8 @@ def tile_rsaffdecoder_b_kernel(
                     link(b)
             return stage
 
-        stages = (in_turn(score, find_max), in_turn(exponentiate, invert_sum), in_turn(divide, flip_att), in_turn(copy_att, weigh),
-                  in_turn(add_residual, rectify), in_turn(mlp_product, mlp_bias), in_turn(mlp_mean, mlp_square), mlp_rstd,
-                  in_turn(mlp_normalise, flip_back), finish)
+        stages = (in_turn(score, find_max), exponentiate, in_turn(invert_sum, divide), flip_att, copy_att, weigh, add_residual, rectify,
+                  mlp_product, mlp_bias, in_turn(mlp_mean, mlp_square), mlp_rstd, mlp_normalise, flip_back, finish)
         out_blocks = out.rearrange("(rb p) n -> p rb n", p=P)
         for tick in range(-PROJECT_LEAD, N_SAMPLES + len(stages) - 1):
             for lag in reversed(range(len(stages))):

@@ -31,7 +31,7 @@ PIECE_SAMPLES = PIECE // SLOTS
 NORMALISE_LEAD = 2
 MEASURE_LEAD = 4
 PROJECT_LEAD = 6
-EARLY_BLOCKS = 6
+EARLY_BLOCKS = 7
 TERM_GROUPS = 6
 QUADRANT = 32
 EPS = 1e-5
@@ -49,7 +49,7 @@ SUM_EPS = 9
 N_SUMS = 10
 
 SBUF_RINGS = (
-    ("scaled", 3), ("z", 8), ("squares", 2), ("var_eps", 3), ("rstd", 3), ("exp_scores", 3), ("att", 3), ("att_flipped", 3), ("mem1_biased", 8),
+    ("scaled", 3), ("z", 8), ("y_v", 3), ("squares", 2), ("var_eps", 3), ("rstd", 3), ("exp_scores", 3), ("att", 3), ("att_flipped", 3), ("mem1_biased", 8),
     ("relu_mem1", 3), ("f", 3), ("normed", 3), ("result", 2), ("minus_max", 3), ("exp_sum", 3),
     ("exp_rsum", 3), ("f_sum", 3), ("minus_mu2", 4), ("f_squares", 2),
     ("f_square_sum", 3), ("var2", 3), ("rstd2", 3),
@@ -106,7 +106,7 @@ def tile_rsaffdecoder_b_kernel(
             nc.sync.dma_start(w_lab_sb[:], w_lab)
             nc.sync.dma_start(rows[COL_PRE_B:COL_PRE_B + HID_BLOCKS, :], as_rows(pre_b))
             nc.sync.dma_start(rows[COL_MLP_LN_B:COL_MLP_LN_B + HID_BLOCKS, :], as_rows(mlp_ln_b))
-            v_bias = setup.tile([P, HEADS, P], F32)
+            v_bias = held.tile([P, HEADS, P], F32)
             nc.sync.dma_start(v_bias[:], qkv_b.rearrange("(t c u) o -> t c (u o)", c=3, u=P)[:, 2, :].partition_broadcast(P))
             nc.sync.dma_start(late_rows[LATE_COL_QKV_B:LATE_COL_QKV_B + PROJ // P, :], as_rows(qkv_b))
             nc.sync.dma_start(late_rows[LATE_COL_MLP_LN_W:LATE_COL_MLP_LN_W + HID_BLOCKS, :], as_rows(mlp_ln_w))
@@ -186,13 +186,6 @@ def tile_rsaffdecoder_b_kernel(
                                          d_of_row[:].unsqueeze(1).to_broadcast(shape), ALU.mult)
 
             make_d_rows(nc.vector, 0, 1)
-
-            picked = setup.tile([P, 1], F32)
-            nc.vector.tensor_reduce(picked[:], identity_f32[:, 0:3 * N_SAMPLES:N_SAMPLES], AXIS_X, ALU.add)
-            pick_rows = held.tile([P, P], BF16)
-            nc.vector.tensor_scalar_mul(pick_rows[:], ones[:], picked[:])
-            v_bias_rows = held.tile([P, HEADS, P], BF16)
-            take_terms(v_bias_rows, v_bias, later_w[:], third_w, [P, HEADS, P], "v_bias")
 
         ring = {kind: ctx.enter_context(tc.tile_pool(name=kind, bufs=bufs)) for kind, bufs in SBUF_RINGS}
 
@@ -286,13 +279,13 @@ def tile_rsaffdecoder_b_kernel(
             v_ps = bank.tile([P, HEADS, P], F32, tag="bank")
             for hb in range(HID_BLOCKS):
                 nc.tensor.matmul(v_ps[:], mem0_bf16[u][:, hb, start + s * SLOTS:start + (s + 1) * SLOTS], v_weights[:, hb, :, :],
-                                 start=(hb == 0), stop=False)
-            nc.tensor.matmul(v_ps[:], pick_rows[:], v_bias_rows[:], start=False, stop=True)
-            nc.vector.scalar_tensor_tensor(scaled_of_piece[g][:, s, :].rearrange("p (t c u) -> p t c u", c=3, u=P)[:, :, 2, :],
-                                           v_ps[:], v_shift, gain_by_kind[:, :, 2, :], ALU.add, ALU.mult)
+                                 start=(hb == 0), stop=(hb == HID_BLOCKS - 1))
+            y_v = ring["y_v"].tile([P, HEADS, P], F32)
+            nc.vector.scalar_tensor_tensor(y_v[:], v_ps[:], v_shift, v_bias[:], ALU.add, ALU.add)
             squares = ring["squares"].tile([P, HEADS, P], BF16)
-            nc.scalar.activation(squares[:], v_ps[:], FUNC.Square, bias=v_shift,
-                                 accum_out=square_sums[:, b, SUM_V:SUM_V + 1])
+            nc.scalar.activation(squares[:], y_v[:], FUNC.Square, accum_out=square_sums[:, b, SUM_V:SUM_V + 1])
+            nc.vector.tensor_tensor(scaled_of_piece[g][:, s, :].rearrange("p (t c u) -> p t c u", c=3, u=P)[:, :, 2, :],
+                                    y_v[:], gain_by_kind[:, :, 2, :], ALU.mult)
 
         def project_qk(g, t):
             u, start = divmod(g * PIECE, LOOKUP)
@@ -315,16 +308,12 @@ def tile_rsaffdecoder_b_kernel(
 
         parts_of_piece = [lambda g: project_v(g, 0), lambda g: project_qk(g, 0), lambda g: project_qk(g, 1),
                           lambda g: project_v(g, 1), lambda g: project_qk(g, 2), lambda g: project_qk(g, 3)]
-        parts_done = []
-
         def project(g):
             start_piece(g)
-            for project_part in parts_of_piece:
+            for part, project_part in enumerate(parts_of_piece):
                 project_part(g)
-                parts_done.append(g)
-                n = len(parts_done)
-                turn = n // 4 if n <= 16 else 4 + (n - 16) // 3
-                if (n % 4 == 0 if n <= 16 else (n - 16) % 3 == 0) and turn <= len(later_blocks):
+                turn, rest = divmod(g * len(parts_of_piece) + part + 1, 4)
+                if rest == 0 and turn <= len(later_blocks):
                     u, hb = later_blocks[turn - 1]
                     mem_ps = open_mem(u, hb, "bank")
                     add_dist(u, hb, mem_ps)
@@ -367,7 +356,8 @@ def tile_rsaffdecoder_b_kernel(
             nc.scalar.activation(query_term[:, hb, :], query_ps[:, hb, :], FUNC.Identity, bias=both_biases[:, hb:hb + 1])
         blocks = [(u, hb) for u in range(LOOKUPS) for hb in range(HID_BLOCKS)]
         early_blocks, later_blocks = blocks[:EARLY_BLOCKS], blocks[EARLY_BLOCKS:]
-        opened = [(u, hb, open_mem(u, hb, "bank" if u == 0 else "short")) for u, hb in early_blocks]
+        kinds = ["bank"] * HID_BLOCKS + ["short"] * 2 + ["scores"]
+        opened = [(u, hb, open_mem(u, hb, kind)) for (u, hb), kind in zip(early_blocks, kinds)]
         for u, hb, mem_ps in opened:
             add_dist(u, hb, mem_ps)
         for u, hb, mem_ps in opened:

from contextlib import ExitStack

import concourse.mybir as mybir
from concourse.masks import make_identity

F32 = mybir.dt.float32
BF16 = mybir.dt.bfloat16
U16 = mybir.dt.uint16
FUNC = mybir.ActivationFunctionType
ALU = mybir.AluOpType
AXIS_X = mybir.AxisListType.X
AXIS_XY = mybir.AxisListType.XY

P = 128
TABLE_COLS = 4096
N_TOK = 2048
N_SAMPLES = 16
SLOTS = 128
HID = 512
HID_BLOCKS = HID // P
EMB_BLOCKS = 2
HEADS = 4
HEAD_ROWS = 384
PROJ = 3 * HEADS * P
LOOKUP = 512
LOOKUPS = N_TOK // LOOKUP
LOOKUP_SAMPLES = LOOKUP // SLOTS
PIECE = 256
PIECES = N_TOK // PIECE
PIECE_SAMPLES = PIECE // SLOTS
NORMALISE_LEAD = 2
MEASURE_LEAD = 4
PROJECT_LEAD = 6
EARLY_BLOCKS = 7
TERM_GROUPS = 6
QUADRANT = 32
EPS = 1e-5
Q_SCALE = 128.0 ** -0.5

COL_PRE_B = 0
COL_MLP_LN_B = 4
N_COLS = 8
LATE_COL_MLP_LN_W = 0
LATE_COL_QKV_B = 4
N_LATE_COLS = 16

SUM_V = 8
SUM_EPS = 9
N_SUMS = 10

SBUF_RINGS = (
    ("scaled", 3), ("z", 8), ("y_v", 3), ("squares", 2), ("var_eps", 3), ("rstd", 3), ("exp_scores", 3), ("att", 3), ("att_flipped", 3), ("mem1_biased", 8),
    ("relu_mem1", 3), ("f", 3), ("normed", 3), ("result", 2), ("minus_max", 3), ("exp_sum", 3),
    ("exp_rsum", 3), ("f_sum", 3), ("minus_mu2", 4), ("f_squares", 2),
    ("f_square_sum", 3), ("var2", 3), ("rstd2", 3),
)
PSUM_RINGS = (("bank", 4), ("scores", 1), ("short", 3))

FLOPS = 2 * (128 + 256) * HID * N_TOK + 2 * 256 * HID * N_SAMPLES + 2 * HID * PROJ * N_TOK \
    + 2 * 2 * HEADS * N_SAMPLES * SLOTS * SLOTS * P + 2 * HID * HID * N_TOK


def tile_rsaffdecoder_b_kernel(
    tc, table, w_lab, emb, w_emb, query, w_qry, distances, w_dist, pre_b, qkv_w, qkv_b,
    qkv_ln_w, qkv_ln_b, mlp_w, mlp_b, mlp_ln_w, mlp_ln_b, offs, out,
):
    nc = tc.nc
    with ExitStack() as ctx:
        held = ctx.enter_context(tc.tile_pool(name="held", bufs=1))
        in_order = ctx.enter_context(tc.tile_pool(name="in_order", bufs=1))
        identity_f32 = held.tile([P, P], F32)
        make_identity(nc, identity_f32[:])
        identity_bf16 = held.tile([P, P], BF16)
        nc.vector.tensor_copy(identity_bf16[:], identity_f32[:])

        psum_ring = {kind: ctx.enter_context(tc.psum_pool(name="psum_" + kind, bufs=bufs)) for kind, bufs in PSUM_RINGS}
        bank = psum_ring["bank"]

        with tc.tile_pool(name="setup", bufs=1) as setup:
            def as_rows(vector):
                return vector.rearrange("(k p) o -> k (p o)", p=P)

            rows = held.tile([P, P], F32)
            nc.vector.memset(rows[:], 0.0)
            late_rows = held.tile([P, P], F32)
            nc.vector.memset(late_rows[:], 0.0)

            dist = held.tile([P, SLOTS], F32)
            nc.vector.memset(dist[:], 0.0)
            for g in range(TERM_GROUPS):
                queue = nc.sync if g % 2 == 0 else nc.scalar
                queue.dma_start(dist[g * N_SAMPLES:(g + 1) * N_SAMPLES, :], distances.rearrange("o (b n) -> (o b) n", n=SLOTS))
            table_sb = held.tile([P, TABLE_COLS], BF16)
            nc.scalar.dma_start(table_sb[:], table)
            w_emb_sb = held.tile([P, EMB_BLOCKS, HID], BF16)
            nc.sync.dma_start(w_emb_sb[:], w_emb.rearrange("(k p) h -> p k h", p=P))
            emb_sb = [held.tile([P, EMB_BLOCKS, LOOKUP], BF16, name=f"emb{u}") for u in range(LOOKUPS)]
            emb_blocks = emb.rearrange("(k p) n -> p k n", p=P)
            for u in (0, 1):
                nc.sync.dma_start(emb_sb[u][:], emb_blocks[:, :, u * LOOKUP:(u + 1) * LOOKUP])
            w_dist_row = setup.tile([P, HID], F32)
            nc.sync.dma_start(w_dist_row[:], w_dist.rearrange("h o -> (h o)").partition_broadcast(P))
            offsets = held.tile([P, N_TOK // 16], U16, name="offsets")
            nc.sync.dma_start(offsets[:], offs)
            w_lab_sb = held.tile([P, HID], BF16)
            nc.sync.dma_start(w_lab_sb[:], w_lab)
            nc.sync.dma_start(rows[COL_PRE_B:COL_PRE_B + HID_BLOCKS, :], as_rows(pre_b))
            nc.sync.dma_start(rows[COL_MLP_LN_B:COL_MLP_LN_B + HID_BLOCKS, :], as_rows(mlp_ln_b))
            v_bias = held.tile([P, HEADS, P], F32)
            nc.sync.dma_start(v_bias[:], qkv_b.rearrange("(t c u) o -> t c (u o)", c=3, u=P)[:, 2, :].partition_broadcast(P))
            nc.sync.dma_start(late_rows[LATE_COL_QKV_B:LATE_COL_QKV_B + PROJ // P, :], as_rows(qkv_b))
            nc.sync.dma_start(late_rows[LATE_COL_MLP_LN_W:LATE_COL_MLP_LN_W + HID_BLOCKS, :], as_rows(mlp_ln_w))

            w_qry_sb = held.tile([P, EMB_BLOCKS, HID], BF16)
            nc.gpsimd.dma_start(w_qry_sb[:], w_qry.rearrange("(k p) h -> p k h", p=P))
            query_sb = held.tile([P, EMB_BLOCKS, N_SAMPLES], BF16)
            nc.gpsimd.dma_start(query_sb[:], query.rearrange("(k p) b -> p k b", p=P))
            qkv_w_sb = held.tile([P, HID_BLOCKS, PROJ], BF16)
            nc.gpsimd.dma_start(qkv_w_sb[:], qkv_w.rearrange("(hb p) r -> p hb r", p=P))
            ln_gain = held.tile([P, PROJ], F32)
            nc.gpsimd.dma_start(ln_gain[:].rearrange("p (r n) -> p r n", n=SLOTS),
                                qkv_ln_w.rearrange("(r p) n -> p r n", p=P))
            ln_bias = held.tile([P, PROJ], F32)
            nc.gpsimd.dma_start(ln_bias[:].rearrange("p (r n) -> p r n", n=SLOTS),
                                qkv_ln_b.rearrange("(r p) n -> p r n", p=P))
            for u in (2, 3):
                nc.gpsimd.dma_start(emb_sb[u][:], emb_blocks[:, :, u * LOOKUP:(u + 1) * LOOKUP])
            mlp_b_sb = held.tile([P, HID], F32)
            nc.gpsimd.dma_start(mlp_b_sb[:], mlp_b.rearrange("r o -> (r o)").partition_broadcast(P))
            mlp_w_sb = held.tile([P, HID_BLOCKS, HID], BF16)
            nc.gpsimd.dma_start(mlp_w_sb[:], mlp_w.rearrange("(hb p) r -> p hb r", p=P))

            spread_mean = held.tile([P, P], F32)
            nc.vector.memset(spread_mean[:], 1.0 / (P * PROJ))
            spread_bias = held.tile([P, P], F32)
            nc.vector.memset(spread_bias[:], 1.0 / PROJ)
            ones = held.tile([P, P], F32)
            nc.vector.memset(ones[:], 1.0)
            minus_half = held.tile([P, PIECE_SAMPLES], F32)
            nc.vector.memset(minus_half[:], -0.5)

            in_group = setup.tile([P, P // N_SAMPLES], F32)
            nc.vector.tensor_reduce(in_group[:], identity_f32[:].rearrange("p (g b) -> p g b", b=N_SAMPLES), AXIS_X, ALU.add)
            sample_of_row = held.tile([P, N_SAMPLES], BF16)
            with nc.allow_low_precision(reason="no sum has more than one term that is not 0"):
                nc.vector.tensor_reduce(sample_of_row[:], identity_f32[:].rearrange("p (g b) -> p b g", b=N_SAMPLES)[:, :, 0:TERM_GROUPS],
                                        AXIS_X, ALU.add)
            later_d = setup.tile([P, 1], F32)
            nc.vector.tensor_reduce(later_d[:], in_group[:, 3:6], AXIS_X, ALU.add)
            third_d = in_group[:, 5:6]
            later_w = setup.tile([P, 1], F32)
            second_w = setup.tile([P, 1], F32)
            nc.vector.tensor_tensor(second_w[:], in_group[:, 1:2], in_group[:, 4:5], ALU.add)
            nc.vector.tensor_tensor(later_w[:], second_w[:], in_group[:, 2:3], ALU.add)
            third_w = in_group[:, 2:3]

            def take_terms(out, value, later, third, shape, name):
                first = in_order.tile(shape, BF16, tag="slot", name=f"{name}_first")
                nc.vector.tensor_copy(first[:], value[:])
                minus_rest = setup.tile(shape, F32, name=f"{name}_minus_rest")
                nc.vector.scalar_tensor_tensor(minus_rest[:], first[:], later, value[:], ALU.mult, ALU.subtract)
                minus_second = setup.tile(shape, BF16, name=f"{name}_minus_second")
                nc.vector.tensor_copy(minus_second[:], minus_rest[:])
                nc.vector.scalar_tensor_tensor(out[:], minus_second[:], third, minus_rest[:], ALU.mult, ALU.subtract)

            d_min = setup.tile([P, 1], F32)
            nc.vector.tensor_reduce(d_min[:], dist[:], AXIS_X, ALU.min)
            e_dist = setup.tile([P, SLOTS], F32)
            d_sum = setup.tile([P, 1], F32)
            nc.scalar.activation(e_dist[:], dist[:], FUNC.Exp, bias=d_min[:], scale=-1.0, accum_out=d_sum[:])
            d_rsum = setup.tile([P, 1], F32)
            nc.vector.reciprocal(d_rsum[:], d_sum[:])
            d = setup.tile([P, SLOTS], F32)
            nc.vector.tensor_scalar_mul(d[:], e_dist[:], d_rsum[:])
            d_of_row = held.tile([P, SLOTS], BF16)
            take_terms(d_of_row, d, later_d[:], third_d, [P, SLOTS], "d")
            w_dist_rows = held.tile([P, HID], BF16)
            take_terms(w_dist_rows, w_dist_row, later_w[:], third_w, [P, HID], "w_dist")
            d_rows = [held.tile([P, LOOKUP_SAMPLES, SLOTS], BF16, name=f"d_rows{u}") for u in range(LOOKUPS)]

            def make_d_rows(engine, *lookups):
                for u in lookups:
                    group = slice(u * LOOKUP_SAMPLES, (u + 1) * LOOKUP_SAMPLES)
                    shape = [P, LOOKUP_SAMPLES, SLOTS]
                    engine.tensor_tensor(d_rows[u][:], sample_of_row[:, group].unsqueeze(2).to_broadcast(shape),
                                         d_of_row[:].unsqueeze(1).to_broadcast(shape), ALU.mult)

            make_d_rows(nc.vector, 0, 1)

        ring = {kind: ctx.enter_context(tc.tile_pool(name=kind, bufs=bufs)) for kind, bufs in SBUF_RINGS}

        mem = [held.tile([P, HID_BLOCKS, LOOKUP], F32, name=f"mem{u}") for u in range(LOOKUPS)]
        mem0_bf16 = [held.tile([P, HID_BLOCKS, LOOKUP], BF16, name=f"mem0_bf16_{u}") for u in range(LOOKUPS)]
        mem_sums = held.tile([P, HID_BLOCKS, N_SAMPLES], F32)
        cols = held.tile([P, N_COLS], F32)
        late_cols = held.tile([P, N_LATE_COLS], F32)
        minus_last_bias = held.tile([P, HID_BLOCKS], F32)
        query_term = held.tile([P, HID_BLOCKS, N_SAMPLES], F32)

        def open_mem(u, hb, kind):
            mem_ps = psum_ring[kind].tile([P, LOOKUP], F32, tag=kind)
            for kb in range(EMB_BLOCKS):
                nc.tensor.matmul(mem_ps[:], w_emb_sb[:, kb, hb * P:(hb + 1) * P], emb_sb[u][:, kb, :],
                                 start=(kb == 0), stop=False)
            return mem_ps

        def add_dist(u, hb, mem_ps):
            nc.tensor.matmul(mem_ps[:], w_dist_rows[:, hb * P:(hb + 1) * P], d_rows[u][:].rearrange("p b n -> p (b n)"),
                             start=False, stop=False)

        def close_mem(u, hb, mem_ps):
            nc.tensor.matmul(mem_ps[:], w_lab_sb[:, hb * P:(hb + 1) * P],
                             table_sb[:].indirect(offsets[:, u * (LOOKUP // 16):(u + 1) * (LOOKUP // 16)]),
                             start=False, stop=True)
            for k in range(LOOKUP_SAMPLES):
                b = u * LOOKUP_SAMPLES + k
                sample = slice(k * SLOTS, (k + 1) * SLOTS)
                nc.scalar.activation(mem[u][:, hb, sample], mem_ps[:, sample],
                                     FUNC.Identity, bias=query_term[:, hb, b:b + 1], accum_out=mem_sums[:, hb, b:b + 1])
            nc.vector.tensor_scalar_add(mem0_bf16[u][:, hb, :], mem[u][:, hb, :], minus_last_bias[:, hb:hb + 1])

        def sum_weights():
            w_copy = held.tile([P, PROJ], BF16)
            nc.scalar.activation(w_copy[:], qkv_w_sb[:, 0, :], FUNC.Copy, accum_out=first_w_sum[:])
            for hb in range(1, HID_BLOCKS):
                nc.vector.tensor_reduce(later_w_sums[:, hb - 1:hb], qkv_w_sb[:, hb, :], AXIS_X, ALU.add)
            for hb in range(HID_BLOCKS):
                w_sum = first_w_sum[:] if hb == 0 else later_w_sums[:, hb - 1:hb]
                nc.vector.tensor_scalar(mean_weights[:, hb, :], ones[:], w_sum, 1.0 / (P * PROJ), ALU.mult, ALU.mult)

        def centre_bias():
            qkv_b_cols = late_cols[:, LATE_COL_QKV_B:LATE_COL_QKV_B + PROJ // P]
            addends = held.tile([P, PROJ // P + HID_BLOCKS], F32)
            nc.gpsimd.tensor_copy(addends[:, 0:PROJ // P], qkv_b_cols)
            nc.gpsimd.tensor_tensor(addends[:, PROJ // P:PROJ // P + 1], first_w_sum[:], minus_last_bias[:, 0:1], ALU.mult)
            nc.gpsimd.tensor_tensor(addends[:, PROJ // P + 1:PROJ // P + HID_BLOCKS], later_w_sums[:],
                                    minus_last_bias[:, 1:HID_BLOCKS], ALU.mult)
            bias_ps = psum_ring["scores"].tile([P, PROJ // P + HID_BLOCKS], F32, tag="scores")
            nc.tensor.matmul(bias_ps[:], spread_bias[:], addends[:], start=True, stop=True)
            bias_mean = held.tile([P, 1], F32)
            nc.vector.tensor_reduce(bias_mean[:], bias_ps[:], AXIS_X, ALU.add)
            nc.gpsimd.memset(centred_bias[:], 0.0)
            by_kind = centred_bias[:].rearrange("p (t c) -> p t c", c=3)
            nc.gpsimd.tensor_copy(by_kind[:, :, 0:2], qkv_b_cols.rearrange("p (t c) -> p t c", c=3)[:, :, 0:2])
            nc.vector.tensor_scalar(centred_bias[:], centred_bias[:], bias_mean[:], None, ALU.subtract)

        def find_mean(u, kind):
            group = slice(u * LOOKUP_SAMPLES, (u + 1) * LOOKUP_SAMPLES)
            mean_ps = psum_ring[kind].tile([P, LOOKUP_SAMPLES], F32, tag=kind)
            for hb in range(HID_BLOCKS):
                nc.tensor.matmul(mean_ps[:], mean_weights[:, hb, :], mem_sums[:, hb, group],
                                 start=(hb == 0), stop=(hb == HID_BLOCKS - 1))
            shape = [P, LOOKUP_SAMPLES, PROJ // P]
            nc.vector.tensor_tensor(shift[:, group, :], centred_bias[:].unsqueeze(1).to_broadcast(shape),
                                    mean_ps[:].unsqueeze(2).to_broadcast(shape), ALU.subtract)

        first_w_sum = held.tile([P, 1], F32)
        later_w_sums = in_order.tile([P, HID_BLOCKS - 1], F32, tag="slot")
        mean_weights = held.tile([P, HID_BLOCKS, P], F32)
        centred_bias = held.tile([P, PROJ // P], F32)
        shift = held.tile([P, N_SAMPLES, PROJ // P], F32)
        square_sums = held.tile([P, N_SAMPLES, N_SUMS], F32)
        nc.vector.memset(square_sums[:], EPS * PROJ)
        scaled_of_piece = {}
        q_k_v_of_sample = {}
        rstd_of_piece = {}

        gain_by_kind = ln_gain[:].rearrange("p (t c n) -> p t c n", c=3, n=SLOTS)
        v_weights = qkv_w_sb[:].rearrange("p hb (t c u) -> p hb t c u", c=3, u=P)[:, :, :, 2, :]

        def start_piece(g):
            scaled = ring["scaled"].tile([P, PIECE_SAMPLES, PROJ], F32)
            scaled_of_piece[g] = scaled

        def project_v(g, s):
            u, start = divmod(g * PIECE, LOOKUP)
            b = g * PIECE_SAMPLES + s
            v_shift = shift[:, b, 2:3]
            v_ps = bank.tile([P, HEADS, P], F32, tag="bank")
            for hb in range(HID_BLOCKS):
                nc.tensor.matmul(v_ps[:], mem0_bf16[u][:, hb, start + s * SLOTS:start + (s + 1) * SLOTS], v_weights[:, hb, :, :],
                                 start=(hb == 0), stop=(hb == HID_BLOCKS - 1))
            y_v = ring["y_v"].tile([P, HEADS, P], F32)
            nc.vector.scalar_tensor_tensor(y_v[:], v_ps[:], v_shift, v_bias[:], ALU.add, ALU.add)
            squares = ring["squares"].tile([P, HEADS, P], BF16)
            nc.scalar.activation(squares[:], y_v[:], FUNC.Square, accum_out=square_sums[:, b, SUM_V:SUM_V + 1])
            nc.vector.tensor_tensor(scaled_of_piece[g][:, s, :].rearrange("p (t c u) -> p t c u", c=3, u=P)[:, :, 2, :],
                                    y_v[:], gain_by_kind[:, :, 2, :], ALU.mult)

        def project_qk(g, t):
            u, start = divmod(g * PIECE, LOOKUP)
            qk_ps = bank.tile([P, 2, PIECE_SAMPLES, SLOTS], F32, tag="bank")
            for c in range(2):
                r = 3 * t + c
                for hb in range(HID_BLOCKS):
                    nc.tensor.matmul(qk_ps[:, c, :, :].rearrange("p s n -> p (s n)"),
                                     qkv_w_sb[:, hb, r * P:(r + 1) * P],
                                     mem0_bf16[u][:, hb, start:start + PIECE], start=(hb == 0), stop=(hb == HID_BLOCKS - 1))
            blocks = [(c, s, 3 * t + c, g * PIECE_SAMPLES + s) for c in range(2) for s in range(PIECE_SAMPLES)]
            for c, s, r, b in blocks:
                nc.vector.scalar_tensor_tensor(scaled_of_piece[g][:, s, r * P:(r + 1) * P], qk_ps[:, c, s, :],
                                               shift[:, b, r:r + 1], ln_gain[:, r * P:(r + 1) * P],
                                               ALU.add, ALU.mult)
            for c, s, r, b in blocks:
                squares = ring["squares"].tile([P, HEADS, P], BF16)
                nc.scalar.activation(squares[:, 0, :], qk_ps[:, c, s, :], FUNC.Square, bias=shift[:, b, r:r + 1],
                                     accum_out=square_sums[:, b, 2 * t + c:2 * t + c + 1])

        parts_of_piece = [lambda g: project_v(g, 0), lambda g: project_qk(g, 0), lambda g: project_qk(g, 1),
                          lambda g: project_v(g, 1), lambda g: project_qk(g, 2), lambda g: project_qk(g, 3)]
        def project(g):
            start_piece(g)
            for part, project_part in enumerate(parts_of_piece):
                project_part(g)
                turn, rest = divmod(g * len(parts_of_piece) + part + 1, 4)
                if rest == 0 and turn <= len(later_blocks):
                    u, hb = later_blocks[turn - 1]
                    mem_ps = open_mem(u, hb, "bank")
                    add_dist(u, hb, mem_ps)
                    close_mem(u, hb, mem_ps)
                    if hb == HID_BLOCKS - 1:
                        find_mean(u, "bank")

        def measure(g):
            samples = slice(g * PIECE_SAMPLES, (g + 1) * PIECE_SAMPLES)
            sample_ps = psum_ring["short"].tile([P, PIECE_SAMPLES, N_SUMS], F32, tag="short")
            nc.tensor.matmul(sample_ps[:].rearrange("p s k -> p (s k)"), spread_mean[:],
                             square_sums[:, samples, :].rearrange("p s k -> p (s k)"), start=True, stop=True)
            var_eps = ring["var_eps"].tile([P, PIECE_SAMPLES], F32)
            nc.vector.tensor_reduce(var_eps[:], sample_ps[:], AXIS_X, ALU.add)
            rstd = ring["rstd"].tile([P, PIECE_SAMPLES], F32)
            nc.gpsimd.tensor_tensor(rstd[:], var_eps[:], minus_half[:], ALU.pow)
            rstd_of_piece[g] = rstd

        def prepare_param(param, engine):
            by_kind = param[:].rearrange("p (t c n) -> p t c n", c=3, n=SLOTS)
            v_flipped = psum_ring["short"].tile([P, HEADS, P], F32, tag="short")
            for t in range(HEADS):
                nc.tensor.transpose(v_flipped[:, t, :], by_kind[:, t, 2, :], identity_f32[:])
            nc.vector.tensor_copy(by_kind[:, :, 2, :], v_flipped[:])
            engine.mul(by_kind[:, :, 0, :], by_kind[:, :, 0, :], Q_SCALE)

        cols_ps = psum_ring["short"].tile([P, P], F32, tag="short")
        nc.tensor.transpose(cols_ps[:], rows[:], identity_f32[:])
        nc.scalar.copy(cols[:], cols_ps[:, 0:N_COLS])
        query_ps = psum_ring["short"].tile([P, HID_BLOCKS, N_SAMPLES], F32, tag="short")
        for hb in range(HID_BLOCKS):
            for kb in range(EMB_BLOCKS):
                nc.tensor.matmul(query_ps[:, hb, :], w_qry_sb[:, kb, hb * P:(hb + 1) * P], query_sb[:, kb, :],
                                 start=(kb == 0), stop=(kb == EMB_BLOCKS - 1))
        last_bias = cols[:, COL_MLP_LN_B:COL_MLP_LN_B + HID_BLOCKS]
        nc.gpsimd.tensor_scalar(minus_last_bias[:], last_bias, -1.0, None, ALU.mult)
        both_biases = held.tile([P, HID_BLOCKS], F32)
        nc.gpsimd.tensor_tensor(both_biases[:], cols[:, COL_PRE_B:COL_PRE_B + HID_BLOCKS], last_bias, ALU.add)
        for hb in range(HID_BLOCKS):
            nc.scalar.activation(query_term[:, hb, :], query_ps[:, hb, :], FUNC.Identity, bias=both_biases[:, hb:hb + 1])
        blocks = [(u, hb) for u in range(LOOKUPS) for hb in range(HID_BLOCKS)]
        early_blocks, later_blocks = blocks[:EARLY_BLOCKS], blocks[EARLY_BLOCKS:]
        kinds = ["bank"] * HID_BLOCKS + ["short"] * 2 + ["scores"]
        opened = [(u, hb, open_mem(u, hb, kind)) for (u, hb), kind in zip(early_blocks, kinds)]
        for u, hb, mem_ps in opened:
            add_dist(u, hb, mem_ps)
        for u, hb, mem_ps in opened:
            close_mem(u, hb, mem_ps)
        make_d_rows(nc.gpsimd, 2, 3)
        late_cols_ps = psum_ring["short"].tile([P, P], F32, tag="short")
        nc.tensor.transpose(late_cols_ps[:], late_rows[:], identity_f32[:])
        nc.scalar.copy(late_cols[:], late_cols_ps[:, 0:N_LATE_COLS])
        prepare_param(ln_gain, nc.scalar)
        sum_weights()
        centre_bias()
        find_mean(0, "scores")

        def normalise(b):
            g, s = divmod(b, PIECE_SAMPLES)
            z = ring["z"].tile([P, PROJ], BF16)
            q_k_v_of_sample[b] = z[:].rearrange("p (t c n) -> p t c n", c=3, n=P)
            for third in range(3):
                columns = slice(third * HID, (third + 1) * HID)
                nc.vector.scalar_tensor_tensor(z[:, columns], scaled_of_piece[g][:, s, columns], rstd_of_piece[g][:, s:s + 1],
                                               ln_bias[:, columns], ALU.mult, ALU.add)

        kept = {b: {} for b in range(N_SAMPLES)}

        def score(b):
            q_k_v = q_k_v_of_sample[b]
            scores = psum_ring["scores"].tile([P, HEADS, SLOTS], F32, tag="scores")
            for t in range(HEADS):
                nc.tensor.matmul(scores[:, t, :], q_k_v[:, t, 0, :], q_k_v[:, t, 1, :], start=True, stop=True)
            kept[b]["scores"] = scores

        def find_max(b):
            minus_max = ring["minus_max"].tile([P, HEADS], F32)
            nc.vector.tensor_reduce(minus_max[:], kept[b]["scores"][:], AXIS_X, ALU.max, negate=True)
            kept[b]["minus_max"] = minus_max

        def exponentiate(b):
            scores, minus_max = kept[b]["scores"], kept[b]["minus_max"]
            exp_scores = ring["exp_scores"].tile([P, HEADS, SLOTS], F32)
            exp_sum = ring["exp_sum"].tile([P, HEADS], F32)
            for t in range(HEADS):
                nc.scalar.activation(exp_scores[:, t, :], scores[:, t, :], FUNC.Exp,
                                     bias=minus_max[:, t:t + 1], accum_out=exp_sum[:, t:t + 1])
            kept[b]["exp_scores"] = exp_scores
            kept[b]["exp_sum"] = exp_sum

        def invert_sum(b):
            exp_rsum = ring["exp_rsum"].tile([P, HEADS], F32)
            nc.vector.reciprocal(exp_rsum[:], kept[b]["exp_sum"][:])
            kept[b]["exp_rsum"] = exp_rsum

        def divide(b):
            exp_scores, exp_rsum = kept[b]["exp_scores"], kept[b]["exp_rsum"]
            att = ring["att"].tile([P, HEADS, SLOTS], BF16)
            for t in range(HEADS):
                nc.scalar.activation(att[:, t, :], exp_scores[:, t, :], FUNC.Copy, scale=exp_rsum[:, t:t + 1])
            kept[b]["att"] = att

        def flip_att(b):
            att_flipped_ps = psum_ring["short"].tile([P, HEADS, SLOTS], BF16, tag="short")
            for t in range(HEADS):
                nc.tensor.transpose(att_flipped_ps[:, t, :], kept[b]["att"][:, t, :], identity_bf16[:])
            kept[b]["att_flipped_ps"] = att_flipped_ps

        def copy_att(b):
            att_flipped = ring["att_flipped"].tile([P, HEADS, SLOTS], BF16)
            nc.scalar.copy(att_flipped[:], kept[b]["att_flipped_ps"][:])
            kept[b]["att_flipped"] = att_flipped

        def weigh(b):
            q_k_v = q_k_v_of_sample[b]
            o_ps = psum_ring["short"].tile([P, HEADS, SLOTS], F32, tag="short")
            for t in range(HEADS):
                nc.tensor.matmul(o_ps[:, t, :], q_k_v[:, t, 2, :], kept[b]["att_flipped"][:, t, :], start=True, stop=True)
            kept[b]["o_ps"] = o_ps

        def add_residual(b):
            mem1_biased = ring["mem1_biased"].tile([P, HID_BLOCKS, SLOTS], F32)
            u, start = divmod(b * SLOTS, LOOKUP)
            nc.vector.tensor_tensor(mem1_biased[:], kept[b]["o_ps"][:], mem[u][:, :, start:start + SLOTS], ALU.add)
            kept[b]["mem1_biased"] = mem1_biased

        def rectify(b):
            relu_mem1 = ring["relu_mem1"].tile([P, HID_BLOCKS, SLOTS], BF16)
            for hb in range(HID_BLOCKS):
                nc.scalar.activation(relu_mem1[:, hb, :], kept[b]["mem1_biased"][:, hb, :], FUNC.Relu,
                                     bias=minus_last_bias[:, hb:hb + 1])
            kept[b]["relu_mem1"] = relu_mem1

        def mlp_product(b):
            f_ps = psum_ring["short"].tile([P, HID], F32, tag="short")
            for hb in range(HID_BLOCKS):
                nc.tensor.matmul(f_ps[:], kept[b]["relu_mem1"][:, hb, :], mlp_w_sb[:, hb, :],
                                 start=(hb == 0), stop=(hb == HID_BLOCKS - 1))
            kept[b]["f_ps"] = f_ps

        def mlp_bias(b):
            f = ring["f"].tile([P, HID], F32)
            f_sum = ring["f_sum"].tile([P, 1], F32)
            nc.vector.scalar_tensor_tensor(f[:], kept[b]["f_ps"][:], 1.0, mlp_b_sb[:], ALU.mult, ALU.add, accum_out=f_sum[:])
            kept[b]["f"] = f
            kept[b]["f_sum"] = f_sum

        def mlp_mean(b):
            minus_mu2 = ring["minus_mu2"].tile([P, 1], F32)
            nc.vector.tensor_scalar_mul(minus_mu2[:], kept[b]["f_sum"][:], -1.0 / HID)
            kept[b]["minus_mu2"] = minus_mu2

        def mlp_square(b):
            f_squares = ring["f_squares"].tile([P, HID], BF16)
            f_square_sum = ring["f_square_sum"].tile([P, 1], F32)
            nc.scalar.activation(f_squares[:], kept[b]["f"][:], FUNC.Square, bias=kept[b]["minus_mu2"][:],
                                 accum_out=f_square_sum[:])
            kept[b]["f_square_sum"] = f_square_sum

        def mlp_rstd(b):
            var2 = ring["var2"].tile([P, 1], F32)
            nc.vector.tensor_scalar(var2[:], kept[b]["f_square_sum"][:], 1.0 / HID, EPS, ALU.mult, ALU.add)
            rstd2 = ring["rstd2"].tile([P, 1], F32)
            nc.gpsimd.tensor_tensor(rstd2[:], var2[:], minus_half[:, 0:1], ALU.pow)
            kept[b]["rstd2"] = rstd2

        def mlp_normalise(b):
            normed = ring["normed"].tile([P, HID], F32)
            nc.vector.tensor_scalar(normed[:], kept[b]["f"][:], kept[b]["minus_mu2"][:], kept[b]["rstd2"][:],
                                    ALU.add, ALU.mult)
            kept[b]["normed"] = normed

        def flip_back(b):
            normed_flipped = psum_ring["short"].tile([P, HID_BLOCKS, SLOTS], F32, tag="short")
            for rb in range(HID_BLOCKS):
                nc.tensor.transpose(normed_flipped[:, rb, :], kept[b]["normed"][:, rb * P:(rb + 1) * P], identity_f32[:])
            kept[b]["normed_flipped"] = normed_flipped

        def finish(b):
            result = ring["result"].tile([P, HID_BLOCKS, SLOTS], F32)
            for rb in range(HID_BLOCKS):
                nc.vector.scalar_tensor_tensor(result[:, rb, :], kept[b]["normed_flipped"][:, rb, :],
                                               late_cols[:, LATE_COL_MLP_LN_W + rb:LATE_COL_MLP_LN_W + rb + 1],
                                               kept[b]["mem1_biased"][:, rb, :], ALU.mult, ALU.add)
            nc.sync.dma_start(out_blocks[:, :, b * SLOTS:(b + 1) * SLOTS], result[:])

        def in_turn(*links):
            def stage(b):
                for link in links:
                    link(b)
            return stage

        stages = (in_turn(score, find_max), exponentiate, in_turn(invert_sum, divide), flip_att, copy_att, weigh, add_residual, rectify,
                  mlp_product, mlp_bias, in_turn(mlp_mean, mlp_square), mlp_rstd, mlp_normalise, flip_back, finish)
        out_blocks = out.rearrange("(rb p) n -> p rb n", p=P)
        for tick in range(-PROJECT_LEAD, N_SAMPLES + len(stages) - 1):
            for lag in reversed(range(len(stages))):
                if 0 <= tick - lag < N_SAMPLES:
                    stages[lag](tick - lag)
            if 0 <= tick + NORMALISE_LEAD < N_SAMPLES:
                normalise(tick + NORMALISE_LEAD)
            g, s = divmod(tick + MEASURE_LEAD, PIECE_SAMPLES)
            if s == 0 and 0 <= g < PIECES:
                measure(g)
            g, s = divmod(tick + PROJECT_LEAD, PIECE_SAMPLES)
            if s == 0 and g < PIECES:
                project(g)
                if g == 0:
                    prepare_param(ln_bias, nc.scalar)
